import numpy as np
import ml_dtypes


def mxq(x, axis, fmt="e4m3"):
    dtype, down = {"e4m3": (ml_dtypes.float8_e4m3fn, 7), "e5m2": (ml_dtypes.float8_e5m2, 14)}[fmt]
    v = np.moveaxis(np.asarray(x, np.float32).astype(ml_dtypes.bfloat16).astype(np.float64), axis, -1)
    blocks = v.reshape(v.shape[:-1] + (-1, 32))
    amax = np.abs(blocks).max(-1, keepdims=True)
    byte = np.maximum(np.where(amax > 0, np.frexp(amax)[1] - 1 + 127, 0) - down, 1)
    scale = np.exp2(byte - 127.0)
    codes = (blocks / scale).astype(np.float32).astype(dtype).astype(np.float64)
    return np.moveaxis((codes * scale).reshape(v.shape), -1, axis)


WIDE = False


def mx_kscale(k):
    if not WIDE:
        return np.ones(k)
    levels = np.array([10, -10, 5, -5, 0])
    a = np.random.permutation(np.resize(levels, k // 512 * 4)).reshape(k // 512, 4)
    idx = np.arange(k)
    return np.exp2(a[idx // 512, idx % 128 // 32])


BF16 = ml_dtypes.bfloat16


def bf(x):
    return np.asarray(x, np.float32).astype(BF16)


def f64(x):
    return np.asarray(x).astype(np.float64)


B, N, D1, D2, NS = 512, 8, 512, 256, 2
ND = D1
NP = N // NS


def rolled_concat(arrays, n, axis=-1):
    return np.concatenate(arrays[n:] + arrays[:n], axis=axis)


def setup_inputs():
    t = mx_kscale(NS * D2)
    tb = t.reshape(NS, D2)
    fac = np.stack([np.roll(tb, i, axis=0) for i in range(NS)])
    x2 = np.random.standard_normal((B, NS, NP, NS, NP, D2)) * fac[None, :, None, :, None, :]
    return {"in_1e": bf(np.random.standard_normal((B, N, D1))),
            "in_2e": bf(x2.reshape(B, N, N, D2)),
            "W_unmixed": bf(np.random.standard_normal((D1, ND)) * 0.6 / np.sqrt(D1)),
            "b_unmixed": bf(np.random.standard_normal(ND) * 0.3),
            "W_mixed": bf(np.random.standard_normal((NS * D1, ND)) * 0.6 * np.sqrt(NP) / np.sqrt(NS * D1)),
            "W_2e": bf(np.random.standard_normal((NS * D2, ND)) * 0.6 * np.sqrt(NP) / np.sqrt(NS * D2) / t[:, None])}


def reference(in_1e, in_2e, W_unmixed, b_unmixed, W_mixed, W_2e):
    x1, x2 = f64(in_1e), f64(in_2e)
    dense_unmixed = (mxq(x1, 2, "e4m3") @ mxq(f64(W_unmixed), 0, "e4m3")) + f64(b_unmixed)
    split_unmixed = np.split(dense_unmixed, NS, axis=-2)
    split_1e = np.split(x1, NS, axis=-2)
    split_means = [np.mean(s, axis=-2, keepdims=True) for s in split_1e]
    split_concat = [rolled_concat(split_means, i) for i in range(NS)]
    all_spins = np.concatenate(split_concat, axis=-2)
    dense_mixed = mxq(all_spins, 2, "e4m3") @ mxq(f64(W_mixed), 0, "e4m3")
    dense_mixed_split = np.split(dense_mixed, NS, axis=-2)
    split_2e = np.split(x2, NS, axis=-3)
    concat_2e = []
    for spin in range(NS):
        blocks = np.split(split_2e[spin], NS, axis=-2)
        means = [np.mean(p, axis=-2) for p in blocks]
        concat_2e.append(rolled_concat(means, spin))
    all_2e = np.concatenate(concat_2e, axis=-2)
    dense_2e = mxq(all_2e, 2, "e4m3") @ mxq(f64(W_2e), 0, "e4m3")
    dense_2e_split = np.split(dense_2e, NS, axis=-2)
    out_splits = [u + m + e for u, m, e in zip(split_unmixed, dense_mixed_split, dense_2e_split)]
    dense_out = np.concatenate(out_splits, axis=-2)
    return np.tanh(dense_out) + x1

@@ -1,0 +1,340 @@
+import concourse.mybir as mybir
+from concourse.masks import make_identity
+
+F32 = mybir.dt.float32
+BF16 = mybir.dt.bfloat16
+U32 = mybir.dt.uint32
+U8 = mybir.dt.uint8
+FP8X4 = mybir.dt.float8_e4m3fn_x4
+ADD = mybir.AluOpType.add
+ACT = mybir.ActivationFunctionType
+
+P = 128
+B, N, D1, D2, NS = 512, 8, 512, 256, 2
+ND = D1
+NBLK = B // P
+PIECES = 4
+NPIECE = NBLK * PIECES
+NPAIR = NBLK * 4
+LAG = 4
+AHEAD = 4
+VHALF = (0, 1)
+LAST_LOAD_SLOT = NPIECE - AHEAD - 1
+WU, WA, WB, WE = 0, 1, 2, 3
+
+FLOPS = 2 * (B * N * D1 * ND + B * NS * NS * D1 * ND + B * N * NS * D2 * ND)
+
+
+def tile_ferminetoneelectronlayer_pa_t_kernel(tc, in_1e, in_2e, W_unmixed, b_unmixed, W_mixed, W_2e, out):
+    nc = tc.nc
+    rows2 = in_2e.rearrange("b i j d -> (b i j) d")
+    toks2 = in_2e.rearrange("b i j d -> (b i) j d")
+
+    with tc.manual_schedule(), \
+         tc.tile_pool(name="const", bufs=1) as const, \
+         tc.tile_pool(name="xpool", bufs=4) as xpool, \
+         tc.tile_pool(name="stage", bufs=AHEAD) as stage, \
+         tc.tile_pool(name="grp", bufs=2) as grp, \
+         tc.tile_pool(name="codes", bufs=2) as codes, \
+         tc.tile_pool(name="work", bufs=4) as work, \
+         tc.psum_pool(name="ps", bufs=2) as ps:
+
+        xs = {}
+        pieces = {}
+        g1s = {}
+        g2s = {}
+        msums = {}
+        gms = {}
+        a2s = {}
+        xq = {}
+        mq = {}
+        eq = {}
+        gbs = {}
+        zs = {}
+        os_ = {}
+        outp_box = []
+
+        def load_x(bb):
+            x = xpool.tile([P, N, D1], BF16, name="x%d" % bb, tag="x")
+            nc.sync.dma_start(out=x[:], in_=in_1e[bb * P:(bb + 1) * P, :, :])
+            xs[bb] = x
+
+        def load_piece(k):
+            pc = stage.tile([P, 16, D2], BF16, name="pc%d" % k, tag="pc")
+            r0 = k * 16 * P
+            if k in VHALF:
+                nc.sync.dma_start(out=pc[:, 0:8, :], in_=rows2[r0:r0 + 8 * P, :].rearrange("(r p) d -> p r d", p=P))
+                t0 = (k * 32 + 16) * N
+                nc.sync.dma_start(out=pc[:, 8:16, :], in_=toks2[t0:t0 + P, :, :])
+            else:
+                nc.sync.dma_start(out=pc[:], in_=rows2[r0:r0 + 16 * P, :].rearrange("(r p) d -> p r d", p=P))
+            pieces[k] = pc
+
+        def a_transposes(bb, qs):
+            x = xs[bb]
+            xf = x[:].bitcast(F32)
+            if bb not in g1s:
+                g1s[bb] = grp.tile([P, N, P, 4], BF16, name="g1_%d" % bb, tag="g1", align_bytes=64)
+            g1f = g1s[bb][:].rearrange("p i b t -> p i (b t)").bitcast(F32).rearrange("p i (b u) -> p i b u", u=2)
+            xts = []
+            for q in qs:
+                xt = ps.tile([P, 2, 2, P], F32, name="xt%d_%d" % (bb, q), tag="xt")
+                for i2 in range(2):
+                    for u in range(2):
+                        nc.tensor.transpose(xt[:, i2, u, :], xf[:, 2 * q + i2, u * P:(u + 1) * P], ident_f[:])
+                xts.append(xt)
+            for q, xt in zip(qs, xts):
+                nc.scalar.copy(out=g1f[:, 2 * q:2 * q + 2, :, :], in_=xt[:].rearrange("p i u b -> p i b u"))
+
+        def a_mean(bb, s):
+            x = xs[bb]
+            if bb not in msums:
+                msums[bb] = grp.tile([P, 2, D1], BF16, name="ms%d" % bb, tag="ms")
+            t1 = grp.tile([P, 2, D1], F32, name="t1_%d_%d" % (bb, s), tag="t1")
+            nc.vector.tensor_tensor(out=t1[:], in0=x[:, 4 * s:4 * s + 2, :], in1=x[:, 4 * s + 2:4 * s + 4, :], op=ADD)
+            nc.vector.tensor_tensor(out=msums[bb][:, s, :], in0=t1[:, 0, :], in1=t1[:, 1, :], op=ADD)
+
+        def a_mean_transposes(bb):
+            mt = ps.tile([P, 2, 4, P], BF16, name="mt%d" % bb, tag="aux")
+            for s in range(2):
+                for t in range(4):
+                    nc.tensor.transpose(mt[:, s, t, :], msums[bb][:, s, t * P:(t + 1) * P], ident_b[:])
+            gm = grp.tile([P, 2, P, 4], BF16, name="gm%d" % bb, tag="gm", align_bytes=64)
+            nc.scalar.mul(out=gm[:], in_=mt[:].rearrange("p s t b -> p s b t"), mul=0.25)
+            gms[bb] = gm
+
+        def a_quant_x(bb):
+            xc = codes.tile([P, N * P], U32, name="xc%d" % bb, tag="xc", align_bytes=64)
+            xsc = codes.tile([P, N * P], U8, name="xsc%d" % bb, tag="xsc", align_bytes=64)
+            nc.vector.quantize_mx(out=xc[:].bitcast(FP8X4), scales=xsc[:], in_=g1s[bb][:].rearrange("p i b t -> p (i b t)"))
+            xq[bb] = (xc, xsc)
+
+        def a_quant_m(bb):
+            mc = codes.tile([P, 2 * P], U32, name="mc%d" % bb, tag="mc", align_bytes=64)
+            msc = codes.tile([P, 2 * P], U8, name="msc%d" % bb, tag="msc", align_bytes=64)
+            nc.vector.quantize_mx(out=mc[:].bitcast(FP8X4), scales=msc[:], in_=gms[bb][:].rearrange("p s b t -> p (s b t)"))
+            mq[bb] = (mc, msc)
+
+        def a_g_mx(bb):
+            mc, msc = mq[bb]
+            gps = []
+            for s in range(2):
+                gp = ps.tile([P, ND], F32, name="gp%d_%d" % (bb, s), tag="aux")
+                for a, (w, sp) in enumerate(((WA, s), (WB, 1 - s))):
+                    nc.tensor.matmul_mx(out=gp[:], lhsT=mc[:, sp * P:(sp + 1) * P].bitcast(FP8X4),
+                                        lhsT_scale=msc[:, sp * P:(sp + 1) * P],
+                                        rhs=wcodes[:, w, :].bitcast(FP8X4), rhs_scale=wscales[:, w, :],
+                                        start=(a == 0), stop=(a == 1))
+                gps.append(gp)
+            return gps
+
+        def a_g_add(bb, gps):
+            gb = grp.tile([P, 2, ND], F32, name="gb%d" % bb, tag="gb")
+            for s in range(2):
+                nc.vector.tensor_tensor(out=gb[:, s, :], in0=gps[s][:], in1=bias_bc[:], op=ADD)
+            gbs[bb] = gb
+
+        def pool_half(k, half):
+            bb, kp = divmod(k, PIECES)
+            pc = pieces[k]
+            pp = ps.tile([P, N, 64], F32, name="pp%d_%d" % (k, half), tag="pp")
+            ppv = pp[:].rearrange("p i (r q c) -> p i r q c", r=8, q=4, c=2)
+            for r in range(8):
+                for c in range(2):
+                    nc.tensor.matmul(out=ppv[:, :, r, :, c], lhsT=pc[:, 8 * half + r, c * P:(c + 1) * P],
+                                     rhs=pool_rhs, start=True, stop=True)
+            kk = 2 * kp + half
+            nc.scalar.copy(out=g2s[bb][:, :, 64 * kk:64 * (kk + 1)], in_=pp[:])
+
+        def vhalf_add(k):
+            lv = pieces[k][:, 8:16, :].rearrange("p (a f) d -> p a f d", a=2)
+            t1 = grp.tile([P, 2, 2, D2], F32, name="vt1_%d" % k, tag="t1")
+            nc.vector.tensor_tensor(out=t1[:], in0=lv[:, :, 0:2, :], in1=lv[:, :, 2:4, :], op=ADD)
+            a2 = grp.tile([P, 2, D2], BF16, name="a2_%d" % k, tag="a2")
+            nc.vector.tensor_tensor(out=a2[:], in0=t1[:, :, 0, :], in1=t1[:, :, 1, :], op=ADD)
+            a2s[k] = a2
+
+        def vhalf_finish(k):
+            bb, kp = divmod(k, PIECES)
+            a2 = a2s[k]
+            vt = ps.tile([P, 4, P], BF16, name="vt%d" % k, tag="aux")
+            for sj in range(2):
+                for c in range(2):
+                    nc.tensor.transpose(vt[:, 2 * sj + c, :], a2[:, sj, c * P:(c + 1) * P], ident_b[:])
+            vtv = vt[:].rearrange("p t (b i) -> p i b t", i=N)
+            kk = 2 * kp + 1
+            g2v = g2s[bb][:].rearrange("p i (b t) -> p i b t", t=4)[:, :, 16 * kk:16 * (kk + 1), :]
+            nc.scalar.mul(out=g2v[:, 0:4, :, :], in_=vtv[:, 0:4, :, :], mul=0.25)
+            for h in range(2):
+                nc.scalar.mul(out=g2v[:, 4:8, :, 2 * h:2 * h + 2], in_=vtv[:, 4:8, :, 2 - 2 * h:4 - 2 * h], mul=0.25)
+
+        def quantise_e(bb):
+            ec = codes.tile([P, N * P], U32, name="ec%d" % bb, tag="ec", align_bytes=64)
+            esc = codes.tile([P, N * P], U8, name="esc%d" % bb, tag="esc", align_bytes=64)
+            nc.vector.quantize_mx(out=ec[:].bitcast(FP8X4), scales=esc[:], in_=g2s[bb][:].rearrange("p i c -> p (i c)"))
+            eq[bb] = (ec, esc)
+
+        def c_mx(pair):
+            bb, q = divmod(pair, 4)
+            xc, xsc = xq[bb]
+            ec, esc = eq[bb]
+            accs = []
+            for i2 in range(2):
+                i = 2 * q + i2
+                cols = slice(i * P, (i + 1) * P)
+                acc = ps.tile([P, ND], F32, name="acc%d_%d" % (bb, i), tag="acc")
+                nc.tensor.matmul_mx(out=acc[:], lhsT=xc[:, cols].bitcast(FP8X4), lhsT_scale=xsc[:, cols],
+                                    rhs=wcodes[:, WU, :].bitcast(FP8X4), rhs_scale=wscales[:, WU, :],
+                                    start=True, stop=False)
+                nc.tensor.matmul_mx(out=acc[:], lhsT=ec[:, cols].bitcast(FP8X4), lhsT_scale=esc[:, cols],
+                                    rhs=wcodes[:, WE, :].bitcast(FP8X4), rhs_scale=wscales[:, WE, :],
+                                    start=False, stop=True)
+                accs.append(acc)
+            return accs
+
+        def c_sum_tanh(pair, accs):
+            bb, q = divmod(pair, 4)
+            zz = []
+            for i2 in range(2):
+                z = work.tile([P, ND], F32, name="z%d_%d" % (pair, i2), tag="z")
+                nc.vector.tensor_tensor(out=z[:], in0=accs[i2][:], in1=gbs[bb][:, q // 2, :], op=ADD)
+                zz.append(z)
+            for i2 in range(2):
+                nc.scalar.activation(out=zz[i2][:], in_=zz[i2][:], func=ACT.Tanh)
+            zs[pair] = zz
+
+        def c_skip(pair):
+            bb, q = divmod(pair, 4)
+            o = outp_box[0].tile([P, 2, ND], F32, name="o%d" % pair, tag="o")
+            for i2 in range(2):
+                nc.vector.tensor_tensor(out=o[:, i2, :], in0=zs[pair][i2][:], in1=xs[bb][:, 2 * q + i2, :], op=ADD)
+            os_[pair] = o
+
+        def store(pair):
+            bb, q = divmod(pair, 4)
+            nc.sync.dma_start(out=out[bb * P:(bb + 1) * P, 2 * q:2 * q + 2, :], in_=os_[pair][:])
+
+        def prep_weights(wgrp):
+            srcs = ((WA, raw_m[:, 0:4, :]), (WB, raw_m[:, 4:8, :]), (WU, raw_u[:]), (WE, raw_e[:]))
+            wgs = {}
+
+            def regroup(n):
+                w, src = srcs[n]
+                wg = wgrp.tile([P, ND, 4], BF16, name="wg%d" % w, tag="wg", align_bytes=64)
+                nc.vector.tensor_copy(out=wg[:].rearrange("p (c i) t -> p c t i", i=4),
+                                      in_=src.rearrange("p t (c i) -> p c t i", i=4))
+                wgs[n] = wg
+
+            def quant(n):
+                w = srcs[n][0]
+                nc.vector.quantize_mx(out=wcodes[:, w, :].bitcast(FP8X4), scales=wscales[:, w, :],
+                                      in_=wgs[n][:].rearrange("p n t -> p (n t)"))
+
+            regroup(0)
+            regroup(1)
+            quant(0)
+            regroup(2)
+            quant(1)
+            regroup(3)
+            quant(2)
+            quant(3)
+
+        def slot(s, wgrp):
+            parts = []
+            for bb in range(NBLK):
+                a = s - (PIECES * bb - 1)
+                if 0 <= a <= 4:
+                    parts.append((a, bb))
+            parts = dict(parts)
+            pair = s - LAG
+            has_pair = 0 <= pair < NPAIR
+            accs = c_mx(pair) if has_pair else None
+            gps = a_g_mx(parts[4]) if 4 in parts else None
+            if has_pair:
+                c_sum_tanh(pair, accs)
+            if 0 <= pair - 1 < NPAIR:
+                c_skip(pair - 1)
+            if gps is not None:
+                a_g_add(parts[4], gps)
+            if (s - 1) in VHALF:
+                vhalf_finish(s - 1)
+            if 0 in parts:
+                a_transposes(parts[0], (0, 1))
+                a_mean(parts[0], 0)
+            if 1 in parts:
+                a_transposes(parts[1], (2, 3))
+                a_mean(parts[1], 1)
+            if 2 in parts:
+                a_mean_transposes(parts[2])
+                a_quant_x(parts[2])
+            if 3 in parts:
+                a_quant_m(parts[3])
+            if 0 <= s < NPIECE:
+                bb, kp = divmod(s, PIECES)
+                if kp == 0:
+                    g2s[bb] = grp.tile([P, N, 4 * P], BF16, name="g2_%d" % bb, tag="g2", align_bytes=64)
+                pool_half(s, 0)
+                if s in VHALF:
+                    vhalf_add(s)
+                else:
+                    pool_half(s, 1)
+                if kp == PIECES - 1:
+                    quantise_e(bb)
+            if wgrp is not None:
+                prep_weights(wgrp)
+            if 0 <= s and (s + 1) % PIECES == 0 and (s + 1) // PIECES + 1 < NBLK:
+                load_x((s + 1) // PIECES + 1)
+            if 0 <= s and s + AHEAD < NPIECE:
+                load_piece(s + AHEAD)
+            done = pair - 1
+            if 0 <= done < 4:
+                store(done)
+            elif s == LAST_LOAD_SLOT + 1:
+                for pr in range(4, done + 1):
+                    store(pr)
+            elif s > LAST_LOAD_SLOT + 1 and done < NPAIR:
+                store(done)
+
+        bias_bc = const.tile([P, ND], BF16)
+        nc.scalar.dma_start(out=bias_bc[:], in_=b_unmixed.partition_broadcast(P))
+        wcodes = const.tile([P, 4, ND], U32, align_bytes=64)
+        wscales = const.tile([P, 4, ND], U8, align_bytes=64)
+        ident_f = const.tile([P, P], F32)
+        ident_b = const.tile([P, P], BF16)
+        red = const.tile([P, 2, 2, 4, 2], F32)
+        poolm = const.tile([P, 2, 4, 2, 2], BF16)
+        pool_rhs = poolm[:].rearrange("p s e a h -> p (s e) (a h)")
+
+        with tc.tile_pool(name="wraw", bufs=1) as wraw, tc.tile_pool(name="wgrp", bufs=2) as wgrp_pool:
+            load_x(0)
+            load_piece(0)
+            load_piece(1)
+            raw_m = wraw.tile([P, 8, ND], BF16)
+            nc.sync.dma_start(out=raw_m[:], in_=W_mixed.rearrange("(t p) n -> p t n", p=P))
+            raw_u = wraw.tile([P, 4, ND], BF16)
+            nc.sync.dma_start(out=raw_u[:].rearrange("p (u e) n -> p u e n", e=2),
+                              in_=W_unmixed.rearrange("(u p e) n -> p u e n", u=2, e=2))
+            raw_e = wraw.tile([P, 4, ND], BF16)
+            nc.sync.dma_start(out=raw_e[:], in_=W_2e.rearrange("(t p) n -> p t n", p=P))
+            load_piece(2)
+            load_x(1)
+            load_piece(3)
+
+            make_identity(nc, ident_f[:])
+            make_identity(nc, ident_b[:])
+            nc.vector.tensor_reduce(out=red[:].rearrange("p a s e j -> p (a s e j)"),
+                                    in_=ident_f[:].rearrange("p (g f) -> p g f", f=4),
+                                    axis=mybir.AxisListType.X, op=ADD)
+            for s in range(2):
+                for h in range(2):
+                    nc.vector.tensor_scalar_mul(out=poolm[:, s, :, :, h],
+                                                in0=red[:, :, s, :, h ^ s].rearrange("p a e -> p e a"),
+                                                scalar1=0.25)
+            slot(-1, None)
+            slot(0, None)
+            slot(1, wgrp_pool)
+
+        with tc.tile_pool(name="outp", bufs=12) as outp:
+            outp_box.append(outp)
+            for s in range(2, NPAIR + LAG + 1):
+                slot(s, None)

@@ -207,7 +207,8 @@ def tile_ferminetoneelectronlayer_pa_t_kernel(tc, in_1e, in_2e, W_unmixed, b_unm
             bb, q = divmod(pair, 4)
             o = outp_box[0].tile([P, 2, ND], F32, name="o%d" % pair, tag="o")
             for i2 in range(2):
-                nc.vector.tensor_tensor(out=o[:, i2, :], in0=zs[pair][i2][:], in1=xs[bb][:, 2 * q + i2, :], op=ADD)
+                eng = nc.vector if (bb == NBLK - 1 and i2 == 0) else nc.gpsimd
+                eng.tensor_tensor(out=o[:, i2, :], in0=zs[pair][i2][:], in1=xs[bb][:, 2 * q + i2, :], op=ADD)
             os_[pair] = o
 
         def store(pair):

@@ -17,10 +17,10 @@ PIECES = 4
 NPIECE = NBLK * PIECES
 NPAIR = NBLK * 4
 LAG = 4
-AHEAD = 4
-VHALF = (0, 1)
+AHEAD = 3
+MODES = ("PS", "PS", "PS", "PP") + ("PS", "PP", "PS", "PP") * 3
 LAST_LOAD_SLOT = NPIECE - AHEAD - 1
-WU, WA, WB, WE = 0, 1, 2, 3
+WU, WA, WB, WE0, WE1 = 0, 1, 2, 3, 4
 
 FLOPS = 2 * (B * N * D1 * ND + B * NS * NS * D1 * ND + B * N * NS * D2 * ND)
 
@@ -35,22 +35,22 @@ def tile_ferminetoneelectronlayer_pa_t_kernel(tc, in_1e, in_2e, W_unmixed, b_unm
          tc.tile_pool(name="xpool", bufs=4) as xpool, \
          tc.tile_pool(name="stage", bufs=AHEAD) as stage, \
          tc.tile_pool(name="grp", bufs=2) as grp, \
+         tc.tile_pool(name="one", bufs=1) as one, \
          tc.tile_pool(name="codes", bufs=2) as codes, \
-         tc.tile_pool(name="work", bufs=4) as work, \
+         tc.tile_pool(name="keep", bufs=4) as keep, \
          tc.psum_pool(name="ps", bufs=2) as ps:
 
         xs = {}
         pieces = {}
         g1s = {}
         g2s = {}
-        msums = {}
+        t1s = {}
         gms = {}
-        a2s = {}
+        longs = {}
         xq = {}
         mq = {}
         eq = {}
         gbs = {}
-        zs = {}
         os_ = {}
         outp_box = []
 
@@ -61,61 +61,69 @@ def tile_ferminetoneelectronlayer_pa_t_kernel(tc, in_1e, in_2e, W_unmixed, b_unm
 
         def load_piece(k):
             pc = stage.tile([P, 16, D2], BF16, name="pc%d" % k, tag="pc")
-            r0 = k * 16 * P
-            if k in VHALF:
-                nc.sync.dma_start(out=pc[:, 0:8, :], in_=rows2[r0:r0 + 8 * P, :].rearrange("(r p) d -> p r d", p=P))
-                t0 = (k * 32 + 16) * N
-                nc.sync.dma_start(out=pc[:, 8:16, :], in_=toks2[t0:t0 + P, :, :])
-            else:
+            if MODES[k] == "PP":
+                r0 = k * 16 * P
                 nc.sync.dma_start(out=pc[:], in_=rows2[r0:r0 + 16 * P, :].rearrange("(r p) d -> p r d", p=P))
+            else:
+                for half in range(2):
+                    dst = pc[:, 8 * half:8 * half + 8, :]
+                    if MODES[k][half] == "P":
+                        r0 = (k * 16 + 8 * half) * P
+                        nc.sync.dma_start(out=dst, in_=rows2[r0:r0 + 8 * P, :].rearrange("(r p) d -> p r d", p=P))
+                    else:
+                        t0 = (k * 32 + 16 * half) * N
+                        nc.sync.dma_start(out=dst, in_=toks2[t0:t0 + P, :, :])
             pieces[k] = pc
 
-        def a_transposes(bb, qs):
-            x = xs[bb]
-            xf = x[:].bitcast(F32)
-            if bb not in g1s:
-                g1s[bb] = grp.tile([P, N, P, 4], BF16, name="g1_%d" % bb, tag="g1", align_bytes=64)
+        def tx(bb):
+            xf = xs[bb][:].bitcast(F32)
+            g1s[bb] = grp.tile([P, N, P, 4], BF16, name="g1_%d" % bb, tag="g1", align_bytes=64)
             g1f = g1s[bb][:].rearrange("p i b t -> p i (b t)").bitcast(F32).rearrange("p i (b u) -> p i b u", u=2)
-            xts = []
-            for q in qs:
-                xt = ps.tile([P, 2, 2, P], F32, name="xt%d_%d" % (bb, q), tag="xt")
-                for i2 in range(2):
-                    for u in range(2):
-                        nc.tensor.transpose(xt[:, i2, u, :], xf[:, 2 * q + i2, u * P:(u + 1) * P], ident_f[:])
-                xts.append(xt)
-            for q, xt in zip(qs, xts):
-                nc.scalar.copy(out=g1f[:, 2 * q:2 * q + 2, :, :], in_=xt[:].rearrange("p i u b -> p i b u"))
+            for qs in ((0, 1), (2, 3)):
+                xts = []
+                for q in qs:
+                    xt = ps.tile([P, 2, 2, P], F32, name="xt%d_%d" % (bb, q), tag="xt")
+                    for i2 in range(2):
+                        for u in range(2):
+                            nc.tensor.transpose(xt[:, i2, u, :], xf[:, 2 * q + i2, u * P:(u + 1) * P], ident_f[:])
+                    xts.append(xt)
+                for q, xt in zip(qs, xts):
+                    nc.scalar.copy(out=g1f[:, 2 * q:2 * q + 2, :, :], in_=xt[:].rearrange("p i u b -> p i b u"))
 
-        def a_mean(bb, s):
+        def mean_add(bb):
             x = xs[bb]
-            if bb not in msums:
-                msums[bb] = grp.tile([P, 2, D1], BF16, name="ms%d" % bb, tag="ms")
-            t1 = grp.tile([P, 2, D1], F32, name="t1_%d_%d" % (bb, s), tag="t1")
-            nc.vector.tensor_tensor(out=t1[:], in0=x[:, 4 * s:4 * s + 2, :], in1=x[:, 4 * s + 2:4 * s + 4, :], op=ADD)
-            nc.vector.tensor_tensor(out=msums[bb][:, s, :], in0=t1[:, 0, :], in1=t1[:, 1, :], op=ADD)
-
-        def a_mean_transposes(bb):
-            mt = ps.tile([P, 2, 4, P], BF16, name="mt%d" % bb, tag="aux")
             for s in range(2):
-                for t in range(4):
-                    nc.tensor.transpose(mt[:, s, t, :], msums[bb][:, s, t * P:(t + 1) * P], ident_b[:])
+                t1 = grp.tile([P, 2, D1], F32, name="t1_%d_%d" % (bb, s), tag="t1")
+                nc.vector.tensor_tensor(out=t1[:], in0=x[:, 4 * s:4 * s + 2, :], in1=x[:, 4 * s + 2:4 * s + 4, :], op=ADD)
+                t1s[(bb, s)] = t1
+
+        def tm(bb):
             gm = grp.tile([P, 2, P, 4], BF16, name="gm%d" % bb, tag="gm", align_bytes=64)
-            nc.scalar.mul(out=gm[:], in_=mt[:].rearrange("p s t b -> p s b t"), mul=0.25)
+            mts = []
+            for s in range(2):
+                mt = ps.tile([P, 4, P], F32, name="mt%d_%d" % (bb, s), tag="aux")
+                for t in range(4):
+                    for a in range(2):
+                        nc.tensor.matmul(out=mt[:, t, :], lhsT=t1s[(bb, s)][:, a, t * P:(t + 1) * P], rhs=ident_f[:],
+                                         is_transpose=True, start=(a == 0), stop=(a == 1))
+                mts.append(mt)
+            for s in range(2):
+                nc.scalar.mul(out=gm[:, s, :, :], in_=mts[s][:].rearrange("p t b -> p b t"), mul=0.25)
             gms[bb] = gm
 
-        def a_quant_x(bb):
-            xc = codes.tile([P, N * P], U32, name="xc%d" % bb, tag="xc", align_bytes=64)
-            xsc = codes.tile([P, N * P], U8, name="xsc%d" % bb, tag="xsc", align_bytes=64)
+        def quant_x(bb):
+            xc = keep.tile([P, N * P], U32, name="xc%d" % bb, tag="xc", align_bytes=64)
+            xsc = keep.tile([P, N * P], U8, name="xsc%d" % bb, tag="xsc", align_bytes=64)
             nc.vector.quantize_mx(out=xc[:].bitcast(FP8X4), scales=xsc[:], in_=g1s[bb][:].rearrange("p i b t -> p (i b t)"))
             xq[bb] = (xc, xsc)
 
-        def a_quant_m(bb):
-            mc = codes.tile([P, 2 * P], U32, name="mc%d" % bb, tag="mc", align_bytes=64)
-            msc = codes.tile([P, 2 * P], U8, name="msc%d" % bb, tag="msc", align_bytes=64)
+        def quant_m(bb):
+            mc = keep.tile([P, 2 * P], U32, name="mc%d" % bb, tag="mc", align_bytes=64)
+            msc = keep.tile([P, 2 * P], U8, name="msc%d" % bb, tag="msc", align_bytes=64)
             nc.vector.quantize_mx(out=mc[:].bitcast(FP8X4), scales=msc[:], in_=gms[bb][:].rearrange("p s b t -> p (s b t)"))
             mq[bb] = (mc, msc)
 
-        def a_g_mx(bb):
+        def g_mx(bb):
             mc, msc = mq[bb]
             gps = []
             for s in range(2):
@@ -128,7 +136,7 @@ def tile_ferminetoneelectronlayer_pa_t_kernel(tc, in_1e, in_2e, W_unmixed, b_unm
                 gps.append(gp)
             return gps
 
-        def a_g_add(bb, gps):
+        def g_add(bb, gps):
             gb = grp.tile([P, 2, ND], F32, name="gb%d" % bb, tag="gb")
             for s in range(2):
                 nc.vector.tensor_tensor(out=gb[:, s, :], in0=gps[s][:], in1=bias_bc[:], op=ADD)
@@ -146,27 +154,31 @@ def tile_ferminetoneelectronlayer_pa_t_kernel(tc, in_1e, in_2e, W_unmixed, b_unm
             kk = 2 * kp + half
             nc.scalar.copy(out=g2s[bb][:, :, 64 * kk:64 * (kk + 1)], in_=pp[:])
 
-        def vhalf_add(k):
-            lv = pieces[k][:, 8:16, :].rearrange("p (a f) d -> p a f d", a=2)
-            t1 = grp.tile([P, 2, 2, D2], F32, name="vt1_%d" % k, tag="t1")
-            nc.vector.tensor_tensor(out=t1[:], in0=lv[:, :, 0:2, :], in1=lv[:, :, 2:4, :], op=ADD)
-            a2 = grp.tile([P, 2, D2], BF16, name="a2_%d" % k, tag="a2")
-            nc.vector.tensor_tensor(out=a2[:], in0=t1[:, :, 0, :], in1=t1[:, :, 1, :], op=ADD)
-            a2s[k] = a2
+        def long_first(k, half):
+            lv = pieces[k][:, 8 * half:8 * half + 8, :]
+            if MODES[k][half] == "S":
+                lf = one.tile([P, 8, D2], F32, name="lf%d_%d" % (k, half), tag="lf")
+                nc.scalar.copy(out=lf[:], in_=lv)
+                longs[(k, half)] = (lf, 4)
+            else:
+                l4 = lv.rearrange("p (a f) d -> p a f d", a=2)
+                t1 = grp.tile([P, 4, D2], F32, name="vt1_%d_%d" % (k, half), tag="t1")
+                nc.vector.tensor_tensor(out=t1[:].rearrange("p (a f) d -> p a f d", a=2),
+                                        in0=l4[:, :, 0:2, :], in1=l4[:, :, 2:4, :], op=ADD)
+                longs[(k, half)] = (t1, 2)
 
-        def vhalf_finish(k):
+        def long_finish(k, half):
             bb, kp = divmod(k, PIECES)
-            a2 = a2s[k]
-            vt = ps.tile([P, 4, P], BF16, name="vt%d" % k, tag="aux")
+            src, n = longs[(k, half)]
+            lt = ps.tile([P, 4, P], F32, name="lt%d_%d" % (k, half), tag="aux")
             for sj in range(2):
                 for c in range(2):
-                    nc.tensor.transpose(vt[:, 2 * sj + c, :], a2[:, sj, c * P:(c + 1) * P], ident_b[:])
-            vtv = vt[:].rearrange("p t (b i) -> p i b t", i=N)
-            kk = 2 * kp + 1
+                    for a in range(n):
+                        nc.tensor.matmul(out=lt[:, 2 * sj + c, :], lhsT=src[:, n * sj + a, c * P:(c + 1) * P],
+                                         rhs=ident_f[:], is_transpose=True, start=(a == 0), stop=(a == n - 1))
+            kk = 2 * kp + half
             g2v = g2s[bb][:].rearrange("p i (b t) -> p i b t", t=4)[:, :, 16 * kk:16 * (kk + 1), :]
-            nc.scalar.mul(out=g2v[:, 0:4, :, :], in_=vtv[:, 0:4, :, :], mul=0.25)
-            for h in range(2):
-                nc.scalar.mul(out=g2v[:, 4:8, :, 2 * h:2 * h + 2], in_=vtv[:, 4:8, :, 2 - 2 * h:4 - 2 * h], mul=0.25)
+            nc.scalar.mul(out=g2v, in_=lt[:].rearrange("p t (b i) -> p i b t", i=N), mul=0.25)
 
         def quantise_e(bb):
             ec = codes.tile([P, N * P], U32, name="ec%d" % bb, tag="ec", align_bytes=64)
@@ -178,6 +190,7 @@ def tile_ferminetoneelectronlayer_pa_t_kernel(tc, in_1e, in_2e, W_unmixed, b_unm
             bb, q = divmod(pair, 4)
             xc, xsc = xq[bb]
             ec, esc = eq[bb]
+            we = WE0 if q < 2 else WE1
             accs = []
             for i2 in range(2):
                 i = 2 * q + i2
@@ -187,105 +200,93 @@ def tile_ferminetoneelectronlayer_pa_t_kernel(tc, in_1e, in_2e, W_unmixed, b_unm
                                     rhs=wcodes[:, WU, :].bitcast(FP8X4), rhs_scale=wscales[:, WU, :],
                                     start=True, stop=False)
                 nc.tensor.matmul_mx(out=acc[:], lhsT=ec[:, cols].bitcast(FP8X4), lhsT_scale=esc[:, cols],
-                                    rhs=wcodes[:, WE, :].bitcast(FP8X4), rhs_scale=wscales[:, WE, :],
+                                    rhs=wcodes[:, we, :].bitcast(FP8X4), rhs_scale=wscales[:, we, :],
                                     start=False, stop=True)
                 accs.append(acc)
             return accs
 
         def c_sum_tanh(pair, accs):
             bb, q = divmod(pair, 4)
-            zz = []
+            o = outp_box[0].tile([P, 2, ND], F32, name="o%d" % pair, tag="o")
             for i2 in range(2):
-                z = work.tile([P, ND], F32, name="z%d_%d" % (pair, i2), tag="z")
-                nc.vector.tensor_tensor(out=z[:], in0=accs[i2][:], in1=gbs[bb][:, q // 2, :], op=ADD)
-                zz.append(z)
-            for i2 in range(2):
-                nc.scalar.activation(out=zz[i2][:], in_=zz[i2][:], func=ACT.Tanh)
-            zs[pair] = zz
+                nc.vector.tensor_tensor(out=o[:, i2, :], in0=accs[i2][:], in1=gbs[bb][:, q // 2, :], op=ADD)
+            nc.scalar.activation(out=o[:], in_=o[:], func=ACT.Tanh)
+            os_[pair] = o
 
         def c_skip(pair):
             bb, q = divmod(pair, 4)
-            o = outp_box[0].tile([P, 2, ND], F32, name="o%d" % pair, tag="o")
-            for i2 in range(2):
-                eng = nc.vector if (bb == NBLK - 1 and i2 == 0) else nc.gpsimd
-                eng.tensor_tensor(out=o[:, i2, :], in0=zs[pair][i2][:], in1=xs[bb][:, 2 * q + i2, :], op=ADD)
-            os_[pair] = o
+            o = os_[pair]
+            nc.vector.tensor_tensor(out=o[:], in0=o[:], in1=xs[bb][:, 2 * q:2 * q + 2, :], op=ADD)
 
         def store(pair):
             bb, q = divmod(pair, 4)
             nc.sync.dma_start(out=out[bb * P:(bb + 1) * P, 2 * q:2 * q + 2, :], in_=os_[pair][:])
 
-        def prep_weights(wgrp):
-            srcs = ((WA, raw_m[:, 0:4, :]), (WB, raw_m[:, 4:8, :]), (WU, raw_u[:]), (WE, raw_e[:]))
-            wgs = {}
+        wgs = {}
 
-            def regroup(n):
-                w, src = srcs[n]
-                wg = wgrp.tile([P, ND, 4], BF16, name="wg%d" % w, tag="wg", align_bytes=64)
-                nc.vector.tensor_copy(out=wg[:].rearrange("p (c i) t -> p c t i", i=4),
-                                      in_=src.rearrange("p t (c i) -> p c t i", i=4))
-                wgs[n] = wg
+        def regroup(w, parts):
+            wg = wgrp_box[0].tile([P, ND, 4], BF16, name="wg%d" % w, tag="wg", align_bytes=64)
+            wgv = wg[:].rearrange("p (c i) t -> p c t i", i=4)
+            for t0, src in parts:
+                nt = src.shape[1]
+                nc.vector.tensor_copy(out=wgv[:, :, t0:t0 + nt, :], in_=src.rearrange("p t (c i) -> p c t i", i=4))
+            wgs[w] = wg
 
-            def quant(n):
-                w = srcs[n][0]
-                nc.vector.quantize_mx(out=wcodes[:, w, :].bitcast(FP8X4), scales=wscales[:, w, :],
-                                      in_=wgs[n][:].rearrange("p n t -> p (n t)"))
+        def quant_w(w):
+            nc.vector.quantize_mx(out=wcodes[:, w, :].bitcast(FP8X4), scales=wscales[:, w, :],
+                                  in_=wgs[w][:].rearrange("p n t -> p (n t)"))
 
-            regroup(0)
-            regroup(1)
-            quant(0)
-            regroup(2)
-            quant(1)
-            regroup(3)
-            quant(2)
-            quant(3)
+        def prep_w_mixed():
+            regroup(WA, ((0, raw_m[:, 0:4, :]),))
+            regroup(WB, ((0, raw_m[:, 4:8, :]),))
+            quant_w(WA)
+            quant_w(WB)
 
-        def slot(s, wgrp):
-            parts = []
-            for bb in range(NBLK):
-                a = s - (PIECES * bb - 1)
-                if 0 <= a <= 4:
-                    parts.append((a, bb))
-            parts = dict(parts)
+        def prep_w_rest():
+            regroup(WU, ((0, raw_u[:]),))
+            regroup(WE0, ((0, raw_e[:]),))
+            quant_w(WU)
+            regroup(WE1, ((0, raw_e[:, 2:4, :]), (2, raw_e[:, 0:2, :])))
+            quant_w(WE0)
+            quant_w(WE1)
+
+        pre = {1: (lambda: tx(3), lambda: mean_add(3)),
+               2: (lambda: tm(3), lambda: quant_x(2), lambda: quant_m(2)),
+               3: (lambda: quant_x(3), lambda: quant_m(3))}
+        post = {0: (lambda: tm(2), prep_w_rest)}
+
+        def slot(s):
             pair = s - LAG
             has_pair = 0 <= pair < NPAIR
+            g_block = (s - 2) // PIECES if (s - 2) % PIECES == 0 and 0 <= (s - 2) // PIECES < NBLK else None
             accs = c_mx(pair) if has_pair else None
-            gps = a_g_mx(parts[4]) if 4 in parts else None
+            gps = g_mx(g_block) if g_block is not None else None
             if has_pair:
                 c_sum_tanh(pair, accs)
             if 0 <= pair - 1 < NPAIR:
                 c_skip(pair - 1)
             if gps is not None:
-                a_g_add(parts[4], gps)
-            if (s - 1) in VHALF:
-                vhalf_finish(s - 1)
-            if 0 in parts:
-                a_transposes(parts[0], (0, 1))
-                a_mean(parts[0], 0)
-            if 1 in parts:
-                a_transposes(parts[1], (2, 3))
-                a_mean(parts[1], 1)
-            if 2 in parts:
-                a_mean_transposes(parts[2])
-                a_quant_x(parts[2])
-            if 3 in parts:
-                a_quant_m(parts[3])
+                g_add(g_block, gps)
+            if 0 <= s - 1 < NPIECE:
+                for half in range(2):
+                    if MODES[s - 1][half] != "P":
+                        long_finish(s - 1, half)
+            for f in pre.get(s, ()):
+                f()
             if 0 <= s < NPIECE:
                 bb, kp = divmod(s, PIECES)
                 if kp == 0:
                     g2s[bb] = grp.tile([P, N, 4 * P], BF16, name="g2_%d" % bb, tag="g2", align_bytes=64)
-                pool_half(s, 0)
-                if s in VHALF:
-                    vhalf_add(s)
-                else:
-                    pool_half(s, 1)
+                for half in range(2):
+                    if MODES[s][half] == "P":
+                        pool_half(s, half)
+                    else:
+                        long_first(s, half)
                 if kp == PIECES - 1:
                     quantise_e(bb)
-            if wgrp is not None:
-                prep_weights(wgrp)
-            if 0 <= s and (s + 1) % PIECES == 0 and (s + 1) // PIECES + 1 < NBLK:
-                load_x((s + 1) // PIECES + 1)
-            if 0 <= s and s + AHEAD < NPIECE:
+            for f in post.get(s, ()):
+                f()
+            if s + AHEAD < NPIECE:
                 load_piece(s + AHEAD)
             done = pair - 1
             if 0 <= done < 4:
@@ -298,44 +299,52 @@ def tile_ferminetoneelectronlayer_pa_t_kernel(tc, in_1e, in_2e, W_unmixed, b_unm
 
         bias_bc = const.tile([P, ND], BF16)
         nc.scalar.dma_start(out=bias_bc[:], in_=b_unmixed.partition_broadcast(P))
-        wcodes = const.tile([P, 4, ND], U32, align_bytes=64)
-        wscales = const.tile([P, 4, ND], U8, align_bytes=64)
+        wcodes = const.tile([P, 5, ND], U32, align_bytes=64)
+        wscales = const.tile([P, 5, ND], U8, align_bytes=64)
         ident_f = const.tile([P, P], F32)
-        ident_b = const.tile([P, P], BF16)
-        red = const.tile([P, 2, 2, 4, 2], F32)
-        poolm = const.tile([P, 2, 4, 2, 2], BF16)
-        pool_rhs = poolm[:].rearrange("p s e a h -> p (s e) (a h)")
+        red = const.tile([P, 2, 8, 2], F32)
+        poolm = const.tile([P, 8, 2, 2], BF16)
+        pool_rhs = poolm[:].rearrange("p i a j -> p i (a j)")
+        wgrp_box = []
 
         with tc.tile_pool(name="wraw", bufs=1) as wraw, tc.tile_pool(name="wgrp", bufs=2) as wgrp_pool:
+            wgrp_box.append(wgrp_pool)
             load_x(0)
-            load_piece(0)
-            load_piece(1)
+            load_x(1)
             raw_m = wraw.tile([P, 8, ND], BF16)
             nc.sync.dma_start(out=raw_m[:], in_=W_mixed.rearrange("(t p) n -> p t n", p=P))
+            load_x(2)
             raw_u = wraw.tile([P, 4, ND], BF16)
             nc.sync.dma_start(out=raw_u[:].rearrange("p (u e) n -> p u e n", e=2),
                               in_=W_unmixed.rearrange("(u p e) n -> p u e n", u=2, e=2))
             raw_e = wraw.tile([P, 4, ND], BF16)
             nc.sync.dma_start(out=raw_e[:], in_=W_2e.rearrange("(t p) n -> p t n", p=P))
-            load_piece(2)
-            load_x(1)
-            load_piece(3)
+            load_x(3)
+            for k in range(AHEAD):
+                load_piece(k)
 
             make_identity(nc, ident_f[:])
-            make_identity(nc, ident_b[:])
-            nc.vector.tensor_reduce(out=red[:].rearrange("p a s e j -> p (a s e j)"),
+            nc.vector.tensor_reduce(out=red[:].rearrange("p a i j -> p (a i j)"),
                                     in_=ident_f[:].rearrange("p (g f) -> p g f", f=4),
                                     axis=mybir.AxisListType.X, op=ADD)
-            for s in range(2):
-                for h in range(2):
-                    nc.vector.tensor_scalar_mul(out=poolm[:, s, :, :, h],
-                                                in0=red[:, :, s, :, h ^ s].rearrange("p a e -> p e a"),
-                                                scalar1=0.25)
-            slot(-1, None)
-            slot(0, None)
-            slot(1, wgrp_pool)
+            nc.vector.tensor_scalar_mul(out=poolm[:], in0=red[:].rearrange("p a i j -> p i a j"), scalar1=0.25)
+
+            tx(0)
+            mean_add(0)
+            tx(1)
+            tm(0)
+            mean_add(1)
+            tm(1)
+            prep_w_mixed()
+            quant_x(0)
+            quant_m(0)
+            quant_x(1)
+            quant_m(1)
+            tx(2)
+            mean_add(2)
+            slot(0)
 
         with tc.tile_pool(name="outp", bufs=12) as outp:
             outp_box.append(outp)
-            for s in range(2, NPAIR + LAG + 1):
-                slot(s, None)
+            for s in range(1, NPAIR + LAG + 1):
+                slot(s)

@@ -16,9 +16,9 @@ NBLK = B // P
 PIECES = 4
 NPIECE = NBLK * PIECES
 NPAIR = NBLK * 4
-LAG = 4
+LAG = 5
 AHEAD = 3
-MODES = ("PS", "PS", "PS", "PP") + ("PS", "PP", "PS", "PP") * 3
+MODES = ("PP", "PP", "PP", "PP", "SP") + ("PP",) * 11
 LAST_LOAD_SLOT = NPIECE - AHEAD - 1
 WU, WA, WB, WE0, WE1 = 0, 1, 2, 3, 4
 
@@ -35,10 +35,11 @@ def tile_ferminetoneelectronlayer_pa_t_kernel(tc, in_1e, in_2e, W_unmixed, b_unm
          tc.tile_pool(name="xpool", bufs=4) as xpool, \
          tc.tile_pool(name="stage", bufs=AHEAD) as stage, \
          tc.tile_pool(name="grp", bufs=2) as grp, \
-         tc.tile_pool(name="one", bufs=1) as one, \
+         tc.tile_pool(name="one", bufs=2) as one, \
          tc.tile_pool(name="codes", bufs=2) as codes, \
          tc.tile_pool(name="keep", bufs=4) as keep, \
-         tc.psum_pool(name="ps", bufs=2) as ps:
+         tc.psum_pool(name="ps", bufs=2) as ps, \
+         tc.psum_pool(name="ps4", bufs=4) as ps4:
 
         xs = {}
         pieces = {}
@@ -47,6 +48,9 @@ def tile_ferminetoneelectronlayer_pa_t_kernel(tc, in_1e, in_2e, W_unmixed, b_unm
         t1s = {}
         gms = {}
         longs = {}
+        lts = {}
+        accs_of = {}
+        gps_of = {}
         xq = {}
         mq = {}
         eq = {}
@@ -77,12 +81,12 @@ def tile_ferminetoneelectronlayer_pa_t_kernel(tc, in_1e, in_2e, W_unmixed, b_unm
 
         def tx(bb):
             xf = xs[bb][:].bitcast(F32)
-            g1s[bb] = grp.tile([P, N, P, 4], BF16, name="g1_%d" % bb, tag="g1", align_bytes=64)
+            g1s[bb] = early_box[0].tile([P, N, P, 4], BF16, name="g1_%d" % bb, tag="g1", align_bytes=64)
             g1f = g1s[bb][:].rearrange("p i b t -> p i (b t)").bitcast(F32).rearrange("p i (b u) -> p i b u", u=2)
             for qs in ((0, 1), (2, 3)):
                 xts = []
                 for q in qs:
-                    xt = ps.tile([P, 2, 2, P], F32, name="xt%d_%d" % (bb, q), tag="xt")
+                    xt = ps4.tile([P, 2, 2, P], F32, name="xt%d_%d" % (bb, q), tag="acc")
                     for i2 in range(2):
                         for u in range(2):
                             nc.tensor.transpose(xt[:, i2, u, :], xf[:, 2 * q + i2, u * P:(u + 1) * P], ident_f[:])
@@ -93,12 +97,12 @@ def tile_ferminetoneelectronlayer_pa_t_kernel(tc, in_1e, in_2e, W_unmixed, b_unm
         def mean_add(bb):
             x = xs[bb]
             for s in range(2):
-                t1 = grp.tile([P, 2, D1], F32, name="t1_%d_%d" % (bb, s), tag="t1")
+                t1 = early_box[0].tile([P, 2, D1], F32, name="t1_%d_%d" % (bb, s), tag="t1")
                 nc.vector.tensor_tensor(out=t1[:], in0=x[:, 4 * s:4 * s + 2, :], in1=x[:, 4 * s + 2:4 * s + 4, :], op=ADD)
                 t1s[(bb, s)] = t1
 
         def tm(bb):
-            gm = grp.tile([P, 2, P, 4], BF16, name="gm%d" % bb, tag="gm", align_bytes=64)
+            gm = early_box[0].tile([P, 2, P, 4], BF16, name="gm%d" % bb, tag="gm", align_bytes=64)
             mts = []
             for s in range(2):
                 mt = ps.tile([P, 4, P], F32, name="mt%d_%d" % (bb, s), tag="aux")
@@ -162,13 +166,12 @@ def tile_ferminetoneelectronlayer_pa_t_kernel(tc, in_1e, in_2e, W_unmixed, b_unm
                 longs[(k, half)] = (lf, 4)
             else:
                 l4 = lv.rearrange("p (a f) d -> p a f d", a=2)
-                t1 = grp.tile([P, 4, D2], F32, name="vt1_%d_%d" % (k, half), tag="t1")
+                t1 = grp.tile([P, 4, D2], F32, name="vt1_%d_%d" % (k, half), tag="t1v")
                 nc.vector.tensor_tensor(out=t1[:].rearrange("p (a f) d -> p a f d", a=2),
                                         in0=l4[:, :, 0:2, :], in1=l4[:, :, 2:4, :], op=ADD)
                 longs[(k, half)] = (t1, 2)
 
-        def long_finish(k, half):
-            bb, kp = divmod(k, PIECES)
+        def long_t(k, half):
             src, n = longs[(k, half)]
             lt = ps.tile([P, 4, P], F32, name="lt%d_%d" % (k, half), tag="aux")
             for sj in range(2):
@@ -176,6 +179,11 @@ def tile_ferminetoneelectronlayer_pa_t_kernel(tc, in_1e, in_2e, W_unmixed, b_unm
                     for a in range(n):
                         nc.tensor.matmul(out=lt[:, 2 * sj + c, :], lhsT=src[:, n * sj + a, c * P:(c + 1) * P],
                                          rhs=ident_f[:], is_transpose=True, start=(a == 0), stop=(a == n - 1))
+            lts[(k, half)] = lt
+
+        def long_evac(k, half):
+            bb, kp = divmod(k, PIECES)
+            lt = lts[(k, half)]
             kk = 2 * kp + half
             g2v = g2s[bb][:].rearrange("p i (b t) -> p i b t", t=4)[:, :, 16 * kk:16 * (kk + 1), :]
             nc.scalar.mul(out=g2v, in_=lt[:].rearrange("p t (b i) -> p i b t", i=N), mul=0.25)
@@ -195,7 +203,7 @@ def tile_ferminetoneelectronlayer_pa_t_kernel(tc, in_1e, in_2e, W_unmixed, b_unm
             for i2 in range(2):
                 i = 2 * q + i2
                 cols = slice(i * P, (i + 1) * P)
-                acc = ps.tile([P, ND], F32, name="acc%d_%d" % (bb, i), tag="acc")
+                acc = ps4.tile([P, ND], F32, name="acc%d_%d" % (bb, i), tag="acc")
                 nc.tensor.matmul_mx(out=acc[:], lhsT=xc[:, cols].bitcast(FP8X4), lhsT_scale=xsc[:, cols],
                                     rhs=wcodes[:, WU, :].bitcast(FP8X4), rhs_scale=wscales[:, WU, :],
                                     start=True, stop=False)
@@ -205,13 +213,15 @@ def tile_ferminetoneelectronlayer_pa_t_kernel(tc, in_1e, in_2e, W_unmixed, b_unm
                 accs.append(acc)
             return accs
 
-        def c_sum_tanh(pair, accs):
+        def c_sum(pair):
             bb, q = divmod(pair, 4)
             o = outp_box[0].tile([P, 2, ND], F32, name="o%d" % pair, tag="o")
             for i2 in range(2):
-                nc.vector.tensor_tensor(out=o[:, i2, :], in0=accs[i2][:], in1=gbs[bb][:, q // 2, :], op=ADD)
-            nc.scalar.activation(out=o[:], in_=o[:], func=ACT.Tanh)
+                nc.vector.tensor_tensor(out=o[:, i2, :], in0=accs_of[pair][i2][:], in1=gbs[bb][:, q // 2, :], op=ADD)
             os_[pair] = o
+
+        def c_tanh(pair):
+            nc.scalar.activation(out=os_[pair][:], in_=os_[pair][:], func=ACT.Tanh)
 
         def c_skip(pair):
             bb, q = divmod(pair, 4)
@@ -250,49 +260,54 @@ def tile_ferminetoneelectronlayer_pa_t_kernel(tc, in_1e, in_2e, W_unmixed, b_unm
             quant_w(WE0)
             quant_w(WE1)
 
-        pre = {1: (lambda: tx(3), lambda: mean_add(3)),
-               2: (lambda: tm(3), lambda: quant_x(2), lambda: quant_m(2)),
-               3: (lambda: quant_x(3), lambda: quant_m(3))}
-        post = {0: (lambda: tm(2), prep_w_rest)}
+        extra = {1: (lambda: tx(3), lambda: tm(2), lambda: mean_add(3)),
+                 2: (lambda: tm(3), prep_w_rest),
+                 3: (lambda: quant_x(2), lambda: quant_m(2), lambda: quant_x(3), lambda: quant_m(3))}
+
+        def long_halves(k):
+            if 0 <= k < NPIECE:
+                return [half for half in range(2) if MODES[k][half] != "P"]
+            return []
 
         def slot(s):
             pair = s - LAG
             has_pair = 0 <= pair < NPAIR
-            g_block = (s - 2) // PIECES if (s - 2) % PIECES == 0 and 0 <= (s - 2) // PIECES < NBLK else None
-            accs = c_mx(pair) if has_pair else None
-            gps = g_mx(g_block) if g_block is not None else None
+            in_pieces = 0 <= s < NPIECE
+            bb, kp = divmod(s, PIECES)
+            if in_pieces and kp == 0:
+                g2s[bb] = grp.tile([P, N, 4 * P], BF16, name="g2_%d" % bb, tag="g2", align_bytes=64)
             if has_pair:
-                c_sum_tanh(pair, accs)
+                c_sum(pair)
             if 0 <= pair - 1 < NPAIR:
                 c_skip(pair - 1)
-            if gps is not None:
-                g_add(g_block, gps)
-            if 0 <= s - 1 < NPIECE:
-                for half in range(2):
-                    if MODES[s - 1][half] != "P":
-                        long_finish(s - 1, half)
-            for f in pre.get(s, ()):
+            if kp == 0 and 0 < bb < NBLK:
+                g_add(bb, gps_of[bb])
+            for f in extra.get(s, ()):
                 f()
-            if 0 <= s < NPIECE:
-                bb, kp = divmod(s, PIECES)
-                if kp == 0:
-                    g2s[bb] = grp.tile([P, N, 4 * P], BF16, name="g2_%d" % bb, tag="g2", align_bytes=64)
+            for half in long_halves(s - 2):
+                long_evac(s - 2, half)
+            if in_pieces:
+                for half in range(2):
+                    if MODES[s][half] != "P":
+                        long_first(s, half)
                 for half in range(2):
                     if MODES[s][half] == "P":
                         pool_half(s, half)
-                    else:
-                        long_first(s, half)
-                if kp == PIECES - 1:
-                    quantise_e(bb)
-            for f in post.get(s, ()):
-                f()
+            if has_pair:
+                c_tanh(pair)
+            if in_pieces and kp == PIECES - 1:
+                quantise_e(bb)
+            for half in long_halves(s - 1):
+                long_t(s - 1, half)
+            if 0 <= pair + 1 < NPAIR:
+                accs_of[pair + 1] = c_mx(pair + 1)
+            if kp == PIECES - 1 and 0 < bb + 1 < NBLK:
+                gps_of[bb + 1] = g_mx(bb + 1)
             if s + AHEAD < NPIECE:
                 load_piece(s + AHEAD)
             done = pair - 1
-            if 0 <= done < 4:
-                store(done)
-            elif s == LAST_LOAD_SLOT + 1:
-                for pr in range(4, done + 1):
+            if s == LAST_LOAD_SLOT + 1:
+                for pr in range(0, done + 1):
                     store(pr)
             elif s > LAST_LOAD_SLOT + 1 and done < NPAIR:
                 store(done)
@@ -306,9 +321,12 @@ def tile_ferminetoneelectronlayer_pa_t_kernel(tc, in_1e, in_2e, W_unmixed, b_unm
         poolm = const.tile([P, 8, 2, 2], BF16)
         pool_rhs = poolm[:].rearrange("p i a j -> p i (a j)")
         wgrp_box = []
+        early_box = []
 
-        with tc.tile_pool(name="wraw", bufs=1) as wraw, tc.tile_pool(name="wgrp", bufs=2) as wgrp_pool:
+        with tc.tile_pool(name="wraw", bufs=1) as wraw, tc.tile_pool(name="wgrp", bufs=2) as wgrp_pool, \
+             tc.tile_pool(name="early", bufs=2) as early_pool:
             wgrp_box.append(wgrp_pool)
+            early_box.append(early_pool)
             load_x(0)
             load_x(1)
             raw_m = wraw.tile([P, 8, ND], BF16)
@@ -340,11 +358,13 @@ def tile_ferminetoneelectronlayer_pa_t_kernel(tc, in_1e, in_2e, W_unmixed, b_unm
             quant_m(0)
             quant_x(1)
             quant_m(1)
+            g_add(0, g_mx(0))
             tx(2)
             mean_add(2)
-            slot(0)
+            for s in range(4):
+                slot(s)
 
-        with tc.tile_pool(name="outp", bufs=12) as outp:
+        with tc.tile_pool(name="outp", bufs=NPAIR) as outp:
             outp_box.append(outp)
-            for s in range(1, NPAIR + LAG + 1):
+            for s in range(4, NPAIR + LAG + 1):
                 slot(s)

@@ -16,13 +16,20 @@ NBLK = B // P
 PIECES = 4
 NPIECE = NBLK * PIECES
 NPAIR = NBLK * 4
-LAG = 5
 AHEAD = 3
-MODES = ("PP", "PP", "PP", "PP", "SP") + ("PP",) * 11
+MODES = ("PP",) * 4 + ("HP",) + ("PP",) * 11
 LAST_LOAD_SLOT = NPIECE - AHEAD - 1
 WU, WA, WB, WE0, WE1 = 0, 1, 2, 3, 4
 
 FLOPS = 2 * (B * N * D1 * ND + B * NS * NS * D1 * ND + B * N * NS * D2 * ND)
+
+
+def sum_slot(pair):
+    return PIECES * (pair // 4) + 5 + (0, 1, 1, 2)[pair % 4]
+
+
+def pairs_at(s):
+    return [pair for pair in range(NPAIR) if sum_slot(pair) == s]
 
 
 def tile_ferminetoneelectronlayer_pa_t_kernel(tc, in_1e, in_2e, W_unmixed, b_unmixed, W_mixed, W_2e, out):
@@ -35,7 +42,6 @@ def tile_ferminetoneelectronlayer_pa_t_kernel(tc, in_1e, in_2e, W_unmixed, b_unm
          tc.tile_pool(name="xpool", bufs=4) as xpool, \
          tc.tile_pool(name="stage", bufs=AHEAD) as stage, \
          tc.tile_pool(name="grp", bufs=2) as grp, \
-         tc.tile_pool(name="one", bufs=2) as one, \
          tc.tile_pool(name="codes", bufs=2) as codes, \
          tc.tile_pool(name="keep", bufs=4) as keep, \
          tc.psum_pool(name="ps", bufs=2) as ps, \
@@ -47,7 +53,7 @@ def tile_ferminetoneelectronlayer_pa_t_kernel(tc, in_1e, in_2e, W_unmixed, b_unm
         g2s = {}
         t1s = {}
         gms = {}
-        longs = {}
+        a2s = {}
         lts = {}
         accs_of = {}
         gps_of = {}
@@ -56,7 +62,11 @@ def tile_ferminetoneelectronlayer_pa_t_kernel(tc, in_1e, in_2e, W_unmixed, b_unm
         eq = {}
         gbs = {}
         os_ = {}
+        quads = {}
+        state = {"ready": []}
         outp_box = []
+        wgrp_box = []
+        wgs = {}
 
         def load_x(bb):
             x = xpool.tile([P, N, D1], BF16, name="x%d" % bb, tag="x")
@@ -81,7 +91,7 @@ def tile_ferminetoneelectronlayer_pa_t_kernel(tc, in_1e, in_2e, W_unmixed, b_unm
 
         def tx(bb):
             xf = xs[bb][:].bitcast(F32)
-            g1s[bb] = early_box[0].tile([P, N, P, 4], BF16, name="g1_%d" % bb, tag="g1", align_bytes=64)
+            g1s[bb] = grp.tile([P, N, P, 4], BF16, name="g1_%d" % bb, tag="g1", align_bytes=64)
             g1f = g1s[bb][:].rearrange("p i b t -> p i (b t)").bitcast(F32).rearrange("p i (b u) -> p i b u", u=2)
             for qs in ((0, 1), (2, 3)):
                 xts = []
@@ -97,12 +107,12 @@ def tile_ferminetoneelectronlayer_pa_t_kernel(tc, in_1e, in_2e, W_unmixed, b_unm
         def mean_add(bb):
             x = xs[bb]
             for s in range(2):
-                t1 = early_box[0].tile([P, 2, D1], F32, name="t1_%d_%d" % (bb, s), tag="t1")
+                t1 = grp.tile([P, 2, D1], F32, name="t1_%d_%d" % (bb, s), tag="t1")
                 nc.vector.tensor_tensor(out=t1[:], in0=x[:, 4 * s:4 * s + 2, :], in1=x[:, 4 * s + 2:4 * s + 4, :], op=ADD)
                 t1s[(bb, s)] = t1
 
         def tm(bb):
-            gm = early_box[0].tile([P, 2, P, 4], BF16, name="gm%d" % bb, tag="gm", align_bytes=64)
+            gm = grp.tile([P, 2, P, 4], BF16, name="gm%d" % bb, tag="gm", align_bytes=64)
             mts = []
             for s in range(2):
                 mt = ps.tile([P, 4, P], F32, name="mt%d_%d" % (bb, s), tag="aux")
@@ -159,34 +169,28 @@ def tile_ferminetoneelectronlayer_pa_t_kernel(tc, in_1e, in_2e, W_unmixed, b_unm
             nc.scalar.copy(out=g2s[bb][:, :, 64 * kk:64 * (kk + 1)], in_=pp[:])
 
         def long_first(k, half):
-            lv = pieces[k][:, 8 * half:8 * half + 8, :]
-            if MODES[k][half] == "S":
-                lf = one.tile([P, 8, D2], F32, name="lf%d_%d" % (k, half), tag="lf")
-                nc.scalar.copy(out=lf[:], in_=lv)
-                longs[(k, half)] = (lf, 4)
-            else:
-                l4 = lv.rearrange("p (a f) d -> p a f d", a=2)
-                t1 = grp.tile([P, 4, D2], F32, name="vt1_%d_%d" % (k, half), tag="t1v")
-                nc.vector.tensor_tensor(out=t1[:].rearrange("p (a f) d -> p a f d", a=2),
-                                        in0=l4[:, :, 0:2, :], in1=l4[:, :, 2:4, :], op=ADD)
-                longs[(k, half)] = (t1, 2)
+            eng = nc.gpsimd if MODES[k][half] == "H" else nc.vector
+            l4 = pieces[k][:, 8 * half:8 * half + 8, :].rearrange("p (a f) d -> p a f d", a=2)
+            t1 = grp.tile([P, 2, 2, D2], F32, name="lt1_%d_%d" % (k, half), tag="t1")
+            for sj in range(2):
+                eng.tensor_tensor(out=t1[:, sj, :, :], in0=l4[:, sj, 0:2, :], in1=l4[:, sj, 2:4, :], op=ADD)
+            a2 = grp.tile([P, 2, D2], BF16, name="a2_%d_%d" % (k, half), tag="a2")
+            eng.tensor_tensor(out=a2[:], in0=t1[:, :, 0, :], in1=t1[:, :, 1, :], op=ADD)
+            a2s[(k, half)] = a2
 
         def long_t(k, half):
-            src, n = longs[(k, half)]
-            lt = ps.tile([P, 4, P], F32, name="lt%d_%d" % (k, half), tag="aux")
+            a2 = a2s[(k, half)]
+            lt = ps.tile([P, 4, P], BF16, name="lt%d_%d" % (k, half), tag="aux")
             for sj in range(2):
                 for c in range(2):
-                    for a in range(n):
-                        nc.tensor.matmul(out=lt[:, 2 * sj + c, :], lhsT=src[:, n * sj + a, c * P:(c + 1) * P],
-                                         rhs=ident_f[:], is_transpose=True, start=(a == 0), stop=(a == n - 1))
+                    nc.tensor.transpose(lt[:, 2 * sj + c, :], a2[:, sj, c * P:(c + 1) * P], ident_b[:])
             lts[(k, half)] = lt
 
         def long_evac(k, half):
             bb, kp = divmod(k, PIECES)
-            lt = lts[(k, half)]
             kk = 2 * kp + half
             g2v = g2s[bb][:].rearrange("p i (b t) -> p i b t", t=4)[:, :, 16 * kk:16 * (kk + 1), :]
-            nc.scalar.mul(out=g2v, in_=lt[:].rearrange("p t (b i) -> p i b t", i=N), mul=0.25)
+            nc.scalar.mul(out=g2v, in_=lts[(k, half)][:].rearrange("p t (b i) -> p i b t", i=N), mul=0.25)
 
         def quantise_e(bb):
             ec = codes.tile([P, N * P], U32, name="ec%d" % bb, tag="ec", align_bytes=64)
@@ -211,28 +215,31 @@ def tile_ferminetoneelectronlayer_pa_t_kernel(tc, in_1e, in_2e, W_unmixed, b_unm
                                     rhs=wcodes[:, we, :].bitcast(FP8X4), rhs_scale=wscales[:, we, :],
                                     start=False, stop=True)
                 accs.append(acc)
-            return accs
+            accs_of[pair] = accs
 
         def c_sum(pair):
             bb, q = divmod(pair, 4)
-            o = outp_box[0].tile([P, 2, ND], F32, name="o%d" % pair, tag="o")
+            if bb < NBLK - 1:
+                if q % 2 == 0:
+                    quads[(bb, q // 2)] = outp_box[0].tile([P, 4, ND], F32, name="oq%d_%d" % (bb, q // 2), tag="oq", bufs=6)
+                o = quads[(bb, q // 2)][:, 2 * (q % 2):2 * (q % 2) + 2, :]
+            else:
+                ot = outp_box[0].tile([P, 2, ND], F32, name="o%d" % pair, tag="o", bufs=4)
+                o = ot[:]
             for i2 in range(2):
                 nc.vector.tensor_tensor(out=o[:, i2, :], in0=accs_of[pair][i2][:], in1=gbs[bb][:, q // 2, :], op=ADD)
             os_[pair] = o
 
         def c_tanh(pair):
-            nc.scalar.activation(out=os_[pair][:], in_=os_[pair][:], func=ACT.Tanh)
+            nc.scalar.activation(out=os_[pair], in_=os_[pair], func=ACT.Tanh)
 
         def c_skip(pair):
             bb, q = divmod(pair, 4)
-            o = os_[pair]
-            nc.vector.tensor_tensor(out=o[:], in0=o[:], in1=xs[bb][:, 2 * q:2 * q + 2, :], op=ADD)
-
-        def store(pair):
-            bb, q = divmod(pair, 4)
-            nc.sync.dma_start(out=out[bb * P:(bb + 1) * P, 2 * q:2 * q + 2, :], in_=os_[pair][:])
-
-        wgs = {}
+            nc.vector.tensor_tensor(out=os_[pair], in0=os_[pair], in1=xs[bb][:, 2 * q:2 * q + 2, :], op=ADD)
+            if bb == NBLK - 1:
+                state["ready"].append((out[bb * P:(bb + 1) * P, 2 * q:2 * q + 2, :], os_[pair]))
+            elif q % 2 == 1:
+                state["ready"].append((out[bb * P:(bb + 1) * P, 2 * q - 2:2 * q + 2, :], quads[(bb, q // 2)][:]))
 
         def regroup(w, parts):
             wg = wgrp_box[0].tile([P, ND, 4], BF16, name="wg%d" % w, tag="wg", align_bytes=64)
@@ -262,7 +269,8 @@ def tile_ferminetoneelectronlayer_pa_t_kernel(tc, in_1e, in_2e, W_unmixed, b_unm
 
         extra = {1: (lambda: tx(3), lambda: tm(2), lambda: mean_add(3)),
                  2: (lambda: tm(3), prep_w_rest),
-                 3: (lambda: quant_x(2), lambda: quant_m(2), lambda: quant_x(3), lambda: quant_m(3))}
+                 4: (lambda: quant_x(2), lambda: quant_m(2)),
+                 5: (lambda: quant_x(3), lambda: quant_m(3))}
 
         def long_halves(k):
             if 0 <= k < NPIECE:
@@ -270,16 +278,14 @@ def tile_ferminetoneelectronlayer_pa_t_kernel(tc, in_1e, in_2e, W_unmixed, b_unm
             return []
 
         def slot(s):
-            pair = s - LAG
-            has_pair = 0 <= pair < NPAIR
             in_pieces = 0 <= s < NPIECE
             bb, kp = divmod(s, PIECES)
             if in_pieces and kp == 0:
                 g2s[bb] = grp.tile([P, N, 4 * P], BF16, name="g2_%d" % bb, tag="g2", align_bytes=64)
-            if has_pair:
+            for pair in pairs_at(s):
                 c_sum(pair)
-            if 0 <= pair - 1 < NPAIR:
-                c_skip(pair - 1)
+            for pair in pairs_at(s - 1):
+                c_skip(pair)
             if kp == 0 and 0 < bb < NBLK:
                 g_add(bb, gps_of[bb])
             for f in extra.get(s, ()):
@@ -293,40 +299,35 @@ def tile_ferminetoneelectronlayer_pa_t_kernel(tc, in_1e, in_2e, W_unmixed, b_unm
                 for half in range(2):
                     if MODES[s][half] == "P":
                         pool_half(s, half)
-            if has_pair:
+            for pair in pairs_at(s):
                 c_tanh(pair)
             if in_pieces and kp == PIECES - 1:
                 quantise_e(bb)
             for half in long_halves(s - 1):
                 long_t(s - 1, half)
-            if 0 <= pair + 1 < NPAIR:
-                accs_of[pair + 1] = c_mx(pair + 1)
+            for pair in pairs_at(s + 1):
+                c_mx(pair)
             if kp == PIECES - 1 and 0 < bb + 1 < NBLK:
                 gps_of[bb + 1] = g_mx(bb + 1)
             if s + AHEAD < NPIECE:
                 load_piece(s + AHEAD)
-            done = pair - 1
-            if s == LAST_LOAD_SLOT + 1:
-                for pr in range(0, done + 1):
-                    store(pr)
-            elif s > LAST_LOAD_SLOT + 1 and done < NPAIR:
-                store(done)
+            if s > LAST_LOAD_SLOT:
+                for dst, src in state["ready"]:
+                    nc.sync.dma_start(out=dst, in_=src)
+                state["ready"] = []
 
         bias_bc = const.tile([P, ND], BF16)
         nc.scalar.dma_start(out=bias_bc[:], in_=b_unmixed.partition_broadcast(P))
         wcodes = const.tile([P, 5, ND], U32, align_bytes=64)
         wscales = const.tile([P, 5, ND], U8, align_bytes=64)
         ident_f = const.tile([P, P], F32)
+        ident_b = const.tile([P, P], BF16)
         red = const.tile([P, 2, 8, 2], F32)
         poolm = const.tile([P, 8, 2, 2], BF16)
         pool_rhs = poolm[:].rearrange("p i a j -> p i (a j)")
-        wgrp_box = []
-        early_box = []
 
-        with tc.tile_pool(name="wraw", bufs=1) as wraw, tc.tile_pool(name="wgrp", bufs=2) as wgrp_pool, \
-             tc.tile_pool(name="early", bufs=2) as early_pool:
+        with tc.tile_pool(name="wraw", bufs=1) as wraw, tc.tile_pool(name="wgrp", bufs=2) as wgrp_pool:
             wgrp_box.append(wgrp_pool)
-            early_box.append(early_pool)
             load_x(0)
             load_x(1)
             raw_m = wraw.tile([P, 8, ND], BF16)
@@ -342,6 +343,7 @@ def tile_ferminetoneelectronlayer_pa_t_kernel(tc, in_1e, in_2e, W_unmixed, b_unm
                 load_piece(k)
 
             make_identity(nc, ident_f[:])
+            make_identity(nc, ident_b[:])
             nc.vector.tensor_reduce(out=red[:].rearrange("p a i j -> p (a i j)"),
                                     in_=ident_f[:].rearrange("p (g f) -> p g f", f=4),
                                     axis=mybir.AxisListType.X, op=ADD)
@@ -361,10 +363,10 @@ def tile_ferminetoneelectronlayer_pa_t_kernel(tc, in_1e, in_2e, W_unmixed, b_unm
             g_add(0, g_mx(0))
             tx(2)
             mean_add(2)
-            for s in range(4):
+            for s in range(3):
                 slot(s)
 
-        with tc.tile_pool(name="outp", bufs=NPAIR) as outp:
+        with tc.tile_pool(name="outp", bufs=1) as outp:
             outp_box.append(outp)
-            for s in range(4, NPAIR + LAG + 1):
+            for s in range(3, sum_slot(NPAIR - 1) + 2):
                 slot(s)

@@ -17,7 +17,7 @@ PIECES = 4
 NPIECE = NBLK * PIECES
 NPAIR = NBLK * 4
 AHEAD = 3
-MODES = ("PP",) * 4 + ("HP",) + ("PP",) * 11
+MODES = ("HP", "HP", "PP", "PP") * 4
 LAST_LOAD_SLOT = NPIECE - AHEAD - 1
 WU, WA, WB, WE0, WE1 = 0, 1, 2, 3, 4
 
@@ -171,7 +171,7 @@ def tile_ferminetoneelectronlayer_pa_t_kernel(tc, in_1e, in_2e, W_unmixed, b_unm
         def long_first(k, half):
             eng = nc.gpsimd if MODES[k][half] == "H" else nc.vector
             l4 = pieces[k][:, 8 * half:8 * half + 8, :].rearrange("p (a f) d -> p a f d", a=2)
-            t1 = grp.tile([P, 2, 2, D2], F32, name="lt1_%d_%d" % (k, half), tag="t1")
+            t1 = grp.tile([P, 2, 2, D2], F32, name="lt1_%d_%d" % (k, half), tag="lt1")
             for sj in range(2):
                 eng.tensor_tensor(out=t1[:, sj, :, :], in0=l4[:, sj, 0:2, :], in1=l4[:, sj, 2:4, :], op=ADD)
             a2 = grp.tile([P, 2, D2], BF16, name="a2_%d_%d" % (k, half), tag="a2")

@@ -7,366 +7,327 @@ U32 = mybir.dt.uint32
 U8 = mybir.dt.uint8
 FP8X4 = mybir.dt.float8_e4m3fn_x4
 ADD = mybir.AluOpType.add
-ACT = mybir.ActivationFunctionType
+TANH = mybir.ActivationFunctionType.Tanh
 
 P = 128
-B, N, D1, D2, NS = 512, 8, 512, 256, 2
+B, N, D1, D2 = 512, 8, 512, 256
 ND = D1
-NBLK = B // P
+PANELS = B // P
 PIECES = 4
-NPIECE = NBLK * PIECES
-NPAIR = NBLK * 4
+N_PIECES = PANELS * PIECES
+PAIRS = 4
+N_PAIRS = PANELS * PAIRS
+UNIT_ROWS = 8
+ROWS_PER_DMA = 4
 AHEAD = 3
-MODES = ("HP", "HP", "PP", "PP") * 4
-LAST_LOAD_SLOT = NPIECE - AHEAD - 1
-WU, WA, WB, WE0, WE1 = 0, 1, 2, 3, 4
+LAG = 5
+ADDED_UNIT = (4, 0)
+W_U, W_OWN, W_OTHER, W_E0, W_E1 = range(5)
 
-FLOPS = 2 * (B * N * D1 * ND + B * NS * NS * D1 * ND + B * N * NS * D2 * ND)
-
-
-def sum_slot(pair):
-    return PIECES * (pair // 4) + 5 + (0, 1, 1, 2)[pair % 4]
-
-
-def pairs_at(s):
-    return [pair for pair in range(NPAIR) if sum_slot(pair) == s]
+FLOPS = 2 * (B * N * D1 * ND + B * 2 * 2 * D1 * ND + B * N * 2 * D2 * ND)
 
 
 def tile_ferminetoneelectronlayer_pa_t_kernel(tc, in_1e, in_2e, W_unmixed, b_unmixed, W_mixed, W_2e, out):
     nc = tc.nc
-    rows2 = in_2e.rearrange("b i j d -> (b i j) d")
-    toks2 = in_2e.rearrange("b i j d -> (b i) j d")
+    rows_2e = in_2e.rearrange("b i j d -> (b i j) d")
+    tokens_2e = in_2e.rearrange("b i j d -> (b i) j d")
 
     with tc.manual_schedule(), \
          tc.tile_pool(name="const", bufs=1) as const, \
-         tc.tile_pool(name="xpool", bufs=4) as xpool, \
+         tc.tile_pool(name="xpool", bufs=PANELS) as xpool, \
          tc.tile_pool(name="stage", bufs=AHEAD) as stage, \
-         tc.tile_pool(name="grp", bufs=2) as grp, \
-         tc.tile_pool(name="codes", bufs=2) as codes, \
-         tc.tile_pool(name="keep", bufs=4) as keep, \
-         tc.psum_pool(name="ps", bufs=2) as ps, \
+         tc.tile_pool(name="two", bufs=2) as two, \
+         tc.tile_pool(name="keep", bufs=PANELS) as keep, \
+         tc.psum_pool(name="ps2", bufs=2) as ps2, \
          tc.psum_pool(name="ps4", bufs=4) as ps4:
 
-        xs = {}
-        pieces = {}
-        g1s = {}
-        g2s = {}
-        t1s = {}
-        gms = {}
-        a2s = {}
-        lts = {}
-        accs_of = {}
-        gps_of = {}
-        xq = {}
-        mq = {}
-        eq = {}
-        gbs = {}
-        os_ = {}
-        quads = {}
-        state = {"ready": []}
-        outp_box = []
-        wgrp_box = []
-        wgs = {}
+        x_of, piece_of, x_grouped, e_grouped, halfsums, m_grouped = {}, {}, {}, {}, {}, {}
+        x_mx, m_mx, e_mx, g_psum, g_bias, acc_of, out_of = {}, {}, {}, {}, {}, {}, {}
+        added = {}
+        pools = {}
 
-        def load_x(bb):
-            x = xpool.tile([P, N, D1], BF16, name="x%d" % bb, tag="x")
-            nc.sync.dma_start(out=x[:], in_=in_1e[bb * P:(bb + 1) * P, :, :])
-            xs[bb] = x
+        def load_x(panel):
+            x = xpool.tile([P, N, D1], BF16, name="x%d" % panel, tag="x")
+            nc.sync.dma_start(out=x[:], in_=in_1e[panel * P:(panel + 1) * P, :, :])
+            x_of[panel] = x
 
-        def load_piece(k):
-            pc = stage.tile([P, 16, D2], BF16, name="pc%d" % k, tag="pc")
-            if MODES[k] == "PP":
-                r0 = k * 16 * P
-                nc.sync.dma_start(out=pc[:], in_=rows2[r0:r0 + 16 * P, :].rearrange("(r p) d -> p r d", p=P))
-            else:
-                for half in range(2):
-                    dst = pc[:, 8 * half:8 * half + 8, :]
-                    if MODES[k][half] == "P":
-                        r0 = (k * 16 + 8 * half) * P
-                        nc.sync.dma_start(out=dst, in_=rows2[r0:r0 + 8 * P, :].rearrange("(r p) d -> p r d", p=P))
-                    else:
-                        t0 = (k * 32 + 16 * half) * N
-                        nc.sync.dma_start(out=dst, in_=toks2[t0:t0 + P, :, :])
-            pieces[k] = pc
+        def load_piece(piece):
+            staged = stage.tile([P, 2 * UNIT_ROWS, D2], BF16, name="piece%d" % piece, tag="piece")
+            for unit in range(2):
+                if (piece, unit) == ADDED_UNIT:
+                    first = (2 * piece + unit) * P
+                    nc.sync.dma_start(out=staged[:, unit * UNIT_ROWS:(unit + 1) * UNIT_ROWS, :],
+                                      in_=tokens_2e[first:first + P, :, :])
+                else:
+                    for r in range(unit * UNIT_ROWS, (unit + 1) * UNIT_ROWS, ROWS_PER_DMA):
+                        first = (2 * UNIT_ROWS * piece + r) * P
+                        nc.sync.dma_start(
+                            out=staged[:, r:r + ROWS_PER_DMA, :],
+                            in_=rows_2e[first:first + ROWS_PER_DMA * P, :].rearrange("(r p) d -> p r d", p=P))
+            piece_of[piece] = staged
 
-        def tx(bb):
-            xf = xs[bb][:].bitcast(F32)
-            g1s[bb] = grp.tile([P, N, P, 4], BF16, name="g1_%d" % bb, tag="g1", align_bytes=64)
-            g1f = g1s[bb][:].rearrange("p i b t -> p i (b t)").bitcast(F32).rearrange("p i (b u) -> p i b u", u=2)
-            for qs in ((0, 1), (2, 3)):
-                xts = []
-                for q in qs:
-                    xt = ps4.tile([P, 2, 2, P], F32, name="xt%d_%d" % (bb, q), tag="acc")
-                    for i2 in range(2):
+        def quantise(pool, name, grouped, width):
+            words = pool.tile([P, width], U32, name=name + "_words", tag=name[0] + "_words", align_bytes=64)
+            scales = pool.tile([P, width], U8, name=name + "_scales", tag=name[0] + "_scales", align_bytes=64)
+            nc.vector.quantize_mx(out=words[:].bitcast(FP8X4), scales=scales[:], in_=grouped)
+            return words, scales
+
+        def mx_pass(acc, operand, columns, weight, start, stop):
+            words, scales = operand
+            nc.tensor.matmul_mx(out=acc[:], lhsT=words[:, columns].bitcast(FP8X4), lhsT_scale=scales[:, columns],
+                                rhs=w_words[:, weight, :].bitcast(FP8X4), rhs_scale=w_scales[:, weight, :],
+                                start=start, stop=stop)
+
+        def transpose_and_add(dst, parts):
+            for n, part in enumerate(parts):
+                nc.tensor.matmul(out=dst, lhsT=part, rhs=ident[:], is_transpose=True,
+                                 start=(n == 0), stop=(n == len(parts) - 1))
+
+        def transpose_x(panel):
+            words = x_of[panel][:].bitcast(F32)
+            grouped = pools["early"].tile([P, N, P, 4], BF16, name="xg%d" % panel, tag="xg", align_bytes=64)
+            grouped_words = (grouped[:].rearrange("p i b t -> p i (b t)").bitcast(F32)
+                             .rearrange("p i (b u) -> p i b u", u=2))
+            for first in (0, 4):
+                banks = []
+                for i0 in (first, first + 2):
+                    bank = ps4.tile([P, 2, 2, P], F32, name="xt%d_%d" % (panel, i0), tag="acc")
+                    for i in range(2):
                         for u in range(2):
-                            nc.tensor.transpose(xt[:, i2, u, :], xf[:, 2 * q + i2, u * P:(u + 1) * P], ident_f[:])
-                    xts.append(xt)
-                for q, xt in zip(qs, xts):
-                    nc.scalar.copy(out=g1f[:, 2 * q:2 * q + 2, :, :], in_=xt[:].rearrange("p i u b -> p i b u"))
+                            nc.tensor.transpose(bank[:, i, u, :], words[:, i0 + i, u * P:(u + 1) * P], ident[:])
+                    banks.append(bank)
+                for i0, bank in zip((first, first + 2), banks):
+                    nc.scalar.copy(out=grouped_words[:, i0:i0 + 2, :, :], in_=bank[:].rearrange("p i u b -> p i b u"))
+            x_grouped[panel] = grouped
 
-        def mean_add(bb):
-            x = xs[bb]
-            for s in range(2):
-                t1 = grp.tile([P, 2, D1], F32, name="t1_%d_%d" % (bb, s), tag="t1")
-                nc.vector.tensor_tensor(out=t1[:], in0=x[:, 4 * s:4 * s + 2, :], in1=x[:, 4 * s + 2:4 * s + 4, :], op=ADD)
-                t1s[(bb, s)] = t1
+        def add_electrons(panel):
+            x = x_of[panel]
+            for spin in range(2):
+                e0 = 4 * spin
+                halfsum = pools["early"].tile([P, 2, D1], F32, name="hs%d_%d" % (panel, spin), tag="hs")
+                nc.vector.tensor_tensor(out=halfsum[:], in0=x[:, e0:e0 + 2, :], in1=x[:, e0 + 2:e0 + 4, :], op=ADD)
+                halfsums[(panel, spin)] = halfsum
 
-        def tm(bb):
-            gm = grp.tile([P, 2, P, 4], BF16, name="gm%d" % bb, tag="gm", align_bytes=64)
-            mts = []
-            for s in range(2):
-                mt = ps.tile([P, 4, P], F32, name="mt%d_%d" % (bb, s), tag="aux")
+        def transpose_means(panel):
+            grouped = pools["early"].tile([P, 2, P, 4], BF16, name="mg%d" % panel, tag="mg", align_bytes=64)
+            banks = []
+            for spin in range(2):
+                bank = ps2.tile([P, 4, P], F32, name="mt%d_%d" % (panel, spin), tag="aux")
                 for t in range(4):
-                    for a in range(2):
-                        nc.tensor.matmul(out=mt[:, t, :], lhsT=t1s[(bb, s)][:, a, t * P:(t + 1) * P], rhs=ident_f[:],
-                                         is_transpose=True, start=(a == 0), stop=(a == 1))
-                mts.append(mt)
-            for s in range(2):
-                nc.scalar.mul(out=gm[:, s, :, :], in_=mts[s][:].rearrange("p t b -> p b t"), mul=0.25)
-            gms[bb] = gm
+                    transpose_and_add(bank[:, t, :],
+                                      [halfsums[(panel, spin)][:, n, t * P:(t + 1) * P] for n in range(2)])
+                banks.append(bank)
+            for spin in range(2):
+                nc.scalar.mul(out=grouped[:, spin, :, :], in_=banks[spin][:].rearrange("p t b -> p b t"), mul=0.25)
+            m_grouped[panel] = grouped
 
-        def quant_x(bb):
-            xc = keep.tile([P, N * P], U32, name="xc%d" % bb, tag="xc", align_bytes=64)
-            xsc = keep.tile([P, N * P], U8, name="xsc%d" % bb, tag="xsc", align_bytes=64)
-            nc.vector.quantize_mx(out=xc[:].bitcast(FP8X4), scales=xsc[:], in_=g1s[bb][:].rearrange("p i b t -> p (i b t)"))
-            xq[bb] = (xc, xsc)
+        def quantise_x(panel):
+            x_mx[panel] = quantise(keep, "x%d" % panel, x_grouped[panel][:].rearrange("p i b t -> p (i b t)"), N * P)
 
-        def quant_m(bb):
-            mc = keep.tile([P, 2 * P], U32, name="mc%d" % bb, tag="mc", align_bytes=64)
-            msc = keep.tile([P, 2 * P], U8, name="msc%d" % bb, tag="msc", align_bytes=64)
-            nc.vector.quantize_mx(out=mc[:].bitcast(FP8X4), scales=msc[:], in_=gms[bb][:].rearrange("p s b t -> p (s b t)"))
-            mq[bb] = (mc, msc)
+        def quantise_means(panel):
+            m_mx[panel] = quantise(keep, "m%d" % panel, m_grouped[panel][:].rearrange("p s b t -> p (s b t)"), 2 * P)
 
-        def g_mx(bb):
-            mc, msc = mq[bb]
-            gps = []
-            for s in range(2):
-                gp = ps.tile([P, ND], F32, name="gp%d_%d" % (bb, s), tag="aux")
-                for a, (w, sp) in enumerate(((WA, s), (WB, 1 - s))):
-                    nc.tensor.matmul_mx(out=gp[:], lhsT=mc[:, sp * P:(sp + 1) * P].bitcast(FP8X4),
-                                        lhsT_scale=msc[:, sp * P:(sp + 1) * P],
-                                        rhs=wcodes[:, w, :].bitcast(FP8X4), rhs_scale=wscales[:, w, :],
-                                        start=(a == 0), stop=(a == 1))
-                gps.append(gp)
-            return gps
+        def multiply_means(panel):
+            g_psum[panel] = []
+            for spin in range(2):
+                acc = ps2.tile([P, ND], F32, name="g%d_%d" % (panel, spin), tag="aux")
+                mx_pass(acc, m_mx[panel], slice(spin * P, (spin + 1) * P), W_OWN, True, False)
+                mx_pass(acc, m_mx[panel], slice((1 - spin) * P, (2 - spin) * P), W_OTHER, False, True)
+                g_psum[panel].append(acc)
 
-        def g_add(bb, gps):
-            gb = grp.tile([P, 2, ND], F32, name="gb%d" % bb, tag="gb")
-            for s in range(2):
-                nc.vector.tensor_tensor(out=gb[:, s, :], in0=gps[s][:], in1=bias_bc[:], op=ADD)
-            gbs[bb] = gb
+        def add_bias(panel):
+            g_bias[panel] = two.tile([P, 2, ND], F32, name="gb%d" % panel, tag="gb")
+            for spin in range(2):
+                nc.vector.tensor_tensor(out=g_bias[panel][:, spin, :], in0=g_psum[panel][spin][:], in1=bias[:], op=ADD)
 
-        def pool_half(k, half):
-            bb, kp = divmod(k, PIECES)
-            pc = pieces[k]
-            pp = ps.tile([P, N, 64], F32, name="pp%d_%d" % (k, half), tag="pp")
-            ppv = pp[:].rearrange("p i (r q c) -> p i r q c", r=8, q=4, c=2)
-            for r in range(8):
+        def pool_unit(piece, unit):
+            panel, place = divmod(2 * piece + unit, 2 * PIECES)
+            staged = piece_of[piece]
+            bank = ps2.tile([P, N, 64], F32, name="pool%d_%d" % (piece, unit), tag="pool")
+            columns = bank[:].rearrange("p i (r a c) -> p i r a c", r=UNIT_ROWS, a=4, c=2)
+            for r in range(UNIT_ROWS):
                 for c in range(2):
-                    nc.tensor.matmul(out=ppv[:, :, r, :, c], lhsT=pc[:, 8 * half + r, c * P:(c + 1) * P],
-                                     rhs=pool_rhs, start=True, stop=True)
-            kk = 2 * kp + half
-            nc.scalar.copy(out=g2s[bb][:, :, 64 * kk:64 * (kk + 1)], in_=pp[:])
+                    nc.tensor.matmul(out=columns[:, :, r, :, c],
+                                     lhsT=staged[:, unit * UNIT_ROWS + r, c * P:(c + 1) * P],
+                                     rhs=pool_matrix, start=True, stop=True)
+            nc.scalar.copy(out=e_grouped[panel][:, :, 64 * place:64 * (place + 1)], in_=bank[:])
 
-        def long_first(k, half):
-            eng = nc.gpsimd if MODES[k][half] == "H" else nc.vector
-            l4 = pieces[k][:, 8 * half:8 * half + 8, :].rearrange("p (a f) d -> p a f d", a=2)
-            t1 = grp.tile([P, 2, 2, D2], F32, name="lt1_%d_%d" % (k, half), tag="lt1")
-            for sj in range(2):
-                eng.tensor_tensor(out=t1[:, sj, :, :], in0=l4[:, sj, 0:2, :], in1=l4[:, sj, 2:4, :], op=ADD)
-            a2 = grp.tile([P, 2, D2], BF16, name="a2_%d_%d" % (k, half), tag="a2")
-            eng.tensor_tensor(out=a2[:], in0=t1[:, :, 0, :], in1=t1[:, :, 1, :], op=ADD)
-            a2s[(k, half)] = a2
+        def add_rows(piece, unit):
+            rows = piece_of[piece][:, unit * UNIT_ROWS:(unit + 1) * UNIT_ROWS, :].rearrange("p (a f) d -> p a f d", a=2)
+            halfsum = two.tile([P, 2, 2, D2], F32, name="added_hs", tag="added_hs")
+            nc.vector.tensor_tensor(out=halfsum[:], in0=rows[:, :, 0:2, :], in1=rows[:, :, 2:4, :], op=ADD)
+            added["halfsum"] = halfsum
 
-        def long_t(k, half):
-            a2 = a2s[(k, half)]
-            lt = ps.tile([P, 4, P], BF16, name="lt%d_%d" % (k, half), tag="aux")
+        def transpose_added():
+            bank = ps2.tile([P, 4, P], F32, name="added_t", tag="aux")
             for sj in range(2):
                 for c in range(2):
-                    nc.tensor.transpose(lt[:, 2 * sj + c, :], a2[:, sj, c * P:(c + 1) * P], ident_b[:])
-            lts[(k, half)] = lt
+                    transpose_and_add(bank[:, 2 * sj + c, :],
+                                      [added["halfsum"][:, sj, n, c * P:(c + 1) * P] for n in range(2)])
+            added["bank"] = bank
 
-        def long_evac(k, half):
-            bb, kp = divmod(k, PIECES)
-            kk = 2 * kp + half
-            g2v = g2s[bb][:].rearrange("p i (b t) -> p i b t", t=4)[:, :, 16 * kk:16 * (kk + 1), :]
-            nc.scalar.mul(out=g2v, in_=lts[(k, half)][:].rearrange("p t (b i) -> p i b t", i=N), mul=0.25)
+        def copy_added(piece, unit):
+            panel, place = divmod(2 * piece + unit, 2 * PIECES)
+            walkers = e_grouped[panel][:].rearrange("p i (b t) -> p i b t", t=4)[:, :, 16 * place:16 * (place + 1), :]
+            nc.scalar.mul(out=walkers, in_=added["bank"][:].rearrange("p t (b i) -> p i b t", i=N), mul=0.25)
 
-        def quantise_e(bb):
-            ec = codes.tile([P, N * P], U32, name="ec%d" % bb, tag="ec", align_bytes=64)
-            esc = codes.tile([P, N * P], U8, name="esc%d" % bb, tag="esc", align_bytes=64)
-            nc.vector.quantize_mx(out=ec[:].bitcast(FP8X4), scales=esc[:], in_=g2s[bb][:].rearrange("p i c -> p (i c)"))
-            eq[bb] = (ec, esc)
+        def quantise_e(panel):
+            e_mx[panel] = quantise(two, "e%d" % panel, e_grouped[panel][:].rearrange("p i c -> p (i c)"), N * P)
 
-        def c_mx(pair):
-            bb, q = divmod(pair, 4)
-            xc, xsc = xq[bb]
-            ec, esc = eq[bb]
-            we = WE0 if q < 2 else WE1
-            accs = []
-            for i2 in range(2):
-                i = 2 * q + i2
-                cols = slice(i * P, (i + 1) * P)
-                acc = ps4.tile([P, ND], F32, name="acc%d_%d" % (bb, i), tag="acc")
-                nc.tensor.matmul_mx(out=acc[:], lhsT=xc[:, cols].bitcast(FP8X4), lhsT_scale=xsc[:, cols],
-                                    rhs=wcodes[:, WU, :].bitcast(FP8X4), rhs_scale=wscales[:, WU, :],
-                                    start=True, stop=False)
-                nc.tensor.matmul_mx(out=acc[:], lhsT=ec[:, cols].bitcast(FP8X4), lhsT_scale=esc[:, cols],
-                                    rhs=wcodes[:, we, :].bitcast(FP8X4), rhs_scale=wscales[:, we, :],
-                                    start=False, stop=True)
-                accs.append(acc)
-            accs_of[pair] = accs
+        def multiply_pair(pair):
+            panel, q = divmod(pair, PAIRS)
+            acc_of[pair] = []
+            for i in (2 * q, 2 * q + 1):
+                acc = ps4.tile([P, ND], F32, name="acc%d_%d" % (panel, i), tag="acc")
+                mx_pass(acc, x_mx[panel], slice(i * P, (i + 1) * P), W_U, True, False)
+                mx_pass(acc, e_mx[panel], slice(i * P, (i + 1) * P), W_E0 if i < 4 else W_E1, False, True)
+                acc_of[pair].append(acc)
 
-        def c_sum(pair):
-            bb, q = divmod(pair, 4)
-            if bb < NBLK - 1:
-                if q % 2 == 0:
-                    quads[(bb, q // 2)] = outp_box[0].tile([P, 4, ND], F32, name="oq%d_%d" % (bb, q // 2), tag="oq", bufs=6)
-                o = quads[(bb, q // 2)][:, 2 * (q % 2):2 * (q % 2) + 2, :]
-            else:
-                ot = outp_box[0].tile([P, 2, ND], F32, name="o%d" % pair, tag="o", bufs=4)
-                o = ot[:]
-            for i2 in range(2):
-                nc.vector.tensor_tensor(out=o[:, i2, :], in0=accs_of[pair][i2][:], in1=gbs[bb][:, q // 2, :], op=ADD)
-            os_[pair] = o
+        def sum_pair(pair):
+            panel, q = divmod(pair, PAIRS)
+            result = pools["out"].tile([P, 2, ND], F32, name="o%d" % pair, tag="o")
+            for n in range(2):
+                nc.vector.tensor_tensor(out=result[:, n, :], in0=acc_of[pair][n][:], in1=g_bias[panel][:, q // 2, :],
+                                        op=ADD)
+            out_of[pair] = result
 
-        def c_tanh(pair):
-            nc.scalar.activation(out=os_[pair], in_=os_[pair], func=ACT.Tanh)
+        def tanh_pair(pair):
+            nc.scalar.activation(out=out_of[pair][:], in_=out_of[pair][:], func=TANH)
 
-        def c_skip(pair):
-            bb, q = divmod(pair, 4)
-            nc.vector.tensor_tensor(out=os_[pair], in0=os_[pair], in1=xs[bb][:, 2 * q:2 * q + 2, :], op=ADD)
-            if bb == NBLK - 1:
-                state["ready"].append((out[bb * P:(bb + 1) * P, 2 * q:2 * q + 2, :], os_[pair]))
-            elif q % 2 == 1:
-                state["ready"].append((out[bb * P:(bb + 1) * P, 2 * q - 2:2 * q + 2, :], quads[(bb, q // 2)][:]))
+        def skip_pair(pair):
+            panel, q = divmod(pair, PAIRS)
+            nc.vector.tensor_tensor(out=out_of[pair][:], in0=out_of[pair][:], in1=x_of[panel][:, 2 * q:2 * q + 2, :],
+                                    op=ADD)
 
-        def regroup(w, parts):
-            wg = wgrp_box[0].tile([P, ND, 4], BF16, name="wg%d" % w, tag="wg", align_bytes=64)
-            wgv = wg[:].rearrange("p (c i) t -> p c t i", i=4)
-            for t0, src in parts:
-                nt = src.shape[1]
-                nc.vector.tensor_copy(out=wgv[:, :, t0:t0 + nt, :], in_=src.rearrange("p t (c i) -> p c t i", i=4))
-            wgs[w] = wg
+        def store_pair(pair):
+            panel, q = divmod(pair, PAIRS)
+            nc.sync.dma_start(out=out[panel * P:(panel + 1) * P, 2 * q:2 * q + 2, :], in_=out_of[pair][:])
 
-        def quant_w(w):
-            nc.vector.quantize_mx(out=wcodes[:, w, :].bitcast(FP8X4), scales=wscales[:, w, :],
-                                  in_=wgs[w][:].rearrange("p n t -> p (n t)"))
+        def group_weight(name, parts):
+            grouped = pools["w_grouped"].tile([P, ND, 4], BF16, name="wg_" + name, tag="wg", align_bytes=64)
+            view = grouped[:].rearrange("p (c i) t -> p c t i", i=4)
+            for t0, rows in parts:
+                nc.vector.tensor_copy(out=view[:, :, t0:t0 + rows.shape[1], :],
+                                      in_=rows.rearrange("p t (c i) -> p c t i", i=4))
+            return grouped
 
-        def prep_w_mixed():
-            regroup(WA, ((0, raw_m[:, 0:4, :]),))
-            regroup(WB, ((0, raw_m[:, 4:8, :]),))
-            quant_w(WA)
-            quant_w(WB)
+        def quantise_weight(weight, grouped):
+            nc.vector.quantize_mx(out=w_words[:, weight, :].bitcast(FP8X4), scales=w_scales[:, weight, :],
+                                  in_=grouped[:].rearrange("p n t -> p (n t)"))
 
-        def prep_w_rest():
-            regroup(WU, ((0, raw_u[:]),))
-            regroup(WE0, ((0, raw_e[:]),))
-            quant_w(WU)
-            regroup(WE1, ((0, raw_e[:, 2:4, :]), (2, raw_e[:, 0:2, :])))
-            quant_w(WE0)
-            quant_w(WE1)
+        def prepare_w_mixed():
+            own = group_weight("own", ((0, raw_mixed[:, 0:4, :]),))
+            other = group_weight("other", ((0, raw_mixed[:, 4:8, :]),))
+            quantise_weight(W_OWN, own)
+            quantise_weight(W_OTHER, other)
 
-        extra = {1: (lambda: tx(3), lambda: tm(2), lambda: mean_add(3)),
-                 2: (lambda: tm(3), prep_w_rest),
-                 4: (lambda: quant_x(2), lambda: quant_m(2)),
-                 5: (lambda: quant_x(3), lambda: quant_m(3))}
+        def prepare_w_unmixed_and_2e():
+            u = group_weight("u", ((0, raw_unmixed[:]),))
+            e0 = group_weight("e0", ((0, raw_2e[:]),))
+            quantise_weight(W_U, u)
+            e1 = group_weight("e1", ((0, raw_2e[:, 2:4, :]), (2, raw_2e[:, 0:2, :])))
+            quantise_weight(W_E0, e0)
+            quantise_weight(W_E1, e1)
 
-        def long_halves(k):
-            if 0 <= k < NPIECE:
-                return [half for half in range(2) if MODES[k][half] != "P"]
-            return []
+        def slot(n):
+            pair = n - LAG
+            panel, place = divmod(n, PIECES)
+            pooling = n < N_PIECES
+            if pooling and place == 0:
+                e_grouped[panel] = two.tile([P, N, 4 * P], BF16, name="eg%d" % panel, tag="eg", align_bytes=64)
+            if 0 <= pair < N_PAIRS:
+                sum_pair(pair)
+            if 0 <= pair - 1 < N_PAIRS:
+                skip_pair(pair - 1)
+            if place == 0 and 0 < panel < PANELS:
+                add_bias(panel)
+            if n - 2 == ADDED_UNIT[0]:
+                copy_added(*ADDED_UNIT)
+            if pooling:
+                for unit in range(2):
+                    if (n, unit) == ADDED_UNIT:
+                        add_rows(n, unit)
+                    else:
+                        pool_unit(n, unit)
+            if 0 <= pair < N_PAIRS:
+                tanh_pair(pair)
+            if pooling and place == PIECES - 1:
+                quantise_e(panel)
+            if n - 1 == ADDED_UNIT[0]:
+                transpose_added()
+            if 0 <= pair + 1 < N_PAIRS:
+                multiply_pair(pair + 1)
+            if place == PIECES - 1 and panel + 1 < PANELS:
+                multiply_means(panel + 1)
+            if n + AHEAD < N_PIECES:
+                load_piece(n + AHEAD)
+            elif n + AHEAD == N_PIECES:
+                for done in range(0, pair):
+                    store_pair(done)
+            elif pair - 1 < N_PAIRS:
+                store_pair(pair - 1)
 
-        def slot(s):
-            in_pieces = 0 <= s < NPIECE
-            bb, kp = divmod(s, PIECES)
-            if in_pieces and kp == 0:
-                g2s[bb] = grp.tile([P, N, 4 * P], BF16, name="g2_%d" % bb, tag="g2", align_bytes=64)
-            for pair in pairs_at(s):
-                c_sum(pair)
-            for pair in pairs_at(s - 1):
-                c_skip(pair)
-            if kp == 0 and 0 < bb < NBLK:
-                g_add(bb, gps_of[bb])
-            for f in extra.get(s, ()):
-                f()
-            for half in long_halves(s - 2):
-                long_evac(s - 2, half)
-            if in_pieces:
-                for half in range(2):
-                    if MODES[s][half] != "P":
-                        long_first(s, half)
-                for half in range(2):
-                    if MODES[s][half] == "P":
-                        pool_half(s, half)
-            for pair in pairs_at(s):
-                c_tanh(pair)
-            if in_pieces and kp == PIECES - 1:
-                quantise_e(bb)
-            for half in long_halves(s - 1):
-                long_t(s - 1, half)
-            for pair in pairs_at(s + 1):
-                c_mx(pair)
-            if kp == PIECES - 1 and 0 < bb + 1 < NBLK:
-                gps_of[bb + 1] = g_mx(bb + 1)
-            if s + AHEAD < NPIECE:
-                load_piece(s + AHEAD)
-            if s > LAST_LOAD_SLOT:
-                for dst, src in state["ready"]:
-                    nc.sync.dma_start(out=dst, in_=src)
-                state["ready"] = []
+        bias = const.tile([P, ND], BF16)
+        nc.scalar.dma_start(out=bias[:], in_=b_unmixed.partition_broadcast(P))
+        w_words = const.tile([P, 5, ND], U32, align_bytes=64)
+        w_scales = const.tile([P, 5, ND], U8, align_bytes=64)
+        ident = const.tile([P, P], F32)
+        group_of_row = const.tile([P, 2, N, 2], F32)
+        pool_tile = const.tile([P, N, 2, 2], BF16)
+        pool_matrix = pool_tile[:].rearrange("p i a j -> p i (a j)")
 
-        bias_bc = const.tile([P, ND], BF16)
-        nc.scalar.dma_start(out=bias_bc[:], in_=b_unmixed.partition_broadcast(P))
-        wcodes = const.tile([P, 5, ND], U32, align_bytes=64)
-        wscales = const.tile([P, 5, ND], U8, align_bytes=64)
-        ident_f = const.tile([P, P], F32)
-        ident_b = const.tile([P, P], BF16)
-        red = const.tile([P, 2, 8, 2], F32)
-        poolm = const.tile([P, 8, 2, 2], BF16)
-        pool_rhs = poolm[:].rearrange("p i a j -> p i (a j)")
-
-        with tc.tile_pool(name="wraw", bufs=1) as wraw, tc.tile_pool(name="wgrp", bufs=2) as wgrp_pool:
-            wgrp_box.append(wgrp_pool)
+        with tc.tile_pool(name="w_raw", bufs=1) as w_raw, tc.tile_pool(name="w_grouped", bufs=2) as w_grouped, \
+             tc.tile_pool(name="early", bufs=2) as early:
+            pools["w_grouped"] = w_grouped
+            pools["early"] = early
             load_x(0)
             load_x(1)
-            raw_m = wraw.tile([P, 8, ND], BF16)
-            nc.sync.dma_start(out=raw_m[:], in_=W_mixed.rearrange("(t p) n -> p t n", p=P))
+            raw_mixed = w_raw.tile([P, 8, ND], BF16)
+            nc.sync.dma_start(out=raw_mixed[:], in_=W_mixed.rearrange("(t p) n -> p t n", p=P))
             load_x(2)
-            raw_u = wraw.tile([P, 4, ND], BF16)
-            nc.sync.dma_start(out=raw_u[:].rearrange("p (u e) n -> p u e n", e=2),
+            raw_unmixed = w_raw.tile([P, 4, ND], BF16)
+            nc.sync.dma_start(out=raw_unmixed[:].rearrange("p (u e) n -> p u e n", e=2),
                               in_=W_unmixed.rearrange("(u p e) n -> p u e n", u=2, e=2))
-            raw_e = wraw.tile([P, 4, ND], BF16)
-            nc.sync.dma_start(out=raw_e[:], in_=W_2e.rearrange("(t p) n -> p t n", p=P))
+            raw_2e = w_raw.tile([P, 4, ND], BF16)
+            nc.sync.dma_start(out=raw_2e[:], in_=W_2e.rearrange("(t p) n -> p t n", p=P))
             load_x(3)
-            for k in range(AHEAD):
-                load_piece(k)
+            for piece in range(AHEAD):
+                load_piece(piece)
 
-            make_identity(nc, ident_f[:])
-            make_identity(nc, ident_b[:])
-            nc.vector.tensor_reduce(out=red[:].rearrange("p a i j -> p (a i j)"),
-                                    in_=ident_f[:].rearrange("p (g f) -> p g f", f=4),
+            make_identity(nc, ident[:])
+            nc.vector.tensor_reduce(out=group_of_row[:].rearrange("p a i j -> p (a i j)"),
+                                    in_=ident[:].rearrange("p (g f) -> p g f", f=4),
                                     axis=mybir.AxisListType.X, op=ADD)
-            nc.vector.tensor_scalar_mul(out=poolm[:], in0=red[:].rearrange("p a i j -> p i a j"), scalar1=0.25)
+            nc.vector.tensor_scalar_mul(out=pool_tile[:], in0=group_of_row[:].rearrange("p a i j -> p i a j"), scalar1=0.25)
 
-            tx(0)
-            mean_add(0)
-            tx(1)
-            tm(0)
-            mean_add(1)
-            tm(1)
-            prep_w_mixed()
-            quant_x(0)
-            quant_m(0)
-            quant_x(1)
-            quant_m(1)
-            g_add(0, g_mx(0))
-            tx(2)
-            mean_add(2)
-            for s in range(3):
-                slot(s)
+            transpose_x(0)
+            add_electrons(0)
+            transpose_x(1)
+            transpose_means(0)
+            add_electrons(1)
+            transpose_means(1)
+            prepare_w_mixed()
+            for panel in range(2):
+                quantise_x(panel)
+                quantise_means(panel)
+            multiply_means(0)
+            add_bias(0)
+            transpose_x(2)
+            add_electrons(2)
+            slot(0)
+            transpose_x(3)
+            transpose_means(2)
+            add_electrons(3)
+            slot(1)
+            transpose_means(3)
+            prepare_w_unmixed_and_2e()
+            slot(2)
+            for panel in range(2, 4):
+                quantise_x(panel)
+                quantise_means(panel)
+            slot(3)
 
-        with tc.tile_pool(name="outp", bufs=1) as outp:
-            outp_box.append(outp)
-            for s in range(3, sum_slot(NPAIR - 1) + 2):
-                slot(s)
+        with tc.tile_pool(name="results", bufs=N_PAIRS) as results:
+            pools["out"] = results
+            for n in range(4, N_PAIRS + LAG + 1):
+                slot(n)

@@ -18,10 +18,9 @@ N_PIECES = PANELS * PIECES
 PAIRS = 4
 N_PAIRS = PANELS * PAIRS
 UNIT_ROWS = 8
-ROWS_PER_DMA = 4
 AHEAD = 3
 LAG = 5
-ADDED_UNIT = (4, 0)
+ADDED_PIECE = 4
 W_U, W_OWN, W_OTHER, W_E0, W_E1 = range(5)
 
 FLOPS = 2 * (B * N * D1 * ND + B * 2 * 2 * D1 * ND + B * N * 2 * D2 * ND)
@@ -43,7 +42,7 @@ def tile_ferminetoneelectronlayer_pa_t_kernel(tc, in_1e, in_2e, W_unmixed, b_unm
 
         x_of, piece_of, x_grouped, e_grouped, halfsums, m_grouped = {}, {}, {}, {}, {}, {}
         x_mx, m_mx, e_mx, g_psum, g_bias, acc_of, out_of = {}, {}, {}, {}, {}, {}, {}
-        added = {}
+        added_halfsum, added_bank = {}, {}
         pools = {}
 
         def load_x(panel):
@@ -53,17 +52,15 @@ def tile_ferminetoneelectronlayer_pa_t_kernel(tc, in_1e, in_2e, W_unmixed, b_unm
 
         def load_piece(piece):
             staged = stage.tile([P, 2 * UNIT_ROWS, D2], BF16, name="piece%d" % piece, tag="piece")
-            for unit in range(2):
-                if (piece, unit) == ADDED_UNIT:
+            if piece == ADDED_PIECE:
+                for unit in range(2):
                     first = (2 * piece + unit) * P
                     nc.sync.dma_start(out=staged[:, unit * UNIT_ROWS:(unit + 1) * UNIT_ROWS, :],
                                       in_=tokens_2e[first:first + P, :, :])
-                else:
-                    for r in range(unit * UNIT_ROWS, (unit + 1) * UNIT_ROWS, ROWS_PER_DMA):
-                        first = (2 * UNIT_ROWS * piece + r) * P
-                        nc.sync.dma_start(
-                            out=staged[:, r:r + ROWS_PER_DMA, :],
-                            in_=rows_2e[first:first + ROWS_PER_DMA * P, :].rearrange("(r p) d -> p r d", p=P))
+            else:
+                first = 2 * UNIT_ROWS * piece * P
+                nc.sync.dma_start(out=staged[:],
+                                  in_=rows_2e[first:first + 2 * UNIT_ROWS * P, :].rearrange("(r p) d -> p r d", p=P))
             piece_of[piece] = staged
 
         def quantise(pool, name, grouped, width):
@@ -152,24 +149,25 @@ def tile_ferminetoneelectronlayer_pa_t_kernel(tc, in_1e, in_2e, W_unmixed, b_unm
                                      rhs=pool_matrix, start=True, stop=True)
             nc.scalar.copy(out=e_grouped[panel][:, :, 64 * place:64 * (place + 1)], in_=bank[:])
 
-        def add_rows(piece, unit):
-            rows = piece_of[piece][:, unit * UNIT_ROWS:(unit + 1) * UNIT_ROWS, :].rearrange("p (a f) d -> p a f d", a=2)
-            halfsum = two.tile([P, 2, 2, D2], F32, name="added_hs", tag="added_hs")
+        def add_rows(unit):
+            rows = (piece_of[ADDED_PIECE][:, unit * UNIT_ROWS:(unit + 1) * UNIT_ROWS, :]
+                    .rearrange("p (a f) d -> p a f d", a=2))
+            halfsum = two.tile([P, 2, 2, D2], F32, name="added_hs%d" % unit, tag="added_hs")
             nc.vector.tensor_tensor(out=halfsum[:], in0=rows[:, :, 0:2, :], in1=rows[:, :, 2:4, :], op=ADD)
-            added["halfsum"] = halfsum
+            added_halfsum[unit] = halfsum
 
-        def transpose_added():
-            bank = ps2.tile([P, 4, P], F32, name="added_t", tag="aux")
+        def transpose_added(unit):
+            bank = ps2.tile([P, 4, P], F32, name="added_t%d" % unit, tag="aux")
             for sj in range(2):
                 for c in range(2):
                     transpose_and_add(bank[:, 2 * sj + c, :],
-                                      [added["halfsum"][:, sj, n, c * P:(c + 1) * P] for n in range(2)])
-            added["bank"] = bank
+                                      [added_halfsum[unit][:, sj, n, c * P:(c + 1) * P] for n in range(2)])
+            added_bank[unit] = bank
 
-        def copy_added(piece, unit):
-            panel, place = divmod(2 * piece + unit, 2 * PIECES)
+        def copy_added(unit):
+            panel, place = divmod(2 * ADDED_PIECE + unit, 2 * PIECES)
             walkers = e_grouped[panel][:].rearrange("p i (b t) -> p i b t", t=4)[:, :, 16 * place:16 * (place + 1), :]
-            nc.scalar.mul(out=walkers, in_=added["bank"][:].rearrange("p t (b i) -> p i b t", i=N), mul=0.25)
+            nc.scalar.mul(out=walkers, in_=added_bank[unit][:].rearrange("p t (b i) -> p i b t", i=N), mul=0.25)
 
         def quantise_e(panel):
             e_mx[panel] = quantise(two, "e%d" % panel, e_grouped[panel][:].rearrange("p i c -> p (i c)"), N * P)
@@ -241,20 +239,21 @@ def tile_ferminetoneelectronlayer_pa_t_kernel(tc, in_1e, in_2e, W_unmixed, b_unm
                 skip_pair(pair - 1)
             if place == 0 and 0 < panel < PANELS:
                 add_bias(panel)
-            if n - 2 == ADDED_UNIT[0]:
-                copy_added(*ADDED_UNIT)
-            if pooling:
+            if n - 2 == ADDED_PIECE:
                 for unit in range(2):
-                    if (n, unit) == ADDED_UNIT:
-                        add_rows(n, unit)
-                    else:
-                        pool_unit(n, unit)
+                    copy_added(unit)
+            for unit in range(2):
+                if n == ADDED_PIECE:
+                    add_rows(unit)
+                elif pooling:
+                    pool_unit(n, unit)
             if 0 <= pair < N_PAIRS:
                 tanh_pair(pair)
             if pooling and place == PIECES - 1:
                 quantise_e(panel)
-            if n - 1 == ADDED_UNIT[0]:
-                transpose_added()
+            if n - 1 == ADDED_PIECE:
+                for unit in range(2):
+                    transpose_added(unit)
             if 0 <= pair + 1 < N_PAIRS:
                 multiply_pair(pair + 1)
             if place == PIECES - 1 and panel + 1 < PANELS:
@@ -267,8 +266,12 @@ def tile_ferminetoneelectronlayer_pa_t_kernel(tc, in_1e, in_2e, W_unmixed, b_unm
             elif pair - 1 < N_PAIRS:
                 store_pair(pair - 1)
 
-        bias = const.tile([P, ND], BF16)
-        nc.scalar.dma_start(out=bias[:], in_=b_unmixed.partition_broadcast(P))
+        bias_row = const.tile([P, ND], BF16)
+        nc.gpsimd.memset(bias_row[:], 0.0)
+        nc.scalar.dma_start(out=bias_row[0:1, :], in_=b_unmixed.unsqueeze(0))
+        ones = const.tile([P, P], BF16)
+        nc.gpsimd.memset(ones[:], 1.0)
+        bias = const.tile([P, ND], F32)
         w_words = const.tile([P, 5, ND], U32, align_bytes=64)
         w_scales = const.tile([P, 5, ND], U8, align_bytes=64)
         ident = const.tile([P, P], F32)
@@ -299,6 +302,9 @@ def tile_ferminetoneelectronlayer_pa_t_kernel(tc, in_1e, in_2e, W_unmixed, b_unm
                                     in_=ident[:].rearrange("p (g f) -> p g f", f=4),
                                     axis=mybir.AxisListType.X, op=ADD)
             nc.vector.tensor_scalar_mul(out=pool_tile[:], in0=group_of_row[:].rearrange("p a i j -> p i a j"), scalar1=0.25)
+            bias_bank = ps2.tile([P, ND], F32, name="bias_bank", tag="aux")
+            nc.tensor.matmul(out=bias_bank[:], lhsT=ones[:], rhs=bias_row[:], start=True, stop=True)
+            nc.scalar.copy(out=bias[:], in_=bias_bank[:])
 
             transpose_x(0)
             add_electrons(0)

@@ -21,7 +21,7 @@ UNIT_ROWS = 8
 AHEAD = 3
 LAG = 5
 ADDED_PIECE = 4
-W_U, W_OWN, W_OTHER, W_E0, W_E1 = range(5)
+W_U, W_OWN, W_OTHER, W_E = range(4)
 
 FLOPS = 2 * (B * N * D1 * ND + B * 2 * 2 * D1 * ND + B * N * 2 * D2 * ND)
 
@@ -141,10 +141,10 @@ def tile_ferminetoneelectronlayer_pa_t_kernel(tc, in_1e, in_2e, W_unmixed, b_unm
             panel, place = divmod(2 * piece + unit, 2 * PIECES)
             staged = piece_of[piece]
             bank = ps2.tile([P, N, 64], F32, name="pool%d_%d" % (piece, unit), tag="pool")
-            columns = bank[:].rearrange("p i (r a c) -> p i r a c", r=UNIT_ROWS, a=4, c=2)
+            columns = bank[:].rearrange("p i (r a t) -> p i r a t", r=UNIT_ROWS, a=2, t=4)
             for r in range(UNIT_ROWS):
                 for c in range(2):
-                    nc.tensor.matmul(out=columns[:, :, r, :, c],
+                    nc.tensor.matmul(out=columns[:, :, r, :, c:4 - c:3 - 2 * c],
                                      lhsT=staged[:, unit * UNIT_ROWS + r, c * P:(c + 1) * P],
                                      rhs=pool_matrix, start=True, stop=True)
             nc.scalar.copy(out=e_grouped[panel][:, :, 64 * place:64 * (place + 1)], in_=bank[:])
@@ -160,14 +160,16 @@ def tile_ferminetoneelectronlayer_pa_t_kernel(tc, in_1e, in_2e, W_unmixed, b_unm
             bank = ps2.tile([P, 4, P], F32, name="added_t%d" % unit, tag="aux")
             for sj in range(2):
                 for c in range(2):
-                    transpose_and_add(bank[:, 2 * sj + c, :],
+                    transpose_and_add(bank[:, 3 - c if sj else c, :],
                                       [added_halfsum[unit][:, sj, n, c * P:(c + 1) * P] for n in range(2)])
             added_bank[unit] = bank
 
         def copy_added(unit):
             panel, place = divmod(2 * ADDED_PIECE + unit, 2 * PIECES)
             walkers = e_grouped[panel][:].rearrange("p i (b t) -> p i b t", t=4)[:, :, 16 * place:16 * (place + 1), :]
-            nc.scalar.mul(out=walkers, in_=added_bank[unit][:].rearrange("p t (b i) -> p i b t", i=N), mul=0.25)
+            means = added_bank[unit][:].rearrange("p t (b i) -> p i b t", i=N)
+            nc.scalar.mul(out=walkers[:, 0:4, :, :], in_=means[:, 0:4, :, :], mul=0.25)
+            nc.scalar.mul(out=walkers[:, 4:8, :, :], in_=means[:, 4:8, :, ::-1], mul=0.25)
 
         def quantise_e(panel):
             e_mx[panel] = quantise(two, "e%d" % panel, e_grouped[panel][:].rearrange("p i c -> p (i c)"), N * P)
@@ -178,7 +180,7 @@ def tile_ferminetoneelectronlayer_pa_t_kernel(tc, in_1e, in_2e, W_unmixed, b_unm
             for i in (2 * q, 2 * q + 1):
                 acc = ps4.tile([P, ND], F32, name="acc%d_%d" % (panel, i), tag="acc")
                 mx_pass(acc, x_mx[panel], slice(i * P, (i + 1) * P), W_U, True, False)
-                mx_pass(acc, e_mx[panel], slice(i * P, (i + 1) * P), W_E0 if i < 4 else W_E1, False, True)
+                mx_pass(acc, e_mx[panel], slice(i * P, (i + 1) * P), W_E, False, True)
                 acc_of[pair].append(acc)
 
         def sum_pair(pair):
@@ -221,11 +223,9 @@ def tile_ferminetoneelectronlayer_pa_t_kernel(tc, in_1e, in_2e, W_unmixed, b_unm
 
         def prepare_w_unmixed_and_2e():
             u = group_weight("u", ((0, raw_unmixed[:]),))
-            e0 = group_weight("e0", ((0, raw_2e[:]),))
+            e = group_weight("e", ((0, raw_2e[:]),))
             quantise_weight(W_U, u)
-            e1 = group_weight("e1", ((0, raw_2e[:, 2:4, :]), (2, raw_2e[:, 0:2, :])))
-            quantise_weight(W_E0, e0)
-            quantise_weight(W_E1, e1)
+            quantise_weight(W_E, e)
 
         def slot(n):
             pair = n - LAG
@@ -272,8 +272,8 @@ def tile_ferminetoneelectronlayer_pa_t_kernel(tc, in_1e, in_2e, W_unmixed, b_unm
         ones = const.tile([P, P], BF16)
         nc.gpsimd.memset(ones[:], 1.0)
         bias = const.tile([P, ND], F32)
-        w_words = const.tile([P, 5, ND], U32, align_bytes=64)
-        w_scales = const.tile([P, 5, ND], U8, align_bytes=64)
+        w_words = const.tile([P, 4, ND], U32, align_bytes=64)
+        w_scales = const.tile([P, 4, ND], U8, align_bytes=64)
         ident = const.tile([P, P], F32)
         group_of_row = const.tile([P, 2, N, 2], F32)
         pool_tile = const.tile([P, N, 2, 2], BF16)
@@ -292,7 +292,10 @@ def tile_ferminetoneelectronlayer_pa_t_kernel(tc, in_1e, in_2e, W_unmixed, b_unm
             nc.sync.dma_start(out=raw_unmixed[:].rearrange("p (u e) n -> p u e n", e=2),
                               in_=W_unmixed.rearrange("(u p e) n -> p u e n", u=2, e=2))
             raw_2e = w_raw.tile([P, 4, ND], BF16)
-            nc.sync.dma_start(out=raw_2e[:], in_=W_2e.rearrange("(t p) n -> p t n", p=P))
+            blocks_2e = W_2e.rearrange("(t p) n -> p t n", p=P)
+            nc.sync.dma_start(out=raw_2e[:, 0:2, :], in_=blocks_2e[:, 0:2, :])
+            for t in (2, 3):
+                nc.sync.dma_start(out=raw_2e[:, t, :], in_=blocks_2e[:, 5 - t, :])
             load_x(3)
             for piece in range(AHEAD):
                 load_piece(piece)
@@ -301,10 +304,10 @@ def tile_ferminetoneelectronlayer_pa_t_kernel(tc, in_1e, in_2e, W_unmixed, b_unm
             nc.vector.tensor_reduce(out=group_of_row[:].rearrange("p a i j -> p (a i j)"),
                                     in_=ident[:].rearrange("p (g f) -> p g f", f=4),
                                     axis=mybir.AxisListType.X, op=ADD)
-            nc.vector.tensor_scalar_mul(out=pool_tile[:], in0=group_of_row[:].rearrange("p a i j -> p i a j"), scalar1=0.25)
-            bias_bank = ps2.tile([P, ND], F32, name="bias_bank", tag="aux")
-            nc.tensor.matmul(out=bias_bank[:], lhsT=ones[:], rhs=bias_row[:], start=True, stop=True)
-            nc.scalar.copy(out=bias[:], in_=bias_bank[:])
+            by_electron = group_of_row[:].rearrange("p a i j -> p i a j")
+            nc.vector.tensor_scalar_mul(out=pool_tile[:, 0:4, :, :], in0=by_electron[:, 0:4, :, :], scalar1=0.25)
+            for j in range(2):
+                nc.vector.tensor_scalar_mul(out=pool_tile[:, 4:8, :, j], in0=by_electron[:, 4:8, :, 1 - j], scalar1=0.25)
 
             transpose_x(0)
             add_electrons(0)
@@ -317,6 +320,9 @@ def tile_ferminetoneelectronlayer_pa_t_kernel(tc, in_1e, in_2e, W_unmixed, b_unm
                 quantise_x(panel)
                 quantise_means(panel)
             multiply_means(0)
+            bias_bank = ps4.tile([P, ND], F32, name="bias_bank", tag="acc")
+            nc.tensor.matmul(out=bias_bank[:], lhsT=ones[:], rhs=bias_row[:], start=True, stop=True)
+            nc.scalar.copy(out=bias[:], in_=bias_bank[:])
             add_bias(0)
             transpose_x(2)
             add_electrons(2)

@@ -140,14 +140,14 @@ def tile_ferminetoneelectronlayer_pa_t_kernel(tc, in_1e, in_2e, W_unmixed, b_unm
         def pool_unit(piece, unit):
             panel, place = divmod(2 * piece + unit, 2 * PIECES)
             staged = piece_of[piece]
-            bank = ps2.tile([P, N, 64], F32, name="pool%d_%d" % (piece, unit), tag="pool")
-            columns = bank[:].rearrange("p i (r a t) -> p i r a t", r=UNIT_ROWS, a=2, t=4)
+            bank = ps2.tile([P, 4, P], F32, name="pool%d_%d" % (piece, unit), tag="pool")
             for r in range(UNIT_ROWS):
                 for c in range(2):
-                    nc.tensor.matmul(out=columns[:, :, r, :, c:4 - c:3 - 2 * c],
+                    nc.tensor.matmul(out=bank[:, c:4 - c:3 - 2 * c, 16 * r:16 * (r + 1)],
                                      lhsT=staged[:, unit * UNIT_ROWS + r, c * P:(c + 1) * P],
                                      rhs=pool_matrix, start=True, stop=True)
-            nc.scalar.copy(out=e_grouped[panel][:, :, 64 * place:64 * (place + 1)], in_=bank[:])
+            nc.scalar.copy(out=e_grouped[panel][:, :, 64 * place:64 * (place + 1)].rearrange("p i (b t) -> p i b t", t=4),
+                           in_=bank[:].rearrange("p t (b i) -> p i b t", i=N))
 
         def add_rows(unit):
             rows = (piece_of[ADDED_PIECE][:, unit * UNIT_ROWS:(unit + 1) * UNIT_ROWS, :]
@@ -276,8 +276,8 @@ def tile_ferminetoneelectronlayer_pa_t_kernel(tc, in_1e, in_2e, W_unmixed, b_unm
         w_scales = const.tile([P, 4, ND], U8, align_bytes=64)
         ident = const.tile([P, P], F32)
         group_of_row = const.tile([P, 2, N, 2], F32)
-        pool_tile = const.tile([P, N, 2, 2], BF16)
-        pool_matrix = pool_tile[:].rearrange("p i a j -> p i (a j)")
+        pool_tile = const.tile([P, 2, 2, N], BF16)
+        pool_matrix = pool_tile[:].rearrange("p s a i -> p (s a i)")
 
         with tc.tile_pool(name="w_raw", bufs=1) as w_raw, tc.tile_pool(name="w_grouped", bufs=2) as w_grouped, \
              tc.tile_pool(name="early", bufs=2) as early:
@@ -304,10 +304,10 @@ def tile_ferminetoneelectronlayer_pa_t_kernel(tc, in_1e, in_2e, W_unmixed, b_unm
             nc.vector.tensor_reduce(out=group_of_row[:].rearrange("p a i j -> p (a i j)"),
                                     in_=ident[:].rearrange("p (g f) -> p g f", f=4),
                                     axis=mybir.AxisListType.X, op=ADD)
-            by_electron = group_of_row[:].rearrange("p a i j -> p i a j")
-            nc.vector.tensor_scalar_mul(out=pool_tile[:, 0:4, :, :], in0=by_electron[:, 0:4, :, :], scalar1=0.25)
+            by_spin = group_of_row[:].rearrange("p a i j -> p j a i")
             for j in range(2):
-                nc.vector.tensor_scalar_mul(out=pool_tile[:, 4:8, :, j], in0=by_electron[:, 4:8, :, 1 - j], scalar1=0.25)
+                nc.vector.tensor_scalar_mul(out=pool_tile[:, j, :, 0:4], in0=by_spin[:, j, :, 0:4], scalar1=0.25)
+                nc.vector.tensor_scalar_mul(out=pool_tile[:, j, :, 4:8], in0=by_spin[:, 1 - j, :, 4:8], scalar1=0.25)
 
             transpose_x(0)
             add_electrons(0)

@@ -15,8 +15,7 @@ ND = D1
 PANELS = B // P
 PIECES = 4
 N_PIECES = PANELS * PIECES
-PAIRS = 4
-N_PAIRS = PANELS * PAIRS
+N_HALVES = 2 * PANELS
 UNIT_ROWS = 8
 AHEAD = 3
 LAG = 5
@@ -34,16 +33,16 @@ def tile_ferminetoneelectronlayer_pa_t_kernel(tc, in_1e, in_2e, W_unmixed, b_unm
     with tc.manual_schedule(), \
          tc.tile_pool(name="const", bufs=1) as const, \
          tc.tile_pool(name="xpool", bufs=PANELS) as xpool, \
+         tc.tile_pool(name="big", bufs=7) as big, \
          tc.tile_pool(name="stage", bufs=AHEAD) as stage, \
          tc.tile_pool(name="two", bufs=2) as two, \
          tc.tile_pool(name="keep", bufs=PANELS) as keep, \
          tc.psum_pool(name="ps2", bufs=2) as ps2, \
          tc.psum_pool(name="ps4", bufs=4) as ps4:
 
-        x_of, piece_of, x_grouped, e_grouped, halfsums, m_grouped = {}, {}, {}, {}, {}, {}
+        x_of, unit_of, x_grouped, e_grouped, halfsums, m_grouped = {}, {}, {}, {}, {}, {}
         x_mx, m_mx, e_mx, g_psum, g_bias, acc_of, out_of = {}, {}, {}, {}, {}, {}, {}
         added_halfsum, added_bank = {}, {}
-        pools = {}
 
         def load_x(panel):
             x = xpool.tile([P, N, D1], BF16, name="x%d" % panel, tag="x")
@@ -52,16 +51,14 @@ def tile_ferminetoneelectronlayer_pa_t_kernel(tc, in_1e, in_2e, W_unmixed, b_unm
 
         def load_piece(piece):
             staged = stage.tile([P, 2 * UNIT_ROWS, D2], BF16, name="piece%d" % piece, tag="piece")
+            rows = rows_2e[2 * UNIT_ROWS * piece * P:2 * UNIT_ROWS * (piece + 1) * P, :]
+            for unit in range(2):
+                unit_of[2 * piece + unit] = staged[:, unit * UNIT_ROWS:(unit + 1) * UNIT_ROWS, :]
             if piece == ADDED_PIECE:
-                for unit in range(2):
-                    first = (2 * piece + unit) * P
-                    nc.sync.dma_start(out=staged[:, unit * UNIT_ROWS:(unit + 1) * UNIT_ROWS, :],
-                                      in_=tokens_2e[first:first + P, :, :])
+                nc.sync.dma_start(out=staged[:].rearrange("p (u r) d -> p u (r d)", u=2),
+                                  in_=rows.rearrange("(u p r) d -> p u (r d)", u=2, p=P))
             else:
-                first = 2 * UNIT_ROWS * piece * P
-                nc.sync.dma_start(out=staged[:],
-                                  in_=rows_2e[first:first + 2 * UNIT_ROWS * P, :].rearrange("(r p) d -> p r d", p=P))
-            piece_of[piece] = staged
+                nc.sync.dma_start(out=staged[:], in_=rows.rearrange("(r p) d -> p r d", p=P))
 
         def quantise(pool, name, grouped, width):
             words = pool.tile([P, width], U32, name=name + "_words", tag=name[0] + "_words", align_bytes=64)
@@ -80,43 +77,37 @@ def tile_ferminetoneelectronlayer_pa_t_kernel(tc, in_1e, in_2e, W_unmixed, b_unm
                 nc.tensor.matmul(out=dst, lhsT=part, rhs=ident[:], is_transpose=True,
                                  start=(n == 0), stop=(n == len(parts) - 1))
 
-        def transpose_x(panel):
+        def transpose_x(panel, first):
             words = x_of[panel][:].bitcast(F32)
-            grouped = pools["early"].tile([P, N, P, 4], BF16, name="xg%d" % panel, tag="xg", align_bytes=64)
-            grouped_words = (grouped[:].rearrange("p i b t -> p i (b t)").bitcast(F32)
+            if first == 0:
+                x_grouped[panel] = two.tile([P, N, P, 4], BF16, name="xg%d" % panel, tag="xg", align_bytes=64)
+            grouped_words = (x_grouped[panel][:].rearrange("p i b t -> p i (b t)").bitcast(F32)
                              .rearrange("p i (b u) -> p i b u", u=2))
-            for first in (0, 4):
-                banks = []
-                for i0 in (first, first + 2):
-                    bank = ps4.tile([P, 2, 2, P], F32, name="xt%d_%d" % (panel, i0), tag="acc")
-                    for i in range(2):
-                        for u in range(2):
-                            nc.tensor.transpose(bank[:, i, u, :], words[:, i0 + i, u * P:(u + 1) * P], ident[:])
-                    banks.append(bank)
-                for i0, bank in zip((first, first + 2), banks):
-                    nc.scalar.copy(out=grouped_words[:, i0:i0 + 2, :, :], in_=bank[:].rearrange("p i u b -> p i b u"))
-            x_grouped[panel] = grouped
-
-        def add_electrons(panel):
-            x = x_of[panel]
-            for spin in range(2):
-                e0 = 4 * spin
-                halfsum = pools["early"].tile([P, 2, D1], F32, name="hs%d_%d" % (panel, spin), tag="hs")
-                nc.vector.tensor_tensor(out=halfsum[:], in0=x[:, e0:e0 + 2, :], in1=x[:, e0 + 2:e0 + 4, :], op=ADD)
-                halfsums[(panel, spin)] = halfsum
-
-        def transpose_means(panel):
-            grouped = pools["early"].tile([P, 2, P, 4], BF16, name="mg%d" % panel, tag="mg", align_bytes=64)
             banks = []
-            for spin in range(2):
-                bank = ps2.tile([P, 4, P], F32, name="mt%d_%d" % (panel, spin), tag="aux")
-                for t in range(4):
-                    transpose_and_add(bank[:, t, :],
-                                      [halfsums[(panel, spin)][:, n, t * P:(t + 1) * P] for n in range(2)])
+            for i0 in (first, first + 2):
+                bank = ps2.tile([P, 2, 2, P], F32, name="xt%d_%d" % (panel, i0), tag="aux")
+                for i in range(2):
+                    for u in range(2):
+                        nc.tensor.transpose(bank[:, i, u, :], words[:, i0 + i, u * P:(u + 1) * P], ident[:])
                 banks.append(bank)
-            for spin in range(2):
-                nc.scalar.mul(out=grouped[:, spin, :, :], in_=banks[spin][:].rearrange("p t b -> p b t"), mul=0.25)
-            m_grouped[panel] = grouped
+            for i0, bank in zip((first, first + 2), banks):
+                nc.scalar.copy(out=grouped_words[:, i0:i0 + 2, :, :], in_=bank[:].rearrange("p i u b -> p i b u"))
+
+        def add_electrons(panel, spin):
+            x = x_of[panel]
+            e0 = 4 * spin
+            halfsum = two.tile([P, 2, D1], F32, name="hs%d_%d" % (panel, spin), tag="hs", bufs=4)
+            nc.vector.tensor_tensor(out=halfsum[:], in0=x[:, e0:e0 + 2, :], in1=x[:, e0 + 2:e0 + 4, :], op=ADD)
+            halfsums[(panel, spin)] = halfsum
+
+        def transpose_means(panel, spin):
+            if spin == 0:
+                m_grouped[panel] = two.tile([P, 2, P, 4], BF16, name="mg%d" % panel, tag="mg", align_bytes=64)
+            bank = ps2.tile([P, 4, P], F32, name="mt%d_%d" % (panel, spin), tag="aux")
+            for t in range(4):
+                transpose_and_add(bank[:, t, :],
+                                  [halfsums[(panel, spin)][:, n, t * P:(t + 1) * P] for n in range(2)])
+            nc.scalar.mul(out=m_grouped[panel][:, spin, :, :], in_=bank[:].rearrange("p t b -> p b t"), mul=0.25)
 
         def quantise_x(panel):
             x_mx[panel] = quantise(keep, "x%d" % panel, x_grouped[panel][:].rearrange("p i b t -> p (i b t)"), N * P)
@@ -137,21 +128,19 @@ def tile_ferminetoneelectronlayer_pa_t_kernel(tc, in_1e, in_2e, W_unmixed, b_unm
             for spin in range(2):
                 nc.vector.tensor_tensor(out=g_bias[panel][:, spin, :], in0=g_psum[panel][spin][:], in1=bias[:], op=ADD)
 
-        def pool_unit(piece, unit):
-            panel, place = divmod(2 * piece + unit, 2 * PIECES)
-            staged = piece_of[piece]
-            bank = ps2.tile([P, 4, P], F32, name="pool%d_%d" % (piece, unit), tag="pool")
+        def pool_unit(unit):
+            panel, place = divmod(unit, 2 * PIECES)
+            bank = ps2.tile([P, 4, P], F32, name="pool%d" % unit, tag="pool")
             for r in range(UNIT_ROWS):
                 for c in range(2):
                     nc.tensor.matmul(out=bank[:, c:4 - c:3 - 2 * c, 16 * r:16 * (r + 1)],
-                                     lhsT=staged[:, unit * UNIT_ROWS + r, c * P:(c + 1) * P],
+                                     lhsT=unit_of[unit][:, r, c * P:(c + 1) * P],
                                      rhs=pool_matrix, start=True, stop=True)
             nc.scalar.copy(out=e_grouped[panel][:, :, 64 * place:64 * (place + 1)].rearrange("p i (b t) -> p i b t", t=4),
                            in_=bank[:].rearrange("p t (b i) -> p i b t", i=N))
 
         def add_rows(unit):
-            rows = (piece_of[ADDED_PIECE][:, unit * UNIT_ROWS:(unit + 1) * UNIT_ROWS, :]
-                    .rearrange("p (a f) d -> p a f d", a=2))
+            rows = unit_of[unit].rearrange("p (a f) d -> p a f d", a=2)
             halfsum = two.tile([P, 2, 2, D2], F32, name="added_hs%d" % unit, tag="added_hs")
             nc.vector.tensor_tensor(out=halfsum[:], in0=rows[:, :, 0:2, :], in1=rows[:, :, 2:4, :], op=ADD)
             added_halfsum[unit] = halfsum
@@ -165,7 +154,7 @@ def tile_ferminetoneelectronlayer_pa_t_kernel(tc, in_1e, in_2e, W_unmixed, b_unm
             added_bank[unit] = bank
 
         def copy_added(unit):
-            panel, place = divmod(2 * ADDED_PIECE + unit, 2 * PIECES)
+            panel, place = divmod(unit, 2 * PIECES)
             walkers = e_grouped[panel][:].rearrange("p i (b t) -> p i b t", t=4)[:, :, 16 * place:16 * (place + 1), :]
             means = added_bank[unit][:].rearrange("p t (b i) -> p i b t", i=N)
             nc.scalar.mul(out=walkers[:, 0:4, :, :], in_=means[:, 0:4, :, :], mul=0.25)
@@ -174,172 +163,198 @@ def tile_ferminetoneelectronlayer_pa_t_kernel(tc, in_1e, in_2e, W_unmixed, b_unm
         def quantise_e(panel):
             e_mx[panel] = quantise(two, "e%d" % panel, e_grouped[panel][:].rearrange("p i c -> p (i c)"), N * P)
 
-        def multiply_pair(pair):
-            panel, q = divmod(pair, PAIRS)
-            acc_of[pair] = []
-            for i in (2 * q, 2 * q + 1):
+        def multiply_half(half):
+            panel, spin = divmod(half, 2)
+            for k in range(4):
+                i = 4 * spin + k
                 acc = ps4.tile([P, ND], F32, name="acc%d_%d" % (panel, i), tag="acc")
                 mx_pass(acc, x_mx[panel], slice(i * P, (i + 1) * P), W_U, True, False)
                 mx_pass(acc, e_mx[panel], slice(i * P, (i + 1) * P), W_E, False, True)
-                acc_of[pair].append(acc)
+                acc_of[4 * half + k] = acc
 
-        def sum_pair(pair):
-            panel, q = divmod(pair, PAIRS)
-            result = pools["out"].tile([P, 2, ND], F32, name="o%d" % pair, tag="o")
-            for n in range(2):
-                nc.vector.tensor_tensor(out=result[:, n, :], in0=acc_of[pair][n][:], in1=g_bias[panel][:, q // 2, :],
-                                        op=ADD)
-            out_of[pair] = result
+        def sum_half(half):
+            panel, spin = divmod(half, 2)
+            out_of[half] = big.tile([P, 4, ND], F32, name="o%d" % half, tag="big", align_bytes=64)
+            for k in range(4):
+                nc.vector.tensor_tensor(out=out_of[half][:, k, :], in0=acc_of[4 * half + k][:],
+                                        in1=g_bias[panel][:, spin, :], op=ADD)
 
-        def tanh_pair(pair):
-            nc.scalar.activation(out=out_of[pair][:], in_=out_of[pair][:], func=TANH)
+        def tanh_pair(half, pair):
+            tiles = out_of[half][:, 2 * pair:2 * pair + 2, :]
+            nc.scalar.activation(out=tiles, in_=tiles, func=TANH)
 
-        def skip_pair(pair):
-            panel, q = divmod(pair, PAIRS)
-            nc.vector.tensor_tensor(out=out_of[pair][:], in0=out_of[pair][:], in1=x_of[panel][:, 2 * q:2 * q + 2, :],
-                                    op=ADD)
+        def skip_pair(half, pair, engine):
+            panel, spin = divmod(half, 2)
+            tiles = out_of[half][:, 2 * pair:2 * pair + 2, :]
+            i0 = 4 * spin + 2 * pair
+            engine.tensor_tensor(out=tiles, in0=tiles, in1=x_of[panel][:, i0:i0 + 2, :], op=ADD)
 
-        def store_pair(pair):
-            panel, q = divmod(pair, PAIRS)
-            nc.sync.dma_start(out=out[panel * P:(panel + 1) * P, 2 * q:2 * q + 2, :], in_=out_of[pair][:])
+        def release_gpsimd():
+            nc.vector.memset(token[:], 0.0)
+            nc.gpsimd.tensor_copy(out=token_read[:], in_=token[:])
 
-        def group_weight(name, parts):
-            grouped = pools["w_grouped"].tile([P, ND, 4], BF16, name="wg_" + name, tag="wg", align_bytes=64)
-            view = grouped[:].rearrange("p (c i) t -> p c t i", i=4)
-            for t0, rows in parts:
-                nc.vector.tensor_copy(out=view[:, :, t0:t0 + rows.shape[1], :],
-                                      in_=rows.rearrange("p t (c i) -> p c t i", i=4))
-            return grouped
+        def store_half(half):
+            panel, spin = divmod(half, 2)
+            rows = out[panel * P:(panel + 1) * P, 4 * spin:4 * spin + 4, :]
+            if half < N_HALVES - 1:
+                nc.sync.dma_start(out=rows, in_=out_of[half][:])
+            else:
+                for pair in range(2):
+                    nc.sync.dma_start(out=rows[:, 2 * pair:2 * pair + 2, :], in_=out_of[half][:, 2 * pair:2 * pair + 2, :])
+
+        def group_weight(grouped, rows):
+            nc.vector.tensor_copy(out=grouped.rearrange("p (c i) t -> p c t i", i=4),
+                                  in_=rows.rearrange("p t (c i) -> p c t i", i=4))
 
         def quantise_weight(weight, grouped):
             nc.vector.quantize_mx(out=w_words[:, weight, :].bitcast(FP8X4), scales=w_scales[:, weight, :],
-                                  in_=grouped[:].rearrange("p n t -> p (n t)"))
+                                  in_=grouped.rearrange("p n t -> p (n t)"))
 
-        def prepare_w_mixed():
-            own = group_weight("own", ((0, raw_mixed[:, 0:4, :]),))
-            other = group_weight("other", ((0, raw_mixed[:, 4:8, :]),))
-            quantise_weight(W_OWN, own)
-            quantise_weight(W_OTHER, other)
-
-        def prepare_w_unmixed_and_2e():
-            u = group_weight("u", ((0, raw_unmixed[:]),))
-            e = group_weight("e", ((0, raw_2e[:]),))
-            quantise_weight(W_U, u)
-            quantise_weight(W_E, e)
+        def pool_piece(piece):
+            panel, place = divmod(piece, PIECES)
+            if place == 0:
+                e_grouped[panel] = two.tile([P, N, 4 * P], BF16, name="eg%d" % panel, tag="eg", align_bytes=64)
+            for unit in (2 * piece, 2 * piece + 1):
+                if piece == ADDED_PIECE:
+                    add_rows(unit)
+                else:
+                    pool_unit(unit)
 
         def slot(n):
-            pair = n - LAG
+            half, odd = divmod(n - LAG, 2)
             panel, place = divmod(n, PIECES)
-            pooling = n < N_PIECES
-            if pooling and place == 0:
-                e_grouped[panel] = two.tile([P, N, 4 * P], BF16, name="eg%d" % panel, tag="eg", align_bytes=64)
-            if 0 <= pair < N_PAIRS:
-                sum_pair(pair)
-            if 0 <= pair - 1 < N_PAIRS:
-                skip_pair(pair - 1)
-            if place == 0 and 0 < panel < PANELS:
-                add_bias(panel)
+            added = (2 * ADDED_PIECE, 2 * ADDED_PIECE + 1)
+            if place == 0 and panel <= PANELS:
+                quantise_e(panel - 1)
+            if not odd and 0 <= half < N_HALVES:
+                if half > 0:
+                    release_gpsimd()
+                    skip_pair(half - 1, 0, nc.gpsimd)
+                sum_half(half)
+                if half > 0:
+                    skip_pair(half - 1, 1, nc.vector)
+            if not odd and half == N_HALVES:
+                for pair in range(2):
+                    skip_pair(half - 1, pair, nc.vector)
+            if odd and 0 <= half < N_HALVES:
+                tanh_pair(half, 1)
             if n - 2 == ADDED_PIECE:
-                for unit in range(2):
+                for unit in added:
                     copy_added(unit)
-            for unit in range(2):
-                if n == ADDED_PIECE:
-                    add_rows(unit)
-                elif pooling:
-                    pool_unit(n, unit)
-            if 0 <= pair < N_PAIRS:
-                tanh_pair(pair)
-            if pooling and place == PIECES - 1:
-                quantise_e(panel)
+            if n == LAG - 1:
+                multiply_half(0)
+            if n in (4, 5):
+                transpose_x(3, 4 * (n - 4))
+                add_electrons(3, n - 4)
+            if n < N_PIECES:
+                pool_piece(n)
+            if n in (6, 7):
+                transpose_means(3, n - 6)
+            if n == 6:
+                quantise_x(3)
+            if n == 8:
+                quantise_means(3)
+            if place == 3 and 0 < panel < PANELS:
+                add_bias(panel)
+            if not odd and 0 <= half < N_HALVES:
+                tanh_pair(half, 0)
             if n - 1 == ADDED_PIECE:
-                for unit in range(2):
+                for unit in added:
                     transpose_added(unit)
-            if 0 <= pair + 1 < N_PAIRS:
-                multiply_pair(pair + 1)
-            if place == PIECES - 1 and panel + 1 < PANELS:
-                multiply_means(panel + 1)
+            if odd == half % 2 and 0 < half + 1 < N_HALVES:
+                multiply_half(half + 1)
+            if place == 2 and 0 < panel < PANELS:
+                multiply_means(panel)
             if n + AHEAD < N_PIECES:
                 load_piece(n + AHEAD)
             elif n + AHEAD == N_PIECES:
-                for done in range(0, pair):
-                    store_pair(done)
-            elif pair - 1 < N_PAIRS:
-                store_pair(pair - 1)
+                for done in range(0, half):
+                    store_half(done)
+            elif not odd and half - 1 < N_HALVES:
+                store_half(half - 1)
 
         bias_row = const.tile([P, ND], BF16)
         nc.gpsimd.memset(bias_row[:], 0.0)
-        nc.scalar.dma_start(out=bias_row[0:1, :], in_=b_unmixed.unsqueeze(0))
         ones = const.tile([P, P], BF16)
         nc.gpsimd.memset(ones[:], 1.0)
         bias = const.tile([P, ND], F32)
         w_words = const.tile([P, 4, ND], U32, align_bytes=64)
         w_scales = const.tile([P, 4, ND], U8, align_bytes=64)
         ident = const.tile([P, P], F32)
+        token = const.tile([P, 1], F32)
+        token_read = const.tile([P, 1], F32)
         group_of_row = const.tile([P, 2, N, 2], F32)
         pool_tile = const.tile([P, 2, 2, N], BF16)
         pool_matrix = pool_tile[:].rearrange("p s a i -> p (s a i)")
 
-        with tc.tile_pool(name="w_raw", bufs=1) as w_raw, tc.tile_pool(name="w_grouped", bufs=2) as w_grouped, \
-             tc.tile_pool(name="early", bufs=2) as early:
-            pools["w_grouped"] = w_grouped
-            pools["early"] = early
-            load_x(0)
-            load_x(1)
-            raw_mixed = w_raw.tile([P, 8, ND], BF16)
-            nc.sync.dma_start(out=raw_mixed[:], in_=W_mixed.rearrange("(t p) n -> p t n", p=P))
-            load_x(2)
-            raw_unmixed = w_raw.tile([P, 4, ND], BF16)
-            nc.sync.dma_start(out=raw_unmixed[:].rearrange("p (u e) n -> p u e n", e=2),
-                              in_=W_unmixed.rearrange("(u p e) n -> p u e n", u=2, e=2))
-            raw_2e = w_raw.tile([P, 4, ND], BF16)
-            blocks_2e = W_2e.rearrange("(t p) n -> p t n", p=P)
-            nc.sync.dma_start(out=raw_2e[:, 0:2, :], in_=blocks_2e[:, 0:2, :])
-            for t in (2, 3):
-                nc.sync.dma_start(out=raw_2e[:, t, :], in_=blocks_2e[:, 5 - t, :])
-            load_x(3)
-            for piece in range(AHEAD):
-                load_piece(piece)
+        make_identity(nc, ident[:])
+        load_x(0)
+        nc.sync.dma_start(out=bias_row[0:1, :], in_=b_unmixed.unsqueeze(0))
+        load_x(1)
+        raw_mixed = big.tile([P, 8, ND], BF16, name="raw_mixed", tag="big", align_bytes=64)
+        nc.sync.dma_start(out=raw_mixed[:], in_=W_mixed.rearrange("(t p) n -> p t n", p=P))
+        load_piece(0)
+        load_x(2)
+        load_piece(1)
+        raw_rest = big.tile([P, 8, ND], BF16, name="raw_rest", tag="big", align_bytes=64)
+        raw_unmixed = raw_rest[:, 0:4, :]
+        nc.sync.dma_start(out=raw_unmixed.rearrange("p (u e) n -> p u e n", e=2),
+                          in_=W_unmixed.rearrange("(u p e) n -> p u e n", u=2, e=2))
+        raw_2e = raw_rest[:, 4:8, :]
+        blocks_2e = W_2e.rearrange("(t p) n -> p t n", p=P)
+        nc.sync.dma_start(out=raw_2e[:, 0:2, :], in_=blocks_2e[:, 0:2, :])
+        for t in (2, 3):
+            nc.sync.dma_start(out=raw_2e[:, t, :], in_=blocks_2e[:, 5 - t, :])
+        load_piece(2)
+        grouped_mixed = big.tile([P, 2, ND, 4], BF16, name="grouped_mixed", tag="big", align_bytes=64)
+        grouped_rest = big.tile([P, 2, ND, 4], BF16, name="grouped_rest", tag="big", align_bytes=64)
 
-            make_identity(nc, ident[:])
-            nc.vector.tensor_reduce(out=group_of_row[:].rearrange("p a i j -> p (a i j)"),
-                                    in_=ident[:].rearrange("p (g f) -> p g f", f=4),
-                                    axis=mybir.AxisListType.X, op=ADD)
-            by_spin = group_of_row[:].rearrange("p a i j -> p j a i")
-            for j in range(2):
-                nc.vector.tensor_scalar_mul(out=pool_tile[:, j, :, 0:4], in0=by_spin[:, j, :, 0:4], scalar1=0.25)
-                nc.vector.tensor_scalar_mul(out=pool_tile[:, j, :, 4:8], in0=by_spin[:, 1 - j, :, 4:8], scalar1=0.25)
+        nc.vector.tensor_reduce(out=group_of_row[:].rearrange("p a i j -> p (a i j)"),
+                                in_=ident[:].rearrange("p (g f) -> p g f", f=4),
+                                axis=mybir.AxisListType.X, op=ADD)
+        by_spin = group_of_row[:].rearrange("p a i j -> p j a i")
+        for j in range(2):
+            nc.vector.tensor_scalar_mul(out=pool_tile[:, j, :, 0:4], in0=by_spin[:, j, :, 0:4], scalar1=0.25)
+            nc.vector.tensor_scalar_mul(out=pool_tile[:, j, :, 4:8], in0=by_spin[:, 1 - j, :, 4:8], scalar1=0.25)
 
-            transpose_x(0)
-            add_electrons(0)
-            transpose_x(1)
-            transpose_means(0)
-            add_electrons(1)
-            transpose_means(1)
-            prepare_w_mixed()
-            for panel in range(2):
-                quantise_x(panel)
-                quantise_means(panel)
-            multiply_means(0)
-            bias_bank = ps4.tile([P, ND], F32, name="bias_bank", tag="acc")
-            nc.tensor.matmul(out=bias_bank[:], lhsT=ones[:], rhs=bias_row[:], start=True, stop=True)
-            nc.scalar.copy(out=bias[:], in_=bias_bank[:])
-            add_bias(0)
-            transpose_x(2)
-            add_electrons(2)
-            slot(0)
-            transpose_x(3)
-            transpose_means(2)
-            add_electrons(3)
-            slot(1)
-            transpose_means(3)
-            prepare_w_unmixed_and_2e()
-            slot(2)
-            for panel in range(2, 4):
-                quantise_x(panel)
-                quantise_means(panel)
-            slot(3)
-
-        with tc.tile_pool(name="results", bufs=N_PAIRS) as results:
-            pools["out"] = results
-            for n in range(4, N_PAIRS + LAG + 1):
-                slot(n)
+        for panel in (0, 1):
+            for spin in range(2):
+                transpose_x(panel, 4 * spin)
+                add_electrons(panel, spin)
+            for spin in range(2):
+                transpose_means(panel, spin)
+        group_weight(grouped_mixed[:, 0], raw_mixed[:, 0:4, :])
+        quantise_x(0)
+        group_weight(grouped_mixed[:, 1], raw_mixed[:, 4:8, :])
+        quantise_means(0)
+        quantise_weight(W_OWN, grouped_mixed[:, 0])
+        quantise_x(1)
+        quantise_weight(W_OTHER, grouped_mixed[:, 1])
+        quantise_means(1)
+        pool_piece(0)
+        load_piece(3)
+        load_x(3)
+        for spin in range(2):
+            transpose_x(2, 4 * spin)
+            add_electrons(2, spin)
+        multiply_means(0)
+        bias_bank = ps4.tile([P, ND], F32, name="bias_bank", tag="acc")
+        nc.tensor.matmul(out=bias_bank[:], lhsT=ones[:], rhs=bias_row[:], start=True, stop=True)
+        nc.scalar.copy(out=bias[:], in_=bias_bank[:])
+        add_bias(0)
+        pool_piece(1)
+        load_piece(4)
+        for spin in range(2):
+            transpose_means(2, spin)
+        group_weight(grouped_rest[:, 0], raw_unmixed)
+        quantise_x(2)
+        group_weight(grouped_rest[:, 1], raw_2e)
+        quantise_means(2)
+        quantise_weight(W_U, grouped_rest[:, 0])
+        quantise_weight(W_E, grouped_rest[:, 1])
+        pool_piece(2)
+        load_piece(5)
+        pool_piece(3)
+        load_piece(6)
+        for n in range(PIECES, 2 * N_HALVES + LAG + 1):
+            slot(n)

@@ -179,28 +179,29 @@ def tile_ferminetoneelectronlayer_pa_t_kernel(tc, in_1e, in_2e, W_unmixed, b_unm
                 nc.vector.tensor_tensor(out=out_of[half][:, k, :], in0=acc_of[4 * half + k][:],
                                         in1=g_bias[panel][:, spin, :], op=ADD)
 
-        def tanh_pair(half, pair):
-            tiles = out_of[half][:, 2 * pair:2 * pair + 2, :]
-            nc.scalar.activation(out=tiles, in_=tiles, func=TANH)
+        def tanh_tiles(half, k0, tiles):
+            part = out_of[half][:, k0:k0 + tiles, :]
+            nc.scalar.activation(out=part, in_=part, func=TANH)
 
-        def skip_pair(half, pair, engine):
+        def skip_tiles(half, k0, tiles):
             panel, spin = divmod(half, 2)
-            tiles = out_of[half][:, 2 * pair:2 * pair + 2, :]
-            i0 = 4 * spin + 2 * pair
-            engine.tensor_tensor(out=tiles, in0=tiles, in1=x_of[panel][:, i0:i0 + 2, :], op=ADD)
-
-        def release_gpsimd():
-            nc.vector.memset(token[:], 0.0)
-            nc.gpsimd.tensor_copy(out=token_read[:], in_=token[:])
+            part = out_of[half][:, k0:k0 + tiles, :]
+            i0 = 4 * spin + k0
+            nc.vector.tensor_tensor(out=part, in0=part, in1=x_of[panel][:, i0:i0 + tiles, :], op=ADD)
 
         def store_half(half):
             panel, spin = divmod(half, 2)
             rows = out[panel * P:(panel + 1) * P, 4 * spin:4 * spin + 4, :]
-            if half < N_HALVES - 1:
-                nc.sync.dma_start(out=rows, in_=out_of[half][:])
-            else:
-                for pair in range(2):
-                    nc.sync.dma_start(out=rows[:, 2 * pair:2 * pair + 2, :], in_=out_of[half][:, 2 * pair:2 * pair + 2, :])
+            nc.sync.dma_start(out=rows, in_=out_of[half][:])
+
+        def finish_last_half():
+            half = N_HALVES - 1
+            panel, spin = divmod(half, 2)
+            for k0, tiles in ((0, 2), (2, 1), (3, 1)):
+                tanh_tiles(half, k0, tiles)
+                skip_tiles(half, k0, tiles)
+                nc.sync.dma_start(out=out[panel * P:(panel + 1) * P, 4 * spin + k0:4 * spin + k0 + tiles, :],
+                                  in_=out_of[half][:, k0:k0 + tiles, :])
 
         def group_weight(grouped, rows):
             nc.vector.tensor_copy(out=grouped.rearrange("p (c i) t -> p c t i", i=4),
@@ -227,22 +228,22 @@ def tile_ferminetoneelectronlayer_pa_t_kernel(tc, in_1e, in_2e, W_unmixed, b_unm
             if place == 0 and panel <= PANELS:
                 quantise_e(panel - 1)
             if not odd and 0 <= half < N_HALVES:
+                if half % 2 == 1:
+                    sum_half(half)
                 if half > 0:
-                    release_gpsimd()
-                    skip_pair(half - 1, 0, nc.gpsimd)
-                sum_half(half)
-                if half > 0:
-                    skip_pair(half - 1, 1, nc.vector)
-            if not odd and half == N_HALVES:
-                for pair in range(2):
-                    skip_pair(half - 1, pair, nc.vector)
-            if odd and 0 <= half < N_HALVES:
-                tanh_pair(half, 1)
+                    for pair in range(2):
+                        skip_tiles(half - 1, 2 * pair, 2)
+                if half % 2 == 0:
+                    sum_half(half)
+            if odd and 0 <= half < N_HALVES - 1:
+                tanh_tiles(half, 2, 2)
             if n - 2 == ADDED_PIECE:
                 for unit in added:
                     copy_added(unit)
             if n == LAG - 1:
                 multiply_half(0)
+            if n == 4:
+                add_bias(0)
             if n in (4, 5):
                 transpose_x(3, 4 * (n - 4))
                 add_electrons(3, n - 4)
@@ -256,8 +257,8 @@ def tile_ferminetoneelectronlayer_pa_t_kernel(tc, in_1e, in_2e, W_unmixed, b_unm
                 quantise_means(3)
             if place == 3 and 0 < panel < PANELS:
                 add_bias(panel)
-            if not odd and 0 <= half < N_HALVES:
-                tanh_pair(half, 0)
+            if not odd and 0 <= half < N_HALVES - 1:
+                tanh_tiles(half, 0, 2)
             if n - 1 == ADDED_PIECE:
                 for unit in added:
                     transpose_added(unit)
@@ -270,7 +271,7 @@ def tile_ferminetoneelectronlayer_pa_t_kernel(tc, in_1e, in_2e, W_unmixed, b_unm
             elif n + AHEAD == N_PIECES:
                 for done in range(0, half):
                     store_half(done)
-            elif not odd and half - 1 < N_HALVES:
+            elif not odd:
                 store_half(half - 1)
 
         bias_row = const.tile([P, ND], BF16)
@@ -281,8 +282,6 @@ def tile_ferminetoneelectronlayer_pa_t_kernel(tc, in_1e, in_2e, W_unmixed, b_unm
         w_words = const.tile([P, 4, ND], U32, align_bytes=64)
         w_scales = const.tile([P, 4, ND], U8, align_bytes=64)
         ident = const.tile([P, P], F32)
-        token = const.tile([P, 1], F32)
-        token_read = const.tile([P, 1], F32)
         group_of_row = const.tile([P, 2, N, 2], F32)
         pool_tile = const.tile([P, 2, 2, N], BF16)
         pool_matrix = pool_tile[:].rearrange("p s a i -> p (s a i)")
@@ -321,6 +320,10 @@ def tile_ferminetoneelectronlayer_pa_t_kernel(tc, in_1e, in_2e, W_unmixed, b_unm
             for spin in range(2):
                 transpose_x(panel, 4 * spin)
                 add_electrons(panel, spin)
+            if panel == 0:
+                bias_bank = ps4.tile([P, ND], F32, name="bias_bank", tag="acc")
+                nc.tensor.matmul(out=bias_bank[:], lhsT=ones[:], rhs=bias_row[:], start=True, stop=True)
+                nc.scalar.copy(out=bias[:], in_=bias_bank[:])
             for spin in range(2):
                 transpose_means(panel, spin)
         group_weight(grouped_mixed[:, 0], raw_mixed[:, 0:4, :])
@@ -337,11 +340,6 @@ def tile_ferminetoneelectronlayer_pa_t_kernel(tc, in_1e, in_2e, W_unmixed, b_unm
         for spin in range(2):
             transpose_x(2, 4 * spin)
             add_electrons(2, spin)
-        multiply_means(0)
-        bias_bank = ps4.tile([P, ND], F32, name="bias_bank", tag="acc")
-        nc.tensor.matmul(out=bias_bank[:], lhsT=ones[:], rhs=bias_row[:], start=True, stop=True)
-        nc.scalar.copy(out=bias[:], in_=bias_bank[:])
-        add_bias(0)
         pool_piece(1)
         load_piece(4)
         for spin in range(2):
@@ -356,5 +354,7 @@ def tile_ferminetoneelectronlayer_pa_t_kernel(tc, in_1e, in_2e, W_unmixed, b_unm
         load_piece(5)
         pool_piece(3)
         load_piece(6)
-        for n in range(PIECES, 2 * N_HALVES + LAG + 1):
+        multiply_means(0)
+        for n in range(PIECES, 2 * N_HALVES + LAG - 1):
             slot(n)
+        finish_last_half()

@@ -19,7 +19,8 @@ N_HALVES = 2 * PANELS
 UNIT_ROWS = 8
 AHEAD = 3
 LAG = 5
-ADDED_PIECE = 4
+ADDED_PLACES = 2
+FIRST_PAIRED = 16
 W_U, W_OWN, W_OTHER, W_E = range(4)
 
 FLOPS = 2 * (B * N * D1 * ND + B * 2 * 2 * D1 * ND + B * N * 2 * D2 * ND)
@@ -49,16 +50,26 @@ def tile_ferminetoneelectronlayer_pa_t_kernel(tc, in_1e, in_2e, W_unmixed, b_unm
             nc.sync.dma_start(out=x[:], in_=in_1e[panel * P:(panel + 1) * P, :, :])
             x_of[panel] = x
 
+        def is_added(unit):
+            return unit % 2 == 1 and unit // 2 % PIECES < ADDED_PLACES
+
+        def run_of(unit):
+            return 2 if unit % 2 == 0 and unit // 2 >= FIRST_PAIRED else 1
+
         def load_piece(piece):
             staged = stage.tile([P, 2 * UNIT_ROWS, D2], BF16, name="piece%d" % piece, tag="piece")
-            rows = rows_2e[2 * UNIT_ROWS * piece * P:2 * UNIT_ROWS * (piece + 1) * P, :]
-            for unit in range(2):
-                unit_of[2 * piece + unit] = staged[:, unit * UNIT_ROWS:(unit + 1) * UNIT_ROWS, :]
-            if piece == ADDED_PIECE:
-                nc.sync.dma_start(out=staged[:].rearrange("p (u r) d -> p u (r d)", u=2),
-                                  in_=rows.rearrange("(u p r) d -> p u (r d)", u=2, p=P))
-            else:
+            units = (2 * piece, 2 * piece + 1)
+            for k, unit in enumerate(units):
+                unit_of[unit] = staged[:, k * UNIT_ROWS:(k + 1) * UNIT_ROWS, :]
+            if run_of(units[0]) == 1 and not is_added(units[1]):
+                rows = rows_2e[units[0] * UNIT_ROWS * P:(units[1] + 1) * UNIT_ROWS * P, :]
                 nc.sync.dma_start(out=staged[:], in_=rows.rearrange("(r p) d -> p r d", p=P))
+            else:
+                for unit in units:
+                    run = UNIT_ROWS if is_added(unit) else run_of(unit)
+                    rows = rows_2e[unit * UNIT_ROWS * P:(unit + 1) * UNIT_ROWS * P, :]
+                    nc.sync.dma_start(out=unit_of[unit].rearrange("p (r e) d -> p r (e d)", e=run),
+                                      in_=rows.rearrange("(r p e) d -> p r (e d)", p=P, e=run))
 
         def quantise(pool, name, grouped, width):
             words = pool.tile([P, width], U32, name=name + "_words", tag=name[0] + "_words", align_bytes=64)
@@ -130,12 +141,16 @@ def tile_ferminetoneelectronlayer_pa_t_kernel(tc, in_1e, in_2e, W_unmixed, b_unm
 
         def pool_unit(unit):
             panel, place = divmod(unit, 2 * PIECES)
+            run = run_of(unit)
+            tiles = UNIT_ROWS // run
+            width = P // tiles
             bank = ps2.tile([P, 4, P], F32, name="pool%d" % unit, tag="pool")
-            for r in range(UNIT_ROWS):
+            for r in range(tiles):
                 for c in range(2):
-                    nc.tensor.matmul(out=bank[:, c:4 - c:3 - 2 * c, 16 * r:16 * (r + 1)],
-                                     lhsT=unit_of[unit][:, r, c * P:(c + 1) * P],
-                                     rhs=pool_matrix, start=True, stop=True)
+                    for e in range(run):
+                        nc.tensor.matmul(out=bank[:, c:4 - c:3 - 2 * c, width * r:width * (r + 1)],
+                                         lhsT=unit_of[unit][:, run * r + e, c * P:(c + 1) * P],
+                                         rhs=pool_matrix[run], start=(e == 0), stop=(e == run - 1))
             nc.scalar.copy(out=e_grouped[panel][:, :, 64 * place:64 * (place + 1)].rearrange("p i (b t) -> p i b t", t=4),
                            in_=bank[:].rearrange("p t (b i) -> p i b t", i=N))
 
@@ -146,7 +161,7 @@ def tile_ferminetoneelectronlayer_pa_t_kernel(tc, in_1e, in_2e, W_unmixed, b_unm
             added_halfsum[unit] = halfsum
 
         def transpose_added(unit):
-            bank = ps2.tile([P, 4, P], F32, name="added_t%d" % unit, tag="aux")
+            bank = ps2.tile([P, 4, P], F32, name="added_t%d" % unit, tag="pool")
             for sj in range(2):
                 for c in range(2):
                     transpose_and_add(bank[:, 3 - c if sj else c, :],
@@ -216,15 +231,23 @@ def tile_ferminetoneelectronlayer_pa_t_kernel(tc, in_1e, in_2e, W_unmixed, b_unm
             if place == 0:
                 e_grouped[panel] = two.tile([P, N, 4 * P], BF16, name="eg%d" % panel, tag="eg", align_bytes=64)
             for unit in (2 * piece, 2 * piece + 1):
-                if piece == ADDED_PIECE:
-                    add_rows(unit)
-                else:
+                if not is_added(unit):
                     pool_unit(unit)
+
+        def add_second(piece):
+            if piece < N_PIECES and is_added(2 * piece + 1):
+                add_rows(2 * piece + 1)
+
+        def finish_added(piece):
+            unit = 2 * piece + 1
+            if 0 <= piece < N_PIECES and is_added(unit):
+                transpose_added(unit)
+                copy_added(unit)
 
         def slot(n):
             half, odd = divmod(n - LAG, 2)
             panel, place = divmod(n, PIECES)
-            added = (2 * ADDED_PIECE, 2 * ADDED_PIECE + 1)
+            finish_added(n - 1)
             if place == 0 and panel <= PANELS:
                 quantise_e(panel - 1)
             if not odd and 0 <= half < N_HALVES:
@@ -237,9 +260,6 @@ def tile_ferminetoneelectronlayer_pa_t_kernel(tc, in_1e, in_2e, W_unmixed, b_unm
                     sum_half(half)
             if odd and 0 <= half < N_HALVES - 1:
                 tanh_tiles(half, 2, 2)
-            if n - 2 == ADDED_PIECE:
-                for unit in added:
-                    copy_added(unit)
             if n == LAG - 1:
                 multiply_half(0)
             if n == 4:
@@ -257,11 +277,9 @@ def tile_ferminetoneelectronlayer_pa_t_kernel(tc, in_1e, in_2e, W_unmixed, b_unm
                 quantise_means(3)
             if place == 3 and 0 < panel < PANELS:
                 add_bias(panel)
+            add_second(n)
             if not odd and 0 <= half < N_HALVES - 1:
                 tanh_tiles(half, 0, 2)
-            if n - 1 == ADDED_PIECE:
-                for unit in added:
-                    transpose_added(unit)
             if odd == half % 2 and 0 < half + 1 < N_HALVES:
                 multiply_half(half + 1)
             if place == 2 and 0 < panel < PANELS:
@@ -282,10 +300,7 @@ def tile_ferminetoneelectronlayer_pa_t_kernel(tc, in_1e, in_2e, W_unmixed, b_unm
         w_words = const.tile([P, 4, ND], U32, align_bytes=64)
         w_scales = const.tile([P, 4, ND], U8, align_bytes=64)
         ident = const.tile([P, P], F32)
-        group_of_row = const.tile([P, 2, N, 2], F32)
-        pool_tile = const.tile([P, 2, 2, N], BF16)
-        pool_matrix = pool_tile[:].rearrange("p s a i -> p (s a i)")
-
+        pool_matrix = {}
         make_identity(nc, ident[:])
         load_x(0)
         nc.sync.dma_start(out=bias_row[0:1, :], in_=b_unmixed.unsqueeze(0))
@@ -308,13 +323,18 @@ def tile_ferminetoneelectronlayer_pa_t_kernel(tc, in_1e, in_2e, W_unmixed, b_unm
         grouped_mixed = big.tile([P, 2, ND, 4], BF16, name="grouped_mixed", tag="big", align_bytes=64)
         grouped_rest = big.tile([P, 2, ND, 4], BF16, name="grouped_rest", tag="big", align_bytes=64)
 
-        nc.vector.tensor_reduce(out=group_of_row[:].rearrange("p a i j -> p (a i j)"),
-                                in_=ident[:].rearrange("p (g f) -> p g f", f=4),
-                                axis=mybir.AxisListType.X, op=ADD)
-        by_spin = group_of_row[:].rearrange("p a i j -> p j a i")
-        for j in range(2):
-            nc.vector.tensor_scalar_mul(out=pool_tile[:, j, :, 0:4], in0=by_spin[:, j, :, 0:4], scalar1=0.25)
-            nc.vector.tensor_scalar_mul(out=pool_tile[:, j, :, 4:8], in0=by_spin[:, 1 - j, :, 4:8], scalar1=0.25)
+        for run in (1, 2):
+            f = 4 // run
+            group_of_run = const.tile([P, 2 * run, N, 2], F32, name="group%d" % run)
+            nc.vector.tensor_reduce(out=group_of_run[:].rearrange("p a i j -> p (a i j)"),
+                                    in_=ident[:].rearrange("p (g f) -> p g f", f=f),
+                                    axis=mybir.AxisListType.X, op=ADD)
+            by_spin = group_of_run[:].rearrange("p a i j -> p j a i")
+            pool_tile = const.tile([P, 2, 2 * run, N], BF16, name="pool_tile%d" % run)
+            for j in range(2):
+                nc.vector.tensor_scalar_mul(out=pool_tile[:, j, :, 0:4], in0=by_spin[:, j, :, 0:4], scalar1=0.25)
+                nc.vector.tensor_scalar_mul(out=pool_tile[:, j, :, 4:8], in0=by_spin[:, 1 - j, :, 4:8], scalar1=0.25)
+            pool_matrix[run] = pool_tile[:].rearrange("p s a i -> p (s a i)")
 
         for panel in (0, 1):
             for spin in range(2):
@@ -340,18 +360,22 @@ def tile_ferminetoneelectronlayer_pa_t_kernel(tc, in_1e, in_2e, W_unmixed, b_unm
         for spin in range(2):
             transpose_x(2, 4 * spin)
             add_electrons(2, spin)
+        add_second(0)
         pool_piece(1)
         load_piece(4)
+        finish_added(0)
         for spin in range(2):
             transpose_means(2, spin)
         group_weight(grouped_rest[:, 0], raw_unmixed)
         quantise_x(2)
+        add_second(1)
         group_weight(grouped_rest[:, 1], raw_2e)
         quantise_means(2)
         quantise_weight(W_U, grouped_rest[:, 0])
         quantise_weight(W_E, grouped_rest[:, 1])
         pool_piece(2)
         load_piece(5)
+        finish_added(1)
         pool_piece(3)
         load_piece(6)
         multiply_means(0)

@@ -20,7 +20,7 @@ UNIT_ROWS = 8
 AHEAD = 3
 LAG = 5
 ADDED_PLACES = 2
-FIRST_PAIRED = 16
+FIRST_PAIRED = 13
 W_U, W_OWN, W_OTHER, W_E = range(4)
 
 FLOPS = 2 * (B * N * D1 * ND + B * 2 * 2 * D1 * ND + B * N * 2 * D2 * ND)
@@ -51,7 +51,7 @@ def tile_ferminetoneelectronlayer_pa_t_kernel(tc, in_1e, in_2e, W_unmixed, b_unm
             x_of[panel] = x
 
         def is_added(unit):
-            return unit % 2 == 1 and unit // 2 % PIECES < ADDED_PLACES
+            return unit % 2 == 1 and unit // 2 % PIECES < (2 if unit < 8 else 1)
 
         def run_of(unit):
             return 2 if unit % 2 == 0 and unit // 2 >= FIRST_PAIRED else 1
@@ -107,8 +107,9 @@ def tile_ferminetoneelectronlayer_pa_t_kernel(tc, in_1e, in_2e, W_unmixed, b_unm
         def add_electrons(panel, spin):
             x = x_of[panel]
             e0 = 4 * spin
-            halfsum = two.tile([P, 2, D1], F32, name="hs%d_%d" % (panel, spin), tag="hs", bufs=4)
-            nc.vector.tensor_tensor(out=halfsum[:], in0=x[:, e0:e0 + 2, :], in1=x[:, e0 + 2:e0 + 4, :], op=ADD)
+            halfsum = two.tile([P, 2, 4, P], F32, name="hs%d_%d" % (panel, spin), tag="hs", bufs=4)
+            by_t = x[:].rearrange("p i (k t) -> p i t k", t=4)
+            nc.vector.tensor_tensor(out=halfsum[:], in0=by_t[:, e0:e0 + 2], in1=by_t[:, e0 + 2:e0 + 4], op=ADD)
             halfsums[(panel, spin)] = halfsum
 
         def transpose_means(panel, spin):
@@ -117,7 +118,7 @@ def tile_ferminetoneelectronlayer_pa_t_kernel(tc, in_1e, in_2e, W_unmixed, b_unm
             bank = ps2.tile([P, 4, P], F32, name="mt%d_%d" % (panel, spin), tag="aux")
             for t in range(4):
                 transpose_and_add(bank[:, t, :],
-                                  [halfsums[(panel, spin)][:, n, t * P:(t + 1) * P] for n in range(2)])
+                                  [halfsums[(panel, spin)][:, n, t, :] for n in range(2)])
             nc.scalar.mul(out=m_grouped[panel][:, spin, :, :], in_=bank[:].rearrange("p t b -> p b t"), mul=0.25)
 
         def quantise_x(panel):
@@ -254,8 +255,7 @@ def tile_ferminetoneelectronlayer_pa_t_kernel(tc, in_1e, in_2e, W_unmixed, b_unm
                 if half % 2 == 1:
                     sum_half(half)
                 if half > 0:
-                    for pair in range(2):
-                        skip_tiles(half - 1, 2 * pair, 2)
+                    skip_tiles(half - 1, 0, 4)
                 if half % 2 == 0:
                     sum_half(half)
             if odd and 0 <= half < N_HALVES - 1:
@@ -306,7 +306,7 @@ def tile_ferminetoneelectronlayer_pa_t_kernel(tc, in_1e, in_2e, W_unmixed, b_unm
         nc.sync.dma_start(out=bias_row[0:1, :], in_=b_unmixed.unsqueeze(0))
         load_x(1)
         raw_mixed = big.tile([P, 8, ND], BF16, name="raw_mixed", tag="big", align_bytes=64)
-        nc.sync.dma_start(out=raw_mixed[:], in_=W_mixed.rearrange("(t p) n -> p t n", p=P))
+        nc.sync.dma_start(out=raw_mixed[:].rearrange("p (h t) n -> p h (t n)", h=2), in_=W_mixed.rearrange("(h p t) n -> p h (t n)", h=2, t=4))
         load_piece(0)
         load_x(2)
         load_piece(1)

@@ -199,11 +199,15 @@ def tile_ferminetoneelectronlayer_pa_t_kernel(tc, in_1e, in_2e, W_unmixed, b_unm
             part = out_of[half][:, k0:k0 + tiles, :]
             nc.scalar.activation(out=part, in_=part, func=TANH)
 
-        def skip_tiles(half, k0, tiles):
+        def release_gpsimd():
+            nc.vector.memset(token[:], 0.0)
+            nc.gpsimd.tensor_copy(out=token_read[:], in_=token[:])
+
+        def skip_tiles(half, k0, tiles, engine):
             panel, spin = divmod(half, 2)
             part = out_of[half][:, k0:k0 + tiles, :]
             i0 = 4 * spin + k0
-            nc.vector.tensor_tensor(out=part, in0=part, in1=x_of[panel][:, i0:i0 + tiles, :], op=ADD)
+            engine.tensor_tensor(out=part, in0=part, in1=x_of[panel][:, i0:i0 + tiles, :], op=ADD)
 
         def store_half(half):
             panel, spin = divmod(half, 2)
@@ -215,7 +219,7 @@ def tile_ferminetoneelectronlayer_pa_t_kernel(tc, in_1e, in_2e, W_unmixed, b_unm
             panel, spin = divmod(half, 2)
             for k0, tiles in ((0, 2), (2, 1), (3, 1)):
                 tanh_tiles(half, k0, tiles)
-                skip_tiles(half, k0, tiles)
+                skip_tiles(half, k0, tiles, nc.vector)
                 nc.sync.dma_start(out=out[panel * P:(panel + 1) * P, 4 * spin + k0:4 * spin + k0 + tiles, :],
                                   in_=out_of[half][:, k0:k0 + tiles, :])
 
@@ -252,12 +256,14 @@ def tile_ferminetoneelectronlayer_pa_t_kernel(tc, in_1e, in_2e, W_unmixed, b_unm
             if place == 0 and panel <= PANELS:
                 quantise_e(panel - 1)
             if not odd and 0 <= half < N_HALVES:
-                if half % 2 == 1:
-                    sum_half(half)
+                if half > 0 and half % 2 == 0:
+                    skip_tiles(half - 1, 2, 2, nc.vector)
                 if half > 0:
-                    skip_tiles(half - 1, 0, 4)
-                if half % 2 == 0:
-                    sum_half(half)
+                    release_gpsimd()
+                    skip_tiles(half - 1, 0, 2, nc.gpsimd)
+                sum_half(half)
+                if half % 2 == 1:
+                    skip_tiles(half - 1, 2, 2, nc.vector)
             if odd and 0 <= half < N_HALVES - 1:
                 tanh_tiles(half, 2, 2)
             if n == LAG - 1:
@@ -300,6 +306,8 @@ def tile_ferminetoneelectronlayer_pa_t_kernel(tc, in_1e, in_2e, W_unmixed, b_unm
         w_words = const.tile([P, 4, ND], U32, align_bytes=64)
         w_scales = const.tile([P, 4, ND], U8, align_bytes=64)
         ident = const.tile([P, P], F32)
+        token = const.tile([P, 1], F32)
+        token_read = const.tile([P, 1], F32)
         pool_matrix = {}
         make_identity(nc, ident[:])
         load_x(0)

@@ -257,10 +257,10 @@ def tile_ferminetoneelectronlayer_pa_t_kernel(tc, in_1e, in_2e, W_unmixed, b_unm
                 quantise_e(panel - 1)
             if not odd and 0 <= half < N_HALVES:
                 if half > 0 and half % 2 == 0:
-                    skip_tiles(half - 1, 2, 2, nc.vector)
+                    skip_tiles(half - 1, 0, 2, nc.vector)
                 if half > 0:
                     release_gpsimd()
-                    skip_tiles(half - 1, 0, 2, nc.gpsimd)
+                    skip_tiles(half - 1, 2 if half % 2 == 0 else 0, 2, nc.gpsimd)
                 sum_half(half)
                 if half % 2 == 1:
                     skip_tiles(half - 1, 2, 2, nc.vector)

@@ -20,7 +20,7 @@ UNIT_ROWS = 8
 AHEAD = 3
 LAG = 5
 ADDED_PLACES = 2
-FIRST_PAIRED = 13
+FIRST_PAIRED = 14
 W_U, W_OWN, W_OTHER, W_E = range(4)
 
 FLOPS = 2 * (B * N * D1 * ND + B * 2 * 2 * D1 * ND + B * N * 2 * D2 * ND)
@@ -51,7 +51,7 @@ def tile_ferminetoneelectronlayer_pa_t_kernel(tc, in_1e, in_2e, W_unmixed, b_unm
             x_of[panel] = x
 
         def is_added(unit):
-            return unit % 2 == 1 and unit // 2 % PIECES < (2 if unit < 8 else 1)
+            return unit % 2 == 1 and unit // 2 % PIECES < 1
 
         def run_of(unit):
             return 2 if unit % 2 == 0 and unit // 2 >= FIRST_PAIRED else 1
@@ -273,6 +273,8 @@ def tile_ferminetoneelectronlayer_pa_t_kernel(tc, in_1e, in_2e, W_unmixed, b_unm
             if n in (4, 5):
                 transpose_x(3, 4 * (n - 4))
                 add_electrons(3, n - 4)
+            if not odd and 0 <= half < N_HALVES - 1:
+                tanh_tiles(half, 0, 2)
             if n < N_PIECES:
                 pool_piece(n)
             if n in (6, 7):
@@ -284,8 +286,6 @@ def tile_ferminetoneelectronlayer_pa_t_kernel(tc, in_1e, in_2e, W_unmixed, b_unm
             if place == 3 and 0 < panel < PANELS:
                 add_bias(panel)
             add_second(n)
-            if not odd and 0 <= half < N_HALVES - 1:
-                tanh_tiles(half, 0, 2)
             if odd == half % 2 and 0 < half + 1 < N_HALVES:
                 multiply_half(half + 1)
             if place == 2 and 0 < panel < PANELS:

import concourse.mybir as mybir
from concourse.masks import make_identity

F32 = mybir.dt.float32
BF16 = mybir.dt.bfloat16
U32 = mybir.dt.uint32
U8 = mybir.dt.uint8
FP8X4 = mybir.dt.float8_e4m3fn_x4
ADD = mybir.AluOpType.add
TANH = mybir.ActivationFunctionType.Tanh

P = 128
B, N, D1, D2 = 512, 8, 512, 256
ND = D1
PANELS = B // P
PIECES = 4
N_PIECES = PANELS * PIECES
N_HALVES = 2 * PANELS
UNIT_ROWS = 8
AHEAD = 3
LAG = 5
ADDED_PLACES = 2
FIRST_PAIRED = 14
W_U, W_OWN, W_OTHER, W_E = range(4)

FLOPS = 2 * (B * N * D1 * ND + B * 2 * 2 * D1 * ND + B * N * 2 * D2 * ND)


def tile_ferminetoneelectronlayer_pa_t_kernel(tc, in_1e, in_2e, W_unmixed, b_unmixed, W_mixed, W_2e, out):
    nc = tc.nc
    rows_2e = in_2e.rearrange("b i j d -> (b i j) d")
    tokens_2e = in_2e.rearrange("b i j d -> (b i) j d")

    with tc.manual_schedule(), \
         tc.tile_pool(name="const", bufs=1) as const, \
         tc.tile_pool(name="xpool", bufs=PANELS) as xpool, \
         tc.tile_pool(name="big", bufs=7) as big, \
         tc.tile_pool(name="stage", bufs=AHEAD) as stage, \
         tc.tile_pool(name="two", bufs=2) as two, \
         tc.tile_pool(name="keep", bufs=PANELS) as keep, \
         tc.psum_pool(name="ps2", bufs=2) as ps2, \
         tc.psum_pool(name="ps4", bufs=4) as ps4:

        x_of, unit_of, x_grouped, e_grouped, halfsums, m_grouped = {}, {}, {}, {}, {}, {}
        x_mx, m_mx, e_mx, g_psum, g_bias, acc_of, out_of = {}, {}, {}, {}, {}, {}, {}
        added_halfsum, added_bank = {}, {}

        def load_x(panel):
            x = xpool.tile([P, N, D1], BF16, name="x%d" % panel, tag="x")
            nc.sync.dma_start(out=x[:], in_=in_1e[panel * P:(panel + 1) * P, :, :])
            x_of[panel] = x

        def is_added(unit):
            return unit % 2 == 1 and unit // 2 % PIECES < 1

        def run_of(unit):
            return 2 if unit % 2 == 0 and unit // 2 >= FIRST_PAIRED else 1

        def load_piece(piece):
            staged = stage.tile([P, 2 * UNIT_ROWS, D2], BF16, name="piece%d" % piece, tag="piece")
            units = (2 * piece, 2 * piece + 1)
            for k, unit in enumerate(units):
                unit_of[unit] = staged[:, k * UNIT_ROWS:(k + 1) * UNIT_ROWS, :]
            if run_of(units[0]) == 1 and not is_added(units[1]):
                rows = rows_2e[units[0] * UNIT_ROWS * P:(units[1] + 1) * UNIT_ROWS * P, :]
                nc.sync.dma_start(out=staged[:], in_=rows.rearrange("(r p) d -> p r d", p=P))
            else:
                for unit in units:
                    run = UNIT_ROWS if is_added(unit) else run_of(unit)
                    rows = rows_2e[unit * UNIT_ROWS * P:(unit + 1) * UNIT_ROWS * P, :]
                    nc.sync.dma_start(out=unit_of[unit].rearrange("p (r e) d -> p r (e d)", e=run),
                                      in_=rows.rearrange("(r p e) d -> p r (e d)", p=P, e=run))

        def quantise(pool, name, grouped, width):
            words = pool.tile([P, width], U32, name=name + "_words", tag=name[0] + "_words", align_bytes=64)
            scales = pool.tile([P, width], U8, name=name + "_scales", tag=name[0] + "_scales", align_bytes=64)
            nc.vector.quantize_mx(out=words[:].bitcast(FP8X4), scales=scales[:], in_=grouped)
            return words, scales

        def mx_pass(acc, operand, columns, weight, start, stop):
            words, scales = operand
            nc.tensor.matmul_mx(out=acc[:], lhsT=words[:, columns].bitcast(FP8X4), lhsT_scale=scales[:, columns],
                                rhs=w_words[:, weight, :].bitcast(FP8X4), rhs_scale=w_scales[:, weight, :],
                                start=start, stop=stop)

        def transpose_and_add(dst, parts):
            for n, part in enumerate(parts):
                nc.tensor.matmul(out=dst, lhsT=part, rhs=ident[:], is_transpose=True,
                                 start=(n == 0), stop=(n == len(parts) - 1))

        def transpose_x(panel, first):
            words = x_of[panel][:].bitcast(F32)
            if first == 0:
                x_grouped[panel] = two.tile([P, N, P, 4], BF16, name="xg%d" % panel, tag="xg", align_bytes=64)
            grouped_words = (x_grouped[panel][:].rearrange("p i b t -> p i (b t)").bitcast(F32)
                             .rearrange("p i (b u) -> p i b u", u=2))
            banks = []
            for i0 in (first, first + 2):
                bank = ps2.tile([P, 2, 2, P], F32, name="xt%d_%d" % (panel, i0), tag="aux")
                for i in range(2):
                    for u in range(2):
                        nc.tensor.transpose(bank[:, i, u, :], words[:, i0 + i, u * P:(u + 1) * P], ident[:])
                banks.append(bank)
            for i0, bank in zip((first, first + 2), banks):
                nc.scalar.copy(out=grouped_words[:, i0:i0 + 2, :, :], in_=bank[:].rearrange("p i u b -> p i b u"))

        def add_electrons(panel, spin):
            x = x_of[panel]
            e0 = 4 * spin
            halfsum = two.tile([P, 2, 4, P], F32, name="hs%d_%d" % (panel, spin), tag="hs", bufs=4)
            by_t = x[:].rearrange("p i (k t) -> p i t k", t=4)
            nc.vector.tensor_tensor(out=halfsum[:], in0=by_t[:, e0:e0 + 2], in1=by_t[:, e0 + 2:e0 + 4], op=ADD)
            halfsums[(panel, spin)] = halfsum

        def transpose_means(panel, spin):
            if spin == 0:
                m_grouped[panel] = two.tile([P, 2, P, 4], BF16, name="mg%d" % panel, tag="mg", align_bytes=64)
            bank = ps2.tile([P, 4, P], F32, name="mt%d_%d" % (panel, spin), tag="aux")
            for t in range(4):
                transpose_and_add(bank[:, t, :],
                                  [halfsums[(panel, spin)][:, n, t, :] for n in range(2)])
            nc.scalar.mul(out=m_grouped[panel][:, spin, :, :], in_=bank[:].rearrange("p t b -> p b t"), mul=0.25)

        def quantise_x(panel):
            x_mx[panel] = quantise(keep, "x%d" % panel, x_grouped[panel][:].rearrange("p i b t -> p (i b t)"), N * P)

        def quantise_means(panel):
            m_mx[panel] = quantise(keep, "m%d" % panel, m_grouped[panel][:].rearrange("p s b t -> p (s b t)"), 2 * P)

        def multiply_means(panel):
            g_psum[panel] = []
            for spin in range(2):
                acc = ps2.tile([P, ND], F32, name="g%d_%d" % (panel, spin), tag="aux")
                mx_pass(acc, m_mx[panel], slice(spin * P, (spin + 1) * P), W_OWN, True, False)
                mx_pass(acc, m_mx[panel], slice((1 - spin) * P, (2 - spin) * P), W_OTHER, False, True)
                g_psum[panel].append(acc)

        def add_bias(panel):
            g_bias[panel] = two.tile([P, 2, ND], F32, name="gb%d" % panel, tag="gb")
            for spin in range(2):
                nc.vector.tensor_tensor(out=g_bias[panel][:, spin, :], in0=g_psum[panel][spin][:], in1=bias[:], op=ADD)

        def pool_unit(unit):
            panel, place = divmod(unit, 2 * PIECES)
            run = run_of(unit)
            tiles = UNIT_ROWS // run
            width = P // tiles
            bank = ps2.tile([P, 4, P], F32, name="pool%d" % unit, tag="pool")
            for r in range(tiles):
                for c in range(2):
                    for e in range(run):
                        nc.tensor.matmul(out=bank[:, c:4 - c:3 - 2 * c, width * r:width * (r + 1)],
                                         lhsT=unit_of[unit][:, run * r + e, c * P:(c + 1) * P],
                                         rhs=pool_matrix[run], start=(e == 0), stop=(e == run - 1))
            nc.scalar.copy(out=e_grouped[panel][:, :, 64 * place:64 * (place + 1)].rearrange("p i (b t) -> p i b t", t=4),
                           in_=bank[:].rearrange("p t (b i) -> p i b t", i=N))

        def add_rows(unit):
            rows = unit_of[unit].rearrange("p (a f) d -> p a f d", a=2)
            halfsum = two.tile([P, 2, 2, D2], F32, name="added_hs%d" % unit, tag="added_hs")
            nc.vector.tensor_tensor(out=halfsum[:], in0=rows[:, :, 0:2, :], in1=rows[:, :, 2:4, :], op=ADD)
            added_halfsum[unit] = halfsum

        def transpose_added(unit):
            bank = ps2.tile([P, 4, P], F32, name="added_t%d" % unit, tag="pool")
            for sj in range(2):
                for c in range(2):
                    transpose_and_add(bank[:, 3 - c if sj else c, :],
                                      [added_halfsum[unit][:, sj, n, c * P:(c + 1) * P] for n in range(2)])
            added_bank[unit] = bank

        def copy_added(unit):
            panel, place = divmod(unit, 2 * PIECES)
            walkers = e_grouped[panel][:].rearrange("p i (b t) -> p i b t", t=4)[:, :, 16 * place:16 * (place + 1), :]
            means = added_bank[unit][:].rearrange("p t (b i) -> p i b t", i=N)
            nc.scalar.mul(out=walkers[:, 0:4, :, :], in_=means[:, 0:4, :, :], mul=0.25)
            nc.scalar.mul(out=walkers[:, 4:8, :, :], in_=means[:, 4:8, :, ::-1], mul=0.25)

        def quantise_e(panel):
            e_mx[panel] = quantise(two, "e%d" % panel, e_grouped[panel][:].rearrange("p i c -> p (i c)"), N * P)

        def multiply_half(half):
            panel, spin = divmod(half, 2)
            for k in range(4):
                i = 4 * spin + k
                acc = ps4.tile([P, ND], F32, name="acc%d_%d" % (panel, i), tag="acc")
                mx_pass(acc, x_mx[panel], slice(i * P, (i + 1) * P), W_U, True, False)
                mx_pass(acc, e_mx[panel], slice(i * P, (i + 1) * P), W_E, False, True)
                acc_of[4 * half + k] = acc

        def sum_half(half):
            panel, spin = divmod(half, 2)
            out_of[half] = big.tile([P, 4, ND], F32, name="o%d" % half, tag="big", align_bytes=64)
            for k in range(4):
                nc.vector.tensor_tensor(out=out_of[half][:, k, :], in0=acc_of[4 * half + k][:],
                                        in1=g_bias[panel][:, spin, :], op=ADD)

        def tanh_tiles(half, k0, tiles):
            part = out_of[half][:, k0:k0 + tiles, :]
            nc.scalar.activation(out=part, in_=part, func=TANH)

        def release_gpsimd():
            nc.vector.memset(token[:], 0.0)
            nc.gpsimd.tensor_copy(out=token_read[:], in_=token[:])

        def skip_tiles(half, k0, tiles, engine):
            panel, spin = divmod(half, 2)
            part = out_of[half][:, k0:k0 + tiles, :]
            i0 = 4 * spin + k0
            engine.tensor_tensor(out=part, in0=part, in1=x_of[panel][:, i0:i0 + tiles, :], op=ADD)

        def store_half(half):
            panel, spin = divmod(half, 2)
            rows = out[panel * P:(panel + 1) * P, 4 * spin:4 * spin + 4, :]
            nc.sync.dma_start(out=rows, in_=out_of[half][:])

        def finish_last_half():
            half = N_HALVES - 1
            panel, spin = divmod(half, 2)
            for k0, tiles in ((0, 2), (2, 1), (3, 1)):
                tanh_tiles(half, k0, tiles)
                skip_tiles(half, k0, tiles, nc.vector)
                nc.sync.dma_start(out=out[panel * P:(panel + 1) * P, 4 * spin + k0:4 * spin + k0 + tiles, :],
                                  in_=out_of[half][:, k0:k0 + tiles, :])

        def group_weight(grouped, rows):
            nc.vector.tensor_copy(out=grouped.rearrange("p (c i) t -> p c t i", i=4),
                                  in_=rows.rearrange("p t (c i) -> p c t i", i=4))

        def quantise_weight(weight, grouped):
            nc.vector.quantize_mx(out=w_words[:, weight, :].bitcast(FP8X4), scales=w_scales[:, weight, :],
                                  in_=grouped.rearrange("p n t -> p (n t)"))

        def pool_piece(piece):
            panel, place = divmod(piece, PIECES)
            if place == 0:
                e_grouped[panel] = two.tile([P, N, 4 * P], BF16, name="eg%d" % panel, tag="eg", align_bytes=64)
            for unit in (2 * piece, 2 * piece + 1):
                if not is_added(unit):
                    pool_unit(unit)

        def add_second(piece):
            if piece < N_PIECES and is_added(2 * piece + 1):
                add_rows(2 * piece + 1)

        def finish_added(piece):
            unit = 2 * piece + 1
            if 0 <= piece < N_PIECES and is_added(unit):
                transpose_added(unit)
                copy_added(unit)

        def slot(n):
            half, odd = divmod(n - LAG, 2)
            panel, place = divmod(n, PIECES)
            finish_added(n - 1)
            if place == 0 and panel <= PANELS:
                quantise_e(panel - 1)
            if not odd and 0 <= half < N_HALVES:
                if half > 0 and half % 2 == 0:
                    skip_tiles(half - 1, 0, 2, nc.vector)
                if half > 0:
                    release_gpsimd()
                    skip_tiles(half - 1, 2 if half % 2 == 0 else 0, 2, nc.gpsimd)
                sum_half(half)
                if half % 2 == 1:
                    skip_tiles(half - 1, 2, 2, nc.vector)
            if odd and 0 <= half < N_HALVES - 1:
                tanh_tiles(half, 2, 2)
            if n == LAG - 1:
                multiply_half(0)
            if n == 4:
                add_bias(0)
            if n in (4, 5):
                transpose_x(3, 4 * (n - 4))
                add_electrons(3, n - 4)
            if not odd and 0 <= half < N_HALVES - 1:
                tanh_tiles(half, 0, 2)
            if n < N_PIECES:
                pool_piece(n)
            if n in (6, 7):
                transpose_means(3, n - 6)
            if n == 6:
                quantise_x(3)
            if n == 8:
                quantise_means(3)
            if place == 3 and 0 < panel < PANELS:
                add_bias(panel)
            add_second(n)
            if odd == half % 2 and 0 < half + 1 < N_HALVES:
                multiply_half(half + 1)
            if place == 2 and 0 < panel < PANELS:
                multiply_means(panel)
            if n + AHEAD < N_PIECES:
                load_piece(n + AHEAD)
            elif n + AHEAD == N_PIECES:
                for done in range(0, half):
                    store_half(done)
            elif not odd:
                store_half(half - 1)

        bias_row = const.tile([P, ND], BF16)
        nc.gpsimd.memset(bias_row[:], 0.0)
        ones = const.tile([P, P], BF16)
        nc.gpsimd.memset(ones[:], 1.0)
        bias = const.tile([P, ND], F32)
        w_words = const.tile([P, 4, ND], U32, align_bytes=64)
        w_scales = const.tile([P, 4, ND], U8, align_bytes=64)
        ident = const.tile([P, P], F32)
        token = const.tile([P, 1], F32)
        token_read = const.tile([P, 1], F32)
        pool_matrix = {}
        make_identity(nc, ident[:])
        load_x(0)
        nc.sync.dma_start(out=bias_row[0:1, :], in_=b_unmixed.unsqueeze(0))
        load_x(1)
        raw_mixed = big.tile([P, 8, ND], BF16, name="raw_mixed", tag="big", align_bytes=64)
        nc.sync.dma_start(out=raw_mixed[:].rearrange("p (h t) n -> p h (t n)", h=2), in_=W_mixed.rearrange("(h p t) n -> p h (t n)", h=2, t=4))
        load_piece(0)
        load_x(2)
        load_piece(1)
        raw_rest = big.tile([P, 8, ND], BF16, name="raw_rest", tag="big", align_bytes=64)
        raw_unmixed = raw_rest[:, 0:4, :]
        nc.sync.dma_start(out=raw_unmixed.rearrange("p (u e) n -> p u e n", e=2),
                          in_=W_unmixed.rearrange("(u p e) n -> p u e n", u=2, e=2))
        raw_2e = raw_rest[:, 4:8, :]
        blocks_2e = W_2e.rearrange("(t p) n -> p t n", p=P)
        nc.sync.dma_start(out=raw_2e[:, 0:2, :], in_=blocks_2e[:, 0:2, :])
        for t in (2, 3):
            nc.sync.dma_start(out=raw_2e[:, t, :], in_=blocks_2e[:, 5 - t, :])
        load_piece(2)
        grouped_mixed = big.tile([P, 2, ND, 4], BF16, name="grouped_mixed", tag="big", align_bytes=64)
        grouped_rest = big.tile([P, 2, ND, 4], BF16, name="grouped_rest", tag="big", align_bytes=64)

        for run in (1, 2):
            f = 4 // run
            group_of_run = const.tile([P, 2 * run, N, 2], F32, name="group%d" % run)
            nc.vector.tensor_reduce(out=group_of_run[:].rearrange("p a i j -> p (a i j)"),
                                    in_=ident[:].rearrange("p (g f) -> p g f", f=f),
                                    axis=mybir.AxisListType.X, op=ADD)
            by_spin = group_of_run[:].rearrange("p a i j -> p j a i")
            pool_tile = const.tile([P, 2, 2 * run, N], BF16, name="pool_tile%d" % run)
            for j in range(2):
                nc.vector.tensor_scalar_mul(out=pool_tile[:, j, :, 0:4], in0=by_spin[:, j, :, 0:4], scalar1=0.25)
                nc.vector.tensor_scalar_mul(out=pool_tile[:, j, :, 4:8], in0=by_spin[:, 1 - j, :, 4:8], scalar1=0.25)
            pool_matrix[run] = pool_tile[:].rearrange("p s a i -> p (s a i)")

        for panel in (0, 1):
            for spin in range(2):
                transpose_x(panel, 4 * spin)
                add_electrons(panel, spin)
            if panel == 0:
                bias_bank = ps4.tile([P, ND], F32, name="bias_bank", tag="acc")
                nc.tensor.matmul(out=bias_bank[:], lhsT=ones[:], rhs=bias_row[:], start=True, stop=True)
                nc.scalar.copy(out=bias[:], in_=bias_bank[:])
            for spin in range(2):
                transpose_means(panel, spin)
        group_weight(grouped_mixed[:, 0], raw_mixed[:, 0:4, :])
        quantise_x(0)
        group_weight(grouped_mixed[:, 1], raw_mixed[:, 4:8, :])
        quantise_means(0)
        quantise_weight(W_OWN, grouped_mixed[:, 0])
        quantise_x(1)
        quantise_weight(W_OTHER, grouped_mixed[:, 1])
        quantise_means(1)
        pool_piece(0)
        load_piece(3)
        load_x(3)
        for spin in range(2):
            transpose_x(2, 4 * spin)
            add_electrons(2, spin)
        add_second(0)
        pool_piece(1)
        load_piece(4)
        finish_added(0)
        for spin in range(2):
            transpose_means(2, spin)
        group_weight(grouped_rest[:, 0], raw_unmixed)
        quantise_x(2)
        add_second(1)
        group_weight(grouped_rest[:, 1], raw_2e)
        quantise_means(2)
        quantise_weight(W_U, grouped_rest[:, 0])
        quantise_weight(W_E, grouped_rest[:, 1])
        pool_piece(2)
        load_piece(5)
        finish_added(1)
        pool_piece(3)
        load_piece(6)
        multiply_means(0)
        for n in range(PIECES, 2 * N_HALVES + LAG - 1):
            slot(n)
        finish_last_half()
